import numpy as np
import ml_dtypes


def mxq(x, axis, fmt="e4m3"):
    dtype, down = {"e4m3": (ml_dtypes.float8_e4m3fn, 7), "e5m2": (ml_dtypes.float8_e5m2, 14)}[fmt]
    v = np.moveaxis(np.asarray(x, np.float32).astype(ml_dtypes.bfloat16).astype(np.float64), axis, -1)
    blocks = v.reshape(v.shape[:-1] + (-1, 32))
    amax = np.abs(blocks).max(-1, keepdims=True)
    byte = np.maximum(np.where(amax > 0, np.frexp(amax)[1] - 1 + 127, 0) - down, 1)
    scale = np.exp2(byte - 127.0)
    codes = (blocks / scale).astype(np.float32).astype(dtype).astype(np.float64)
    return np.moveaxis((codes * scale).reshape(v.shape), -1, axis)


WIDE = False


def mx_kscale(k):
    if not WIDE:
        return np.ones(k)
    levels = np.array([10, -10, 5, -5, 0])
    if k % 512:
        return np.exp2(np.random.permutation(np.resize(levels, k // 32))).repeat(32)
    a = np.empty((k // 512, 16))
    for p in range(k // 512):
        a[p, :8] = np.random.permutation(np.resize(levels, 8))
        for g in range(8):
            far = levels[np.abs(levels - a[p, g]) >= 10]
            a[p, g + 8] = far[np.random.randint(len(far))]
    return np.exp2(a.ravel()).repeat(32)


BF16 = ml_dtypes.bfloat16


def bf(x):
    return np.asarray(x, np.float32).astype(BF16)


def f64(x):
    return np.asarray(x).astype(np.float64)


B, H, N, NMAX, NMIN, V, VI, NH = 4096, 512, 127, 127, 126, 16, 3, 2
TS = 4.0


def distortion(X):
    cols = [np.sum(X[:, :-k] * X[:, k:], axis=1) for k in range(1, N + 1)]
    return np.stack(cols[::-1], axis=1)


def setup_inputs():
    s, t = mx_kscale(H), mx_kscale(H)
    return {"h1": bf(np.maximum(np.random.standard_normal((B, H)), 0.0) * s),
            "w_hid2": bf(np.random.standard_normal((H, H)) * 1.5 / np.sqrt(H) * t[:, None] / s[None, :]),
            "b_hid2": bf(np.random.standard_normal(H) * 0.2 * t),
            "w_out": bf(np.random.standard_normal((N + 1, H)) * 0.18 / np.sqrt(H) / t[None, :]),
            "b_out": bf(np.random.standard_normal(N + 1) * 0.03),
            "norm_root": bf(np.sqrt(TS * np.sqrt(N)) * np.exp(0.15 * np.random.standard_normal((B, 1)))),
            "T": bf(np.random.standard_normal((B, N)) * TS)}


def reference(h1, w_hid2, b_hid2, w_out, b_out, norm_root, T):
    h2 = np.maximum((mxq(f64(h1), 1, "e4m3") @ mxq(f64(w_hid2), 1, "e4m3").T) + f64(b_hid2), 0.0)
    X_hat = ((mxq(h2, 1, "e4m3") @ mxq(f64(w_out), 1, "e4m3").T) + f64(b_out)) * f64(norm_root)
    X_hat_clamped = np.clip(X_hat, -2.0, 2.0)
    error = np.reshape(np.mean((distortion(X_hat) - f64(T)) ** 2), (1,))
    error_clamped = np.reshape(np.mean((distortion(X_hat_clamped) - f64(T)) ** 2), (1,))
    return (X_hat, error, X_hat_clamped, error_clamped)

@@ -1,0 +1,410 @@
+import math
+from contextlib import ExitStack
+
+import concourse.mybir as mybir
+from concourse.masks import make_identity
+
+F32 = mybir.dt.float32
+BF16 = mybir.dt.bfloat16
+I32 = mybir.dt.int32
+U32 = mybir.dt.uint32
+U8 = mybir.dt.uint8
+FP8X4 = mybir.dt.float8_e4m3fn_x4
+ALU = mybir.AluOpType
+AF = mybir.ActivationFunctionType
+AX = mybir.AxisListType
+
+P = 128
+B = 4096
+H = 512
+N = 128
+LAGS = 127
+TILES = B // P
+BLK = 4
+NBLK = TILES // BLK
+G = 64
+FAST = ((0, 1), (1, 0), (1, 1))
+BATCHES = ((0, 1), (1, 2), (3, 2), (5, 2), (7, 1))
+SHARED = 3
+EIGHTHS = ((0, 2), (1, 4), (3, 4))
+RHO = math.sqrt(0.5)
+MEAN = 2.0 * B * LAGS
+
+FLOPS = 2 * B * H * (H + N) + 2 * 2 * B * (N * LAGS // 2)
+
+
+def tile_qdtssolveronnx_pa_kernel(tc, h1, w_hid2, b_hid2, w_out, b_out, norm_root, T, out_0, out_1, out_2, out_3):
+    nc = tc.nc
+    tensor_tensor = nc.vector.tensor_tensor
+    mul_add = nc.vector.scalar_tensor_tensor
+    with ExitStack() as ctx:
+        keep = ctx.enter_context(tc.tile_pool(name="keep", bufs=1))
+        h1_pool = ctx.enter_context(tc.tile_pool(name="h1_pool", bufs=3))
+        stage = ctx.enter_context(tc.tile_pool(name="stage", bufs=2))
+        z_pool = ctx.enter_context(tc.tile_pool(name="z_pool", bufs=3))
+        batch_pool = ctx.enter_context(tc.tile_pool(name="batch_pool", bufs=2))
+        fft = ctx.enter_context(tc.tile_pool(name="fft", bufs=1))
+        ps_in = ctx.enter_context(tc.psum_pool(name="ps_in", bufs=1))
+        ps_h2 = ctx.enter_context(tc.psum_pool(name="ps_h2", bufs=2))
+        ps_x = ctx.enter_context(tc.psum_pool(name="ps_x", bufs=1))
+        ps_spec = ctx.enter_context(tc.psum_pool(name="ps_spec", bufs=4))
+
+        w1_sb = keep.tile([P, 4, H], BF16)
+        nc.sync.dma_start(out=w1_sb[:], in_=w_hid2.rearrange("(p c) k -> p c k", c=4))
+        h1_rows = h1.rearrange("(p t) k -> p t k", t=TILES)
+        h1_tiles = {}
+
+        def load_h1(i):
+            h1_sb = h1_pool.tile([P, BLK, H], BF16, name="h1_sb")
+            nc.sync.dma_start(out=h1_sb[:], in_=h1_rows[:, BLK * i:BLK * (i + 1), :])
+            h1_tiles[i] = h1_sb
+
+        b1_bf = keep.tile([P, 4], BF16)
+        b2_bf = keep.tile([P, 1], BF16)
+        nr_bf = keep.tile([P, TILES], BF16)
+        with nc.allow_non_contiguous_dma(reason="three short vectors, a few bytes a partition"):
+            nc.scalar.dma_start(out=b1_bf[:], in_=b_hid2.rearrange("(p c) -> p c", c=4))
+            nc.scalar.dma_start(out=b2_bf[:], in_=b_out.rearrange("(p o) -> p o", o=1))
+            nc.scalar.dma_start(out=nr_bf[:], in_=norm_root.rearrange("(p t) o -> p (t o)", t=TILES))
+        t_pad = keep.tile([P, TILES, N], BF16)
+        nc.vector.memset(t_pad[:], 0.0)
+        ident = keep.tile([P, P], F32)
+        make_identity(nc, ident[:])
+        ident_bf = keep.tile([P, P], BF16)
+        make_identity(nc, ident_bf[:])
+        load_h1(0)
+        w2_sb = keep.tile([P, H], BF16)
+        nc.sync.dma_start(out=w2_sb[:], in_=w_out)
+        load_h1(1)
+        nc.sync.dma_start(out=t_pad[:, :, 0:LAGS], in_=T.rearrange("(p t) c -> p t c", t=TILES))
+
+        def sines(phase, width, name):
+            nc.vector.tensor_single_scalar(out=phase, in_=phase, scalar=511, op=ALU.bitwise_and)
+            angle = fft.tile([P, width], F32, name=name + "_angle", tag="mid")
+            nc.vector.tensor_scalar(out=angle[:], in0=phase, scalar1=-256.0, scalar2=None, op0=ALU.add)
+            edge = fft.tile([P, width], F32, name=name + "_edge", tag="cross")
+            nc.vector.tensor_scalar(out=edge[:], in0=angle[:], scalar1=-256.0, scalar2=256.0, op0=ALU.is_equal, op1=ALU.mult)
+            nc.vector.tensor_tensor(out=angle[:], in0=angle[:], in1=edge[:], op=ALU.add)
+            table = keep.tile([P, width], F32, name=name + "_table")
+            nc.scalar.activation(out=table[:], in_=angle[:], func=AF.Sin, scale=math.pi / 256.0)
+            return table
+
+        COS = 256 + 128
+
+        W_TW = 4 * 56
+        row_phase = keep.tile([P, W_TW + N], I32)
+        tw_phase = row_phase[:, 0:W_TW].rearrange("p (k j h) -> p k j h", k=4, h=7)
+        for h in range(1, 8):
+            nc.gpsimd.iota(tw_phase[:, :, :, h - 1], pattern=[[128, 4], [8 * h, 8]], base=COS, channel_multiplier=0)
+        LAST_FREQ = 4 * (N - 1) + 1
+        nc.gpsimd.iota(row_phase[:, W_TW:W_TW + N], pattern=[[-LAST_FREQ, N]], base=LAGS * LAST_FREQ + COS, channel_multiplier=0)
+        row_table = sines(row_phase[:], W_TW + N, "row")
+        twiddle = row_table[:, 0:W_TW].rearrange("p (k j h) -> p k j h", k=4, h=7)
+        last_col = keep.tile([P, N], F32)
+        nc.vector.tensor_scalar(out=last_col[:], in0=row_table[:, W_TW:W_TW + N], scalar1=2.0, scalar2=None, op0=ALU.mult)
+
+        p_index = keep.tile([P, 2], I32)
+        nc.gpsimd.iota(p_index[:, 0:1], pattern=[[0, 1]], base=0, channel_multiplier=1)
+        nc.gpsimd.iota(p_index[:, 1:2], pattern=[[0, 1]], base=LAGS, channel_multiplier=-1)
+        p_float = keep.tile([P, 2], F32)
+        nc.vector.tensor_copy(out=p_float[:], in_=p_index[:])
+        freq = keep.tile([P, 2, G], I32)
+        nc.gpsimd.iota(freq[:], pattern=[[4, 2], [8, G]], base=1, channel_multiplier=0)
+        mat_phase = keep.tile([P, 4 * G + 4], I32)
+        for hf in range(2):
+            nc.gpsimd.iota(mat_phase[:, 4 * G + 2 * hf:4 * G + 2 * hf + 2], pattern=[[128, 2]], base=COS, channel_multiplier=1 + 4 * hf)
+        nc.vector.tensor_scalar(out=mat_phase[:, 0:G], in0=freq[:, 0, :], scalar1=p_float[:, 0:1], scalar2=float(COS),
+                                op0=ALU.mult, op1=ALU.add)
+        nc.vector.tensor_scalar(out=mat_phase[:, G:2 * G], in0=freq[:, 0, :], scalar1=p_float[:, 0:1], scalar2=256.0,
+                                op0=ALU.mult, op1=ALU.add)
+        nc.vector.tensor_scalar(out=mat_phase[:, 2 * G:4 * G], in0=freq[:].rearrange("p f g -> p (f g)"), scalar1=p_float[:, 1:2],
+                                scalar2=float(COS), op0=ALU.mult, op1=ALU.add)
+        mat_table = sines(mat_phase[:], 4 * G + 4, "mat")
+        x_matrix = mat_table[:, 0:2 * G]
+        t_matrix = keep.tile([P, 2 * G], F32)
+        nc.vector.tensor_scalar(out=t_matrix[:], in0=mat_table[:, 2 * G:4 * G], scalar1=2.0, scalar2=None, op0=ALU.mult)
+        twist = mat_table[:, 4 * G:4 * G + 4]
+
+        b1 = keep.tile([P, 4], F32)
+        nc.vector.tensor_copy(out=b1[:], in_=b1_bf[:])
+        b2 = keep.tile([P, 1], F32)
+        nc.vector.tensor_copy(out=b2[:], in_=b2_bf[:])
+        nr = keep.tile([P, TILES], F32)
+        nc.vector.tensor_copy(out=nr[:], in_=nr_bf[:])
+
+        w1_grouped = keep.tile([P, 4 * P, 4], BF16, align_bytes=64)
+        w1_grouped32 = w1_grouped[:].bitcast(F32)
+        w1_words = w1_sb[:].bitcast(F32)
+        for a in range(2):
+            w1_t = ps_in.tile([P, 2, 2, P], F32, tag="in")
+            for u in range(2):
+                for c in range(2):
+                    nc.tensor.transpose(w1_t[:, u, c, :], w1_words[:, 2 * a + c, u:2 * P:2], ident[:])
+            nc.vector.tensor_copy(out=w1_grouped32[:, 2 * P * a:2 * P * (a + 1), :], in_=w1_t[:].rearrange("q u c m -> q (c m) u"))
+        w1_codes = keep.tile([P, 4 * P], U32, align_bytes=64)
+        w1_scales = keep.tile([P, 4 * P], U8, align_bytes=64)
+        nc.vector.quantize_mx(out=w1_codes[:].bitcast(FP8X4), scales=w1_scales[:], in_=w1_grouped[:].rearrange("q n f -> q (n f)"))
+        w2_grouped = keep.tile([P, P, 4], BF16, align_bytes=64)
+        w2_words = w2_sb[:].bitcast(F32).rearrange("p (m u) -> p u m", u=2)
+        w2_t = ps_in.tile([P, 2, P], F32, tag="in")
+        for u in range(2):
+            nc.tensor.transpose(w2_t[:, u, :], w2_words[:, u, :], ident[:])
+        nc.vector.tensor_copy(out=w2_grouped[:].bitcast(F32), in_=w2_t[:].rearrange("q u n -> q n u"))
+        w2_codes = keep.tile([P, P], U32, align_bytes=64)
+        w2_scales = keep.tile([P, P], U8, align_bytes=64)
+        nc.vector.quantize_mx(out=w2_codes[:].bitcast(FP8X4), scales=w2_scales[:], in_=w2_grouped[:].rearrange("q n f -> q (n f)"))
+
+        x_rows = keep.tile([P, 2, TILES, N], F32)
+        x_out = (out_0.rearrange("(p t) j -> p t j", t=TILES), out_2.rearrange("(p t) j -> p t j", t=TILES))
+        d2_sums = keep.tile([P, 2, len(BATCHES)], F32)
+        per_batch = {}
+        x_cols = {}
+
+        def place(i):
+            b = [k for k, (first, count) in enumerate(BATCHES) if first <= i < first + count][0]
+            at = BLK * (i - BATCHES[b][0])
+            return b, BLK * BATCHES[b][1], slice(at, at + BLK)
+
+        def network(i):
+            shared = i < SHARED
+            if i + 2 < NBLK:
+                load_h1(i + 2)
+            h1_words = h1_tiles[i][:].bitcast(F32)
+            h1_grouped = stage.tile([P, BLK * P, 4], BF16, align_bytes=64)
+            h1_grouped32 = h1_grouped[:].bitcast(F32)
+            for a in range(2):
+                h1_t = ps_in.tile([P, 2, 2, P], F32, tag="in")
+                for u in range(2):
+                    for t in range(2):
+                        nc.tensor.transpose(h1_t[:, u, t, :], h1_words[:, 2 * a + t, u:2 * P:2], ident[:])
+                if shared:
+                    nc.vector.tensor_copy(out=h1_grouped32[:, 2 * P * a:2 * P * (a + 1), :], in_=h1_t[:].rearrange("q u t p -> q (t p) u"))
+                else:
+                    nc.scalar.copy(out=h1_grouped32[:, 2 * P * a:2 * P * (a + 1), :], in_=h1_t[:].rearrange("q u t p -> q (t p) u"))
+            h1_codes = stage.tile([P, BLK * P], U32, align_bytes=64)
+            h1_scales = stage.tile([P, BLK * P], U8, align_bytes=64)
+            nc.vector.quantize_mx(out=h1_codes[:].bitcast(FP8X4), scales=h1_scales[:], in_=h1_grouped[:].rearrange("q n f -> q (n f)"))
+
+            h2_planes = stage.tile([P, 4, BLK * P], BF16)
+            for c in range(4):
+                h2_acc = ps_h2.tile([P, BLK * P], F32, tag="h2")
+                nc.tensor.matmul_mx(out=h2_acc[:], lhsT=w1_codes[:, P * c:P * (c + 1)].bitcast(FP8X4),
+                                    lhsT_scale=w1_scales[:, P * c:P * (c + 1)],
+                                    rhs=h1_codes[:].bitcast(FP8X4), rhs_scale=h1_scales[:], start=True, stop=True)
+                if shared and c % 2 == 1:
+                    nc.vector.tensor_scalar(out=h2_planes[:, c, :], in0=h2_acc[:], scalar1=b1[:, c:c + 1], scalar2=0.0,
+                                            op0=ALU.add, op1=ALU.max)
+                else:
+                    nc.scalar.activation(out=h2_planes[:, c, :], in_=h2_acc[:], func=AF.Relu, bias=b1[:, c:c + 1], scale=1.0)
+            h2_grouped = stage.tile([P, BLK * P, 4], BF16, align_bytes=64)
+            grouped_runs = h2_grouped[:].rearrange("m (a i) c -> m a c i", i=4)
+            plane_runs = h2_planes[:].rearrange("m c (a i) -> m a c i", i=4)
+            if shared:
+                nc.vector.tensor_copy(out=grouped_runs, in_=plane_runs)
+            else:
+                nc.scalar.copy(out=grouped_runs, in_=plane_runs)
+            h2_codes = stage.tile([P, BLK * P], U32, align_bytes=64)
+            h2_scales = stage.tile([P, BLK * P], U8, align_bytes=64)
+            nc.vector.quantize_mx(out=h2_codes[:].bitcast(FP8X4), scales=h2_scales[:], in_=h2_grouped[:].rearrange("m n f -> m (n f)"))
+
+            y_acc = ps_x.tile([P, BLK * P], F32, tag="x")
+            nc.tensor.matmul_mx(out=y_acc[:], lhsT=w2_codes[:].bitcast(FP8X4), lhsT_scale=w2_scales[:],
+                                rhs=h2_codes[:].bitcast(FP8X4), rhs_scale=h2_scales[:], start=True, stop=True)
+            y_cols = stage.tile([P, BLK * P], F32)
+            nc.scalar.activation(out=y_cols[:], in_=y_acc[:], func=AF.Identity, bias=b2[:, 0:1], scale=1.0)
+            y_rows = ps_x.tile([P, BLK, P], F32, tag="x")
+            for t in range(BLK):
+                nc.tensor.transpose(y_rows[:, t, :], y_cols[:, P * t:P * (t + 1)], ident[:])
+            tiles = slice(BLK * i, BLK * (i + 1))
+            for t in range(BLK):
+                nc.scalar.activation(out=x_rows[:, 0, BLK * i + t, :], in_=y_rows[:, t, :], func=AF.Copy,
+                                     scale=nr[:, BLK * i + t:BLK * i + t + 1])
+            nc.vector.tensor_scalar(out=x_rows[:, 1, tiles, :], in0=x_rows[:, 0, tiles, :], scalar1=-2.0, scalar2=2.0,
+                                    op0=ALU.max, op1=ALU.min)
+            for sig in range(2):
+                nc.sync.dma_start(out=x_out[sig][:, tiles, :], in_=x_rows[:, sig, tiles, :])
+
+        def inputs(i):
+            b, tb, sub = place(i)
+            if b not in per_batch:
+                v_new = batch_pool.tile([P, 2, G * 3 * tb], F32, name="v")
+                th_new = batch_pool.tile([P, 2, G, tb], F32, name="th")
+                sq0_new = batch_pool.tile([P, 2, G, tb], F32, name="sq0")
+                per_batch[b] = (v_new, th_new, sq0_new)
+            v_view = per_batch[b][0][:].rearrange("p r (n s t) -> p r n s t", s=3, t=tb)
+            cols = []
+            for sig in range(2):
+                sig_cols = ps_spec.tile([P, BLK, P], F32, tag="spec", name="sig_cols")
+                for t in range(BLK):
+                    nc.tensor.transpose(sig_cols[:, t, :], x_rows[:, sig, BLK * i + t, :], ident[:])
+                cols.append(sig_cols)
+            for s, (sig, hf) in enumerate(FAST):
+                for r in range(2):
+                    z_cols = z_pool.tile([P, BLK, P], F32, name="z_cols")
+                    nc.scalar.activation(out=z_cols[:], in_=cols[sig][:], func=AF.Copy, scale=twist[:, 2 * hf + r:2 * hf + r + 1])
+                    z_rows = ps_spec.tile([P, BLK, P], F32, tag="spec", name="z_rows")
+                    for t in range(BLK):
+                        nc.tensor.transpose(z_rows[:, t, :], z_cols[:, t, :], ident[:])
+                    z_high = z_pool.tile([P, G, BLK], F32, name="z_high")
+                    nc.scalar.copy(out=z_high[:], in_=z_rows[:, :, G:N].rearrange("p t n -> p n t"))
+                    tensor_tensor(out=v_view[:, r, :, s, sub], in0=z_rows[:, :, 0:G].rearrange("p t n -> p n t"), in1=z_high[:], op=ALU.add)
+                if s == 0:
+                    x_cols[i] = stage.tile([P, BLK, P], F32, name="x_cols")
+                    nc.scalar.copy(out=x_cols[i][:], in_=cols[0][:])
+
+        def matrices(i):
+            b, tb, sub = place(i)
+            v, th, sq0 = per_batch[b]
+            spec0 = ps_spec.tile([P, BLK, P], F32, tag="spec")
+            for t in range(BLK):
+                nc.tensor.matmul(out=spec0[:, t, :], lhsT=x_cols[i][:, t, :], rhs=x_matrix, start=True, stop=True)
+            nc.scalar.activation(out=sq0[:, :, :, sub].rearrange("p r g t -> p (r g) t"), in_=spec0[:].rearrange("p t c -> p c t"),
+                                 func=AF.Square)
+            t_t = ps_spec.tile([P, BLK, P], BF16, tag="spec")
+            for t in range(BLK):
+                nc.tensor.transpose(t_t[:, t, :], t_pad[:, BLK * i + t, :], ident_bf[:])
+            t_cols = stage.tile([P, BLK, P], F32)
+            nc.scalar.copy(out=t_cols[:], in_=t_t[:])
+            th_acc = ps_spec.tile([P, BLK, P], F32, tag="spec")
+            for t in range(BLK):
+                if BLK * i + t == TILES - 1:
+                    nc.tensor.transpose(th_acc[:, t, :], t_cols[:, t, :], ident[:])
+                    nc.tensor.matmul(out=th_acc[:, t, 0:P - 1], lhsT=t_cols[:, t, :], rhs=t_matrix[:, 0:P - 1], start=True, stop=True)
+                else:
+                    nc.tensor.matmul(out=th_acc[:, t, :], lhsT=t_cols[:, t, :], rhs=t_matrix[:], start=True, stop=True)
+            nc.scalar.copy(out=th[:, :, :, sub].rearrange("p f g t -> p (f g) t"), in_=th_acc[:].rearrange("p t c -> p c t"))
+            if i == NBLK - 1:
+                products = stage.tile([P, N], F32)
+                tensor_tensor(out=products[:], in0=t_pad[:, TILES - 1, :], in1=last_col[:], op=ALU.mult)
+                nc.vector.tensor_reduce(out=th[:, 1, G - 1, tb - 1:tb], in_=products[:], axis=AX.X, op=ALU.add)
+
+        def transforms(b):
+            q = 3 * BLK * BATCHES[b][1]
+            x8 = 8 * q
+            v = per_batch[b][0]
+            src = v
+            for l, m in ((8, 1), (1, 8)):
+                y = m * q
+
+                def jy(ap):
+                    return ap.rearrange("p (j y) -> p j y", j=l)
+
+                def rjy(ap):
+                    return ap.rearrange("p r (j y) -> p r j y", j=l)
+
+                x = src[:].rearrange("p r (h x) -> p r h x", h=8)
+                add4 = fft.tile([P, 2, 4, x8], F32, tag="add4")
+                sub4 = fft.tile([P, 2, 4, x8], F32, tag="sub4")
+                tensor_tensor(out=add4[:], in0=x[:, :, 0:4, :], in1=x[:, :, 4:8, :], op=ALU.add)
+                tensor_tensor(out=sub4[:], in0=x[:, :, 0:4, :], in1=x[:, :, 4:8, :], op=ALU.subtract)
+                dst_tile = fft.tile([P, 2, G * q], F32, tag="mid", name="mid") if l > 1 else v
+                dst = dst_tile[:].rearrange("p r (j h y) -> p r j h y", j=l, h=8)
+                add2 = fft.tile([P, 2, 2, x8], F32, tag="add2")
+                sub2 = fft.tile([P, 2, 2, x8], F32, tag="sub2")
+                tensor_tensor(out=add2[:], in0=add4[:, :, 0:2, :], in1=add4[:, :, 2:4, :], op=ALU.add)
+                tensor_tensor(out=sub2[:], in0=add4[:, :, 0:2, :], in1=add4[:, :, 2:4, :], op=ALU.subtract)
+                tensor_tensor(out=dst[:, :, :, 0, :], in0=rjy(add2[:, :, 0, :]), in1=rjy(add2[:, :, 1, :]), op=ALU.add)
+                tensor_tensor(out=dst[:, :, :, 4, :], in0=rjy(add2[:, :, 0, :]), in1=rjy(add2[:, :, 1, :]), op=ALU.subtract)
+                tensor_tensor(out=dst[:, 0, :, 2, :], in0=jy(sub2[:, 0, 0, :]), in1=jy(sub2[:, 1, 1, :]), op=ALU.add)
+                tensor_tensor(out=dst[:, 1, :, 2, :], in0=jy(sub2[:, 1, 0, :]), in1=jy(sub2[:, 0, 1, :]), op=ALU.subtract)
+                tensor_tensor(out=dst[:, 0, :, 6, :], in0=jy(sub2[:, 0, 0, :]), in1=jy(sub2[:, 1, 1, :]), op=ALU.subtract)
+                tensor_tensor(out=dst[:, 1, :, 6, :], in0=jy(sub2[:, 1, 0, :]), in1=jy(sub2[:, 0, 1, :]), op=ALU.add)
+                plus = fft.tile([P, 2, x8], F32, tag="plus")
+                minus = fft.tile([P, 2, x8], F32, tag="minus")
+                tensor_tensor(out=plus[:], in0=sub4[:, 0, 1:4:2, :], in1=sub4[:, 1, 1:4:2, :], op=ALU.add)
+                tensor_tensor(out=minus[:], in0=sub4[:, 1, 1:4:2, :], in1=sub4[:, 0, 1:4:2, :], op=ALU.subtract)
+                e02p = fft.tile([P, 2, x8], F32, tag="e02p")
+                e02m = fft.tile([P, 2, x8], F32, tag="e02m")
+                e13p = fft.tile([P, 2, x8], F32, tag="e13p")
+                e13m = fft.tile([P, 2, x8], F32, tag="e13m")
+                tensor_tensor(out=e02p[:, 0, :], in0=sub4[:, 0, 0, :], in1=sub4[:, 1, 2, :], op=ALU.add)
+                tensor_tensor(out=e02p[:, 1, :], in0=sub4[:, 1, 0, :], in1=sub4[:, 0, 2, :], op=ALU.subtract)
+                tensor_tensor(out=e13p[:, 0, :], in0=plus[:, 0, :], in1=minus[:, 1, :], op=ALU.add)
+                tensor_tensor(out=e13p[:, 1, :], in0=minus[:, 0, :], in1=plus[:, 1, :], op=ALU.subtract)
+                for r in range(2):
+                    mul_add(out=dst[:, r, :, 1, :], in0=jy(e13p[:, r, :]), scalar=RHO, in1=jy(e02p[:, r, :]), op0=ALU.mult, op1=ALU.add)
+                    mul_add(out=dst[:, r, :, 5, :], in0=jy(e13p[:, r, :]), scalar=-RHO, in1=jy(e02p[:, r, :]), op0=ALU.mult, op1=ALU.add)
+                tensor_tensor(out=e02m[:, 0, :], in0=sub4[:, 0, 0, :], in1=sub4[:, 1, 2, :], op=ALU.subtract)
+                tensor_tensor(out=e02m[:, 1, :], in0=sub4[:, 1, 0, :], in1=sub4[:, 0, 2, :], op=ALU.add)
+                tensor_tensor(out=e13m[:, 0, :], in0=plus[:, 0, :], in1=minus[:, 1, :], op=ALU.subtract)
+                tensor_tensor(out=e13m[:, 1, :], in0=minus[:, 0, :], in1=plus[:, 1, :], op=ALU.add)
+                mul_add(out=dst[:, 0, :, 3, :], in0=jy(e13m[:, 1, :]), scalar=RHO, in1=jy(e02m[:, 0, :]), op0=ALU.mult, op1=ALU.add)
+                mul_add(out=dst[:, 1, :, 3, :], in0=jy(e13m[:, 0, :]), scalar=-RHO, in1=jy(e02m[:, 1, :]), op0=ALU.mult, op1=ALU.add)
+                mul_add(out=dst[:, 0, :, 7, :], in0=jy(e13m[:, 1, :]), scalar=-RHO, in1=jy(e02m[:, 0, :]), op0=ALU.mult, op1=ALU.add)
+                mul_add(out=dst[:, 1, :, 7, :], in0=jy(e13m[:, 0, :]), scalar=RHO, in1=jy(e02m[:, 1, :]), op0=ALU.mult, op1=ALU.add)
+                if l > 1:
+                    shape = [P, l - 1, 7, y]
+                    cross = fft.tile([P, 2, l - 1, 7, y], F32, tag="cross")
+                    for r in range(2):
+                        tensor_tensor(out=cross[:, r, :, :, :], in0=dst[:, r, 1:l, 1:8, :],
+                                      in1=twiddle[:, 1 + 2 * r, 1:l, :].unsqueeze(3).to_broadcast(shape), op=ALU.mult)
+                    for r in range(2):
+                        tensor_tensor(out=dst[:, r, 1:l, 1:8, :], in0=dst[:, r, 1:l, 1:8, :],
+                                      in1=twiddle[:, 0, 1:l, :].unsqueeze(3).to_broadcast(shape), op=ALU.mult)
+                    for r in range(2):
+                        tensor_tensor(out=dst[:, r, 1:l, 1:8, :], in0=dst[:, r, 1:l, 1:8, :], in1=cross[:, 1 - r, :, :, :], op=ALU.add)
+                src = dst_tile
+            spectrum = v[:].rearrange("p r (h y) -> p r h y", h=8)
+            for first, step in EIGHTHS:
+                nc.scalar.activation(out=spectrum[:, :, first:8:step, :], in_=spectrum[:, :, first:8:step, :], func=AF.Square)
+
+        def compare(b):
+            v, th, sq0 = per_batch[b]
+            tb = BLK * BATCHES[b][1]
+            squares = v[:].rearrange("p r (h k z) -> p r h k z", h=8, k=8)
+            power = fft.tile([P, G, 4, tb], F32, tag="power")
+            power_eighths = power[:].rearrange("p (h k) s t -> p h k (s t)", h=8)
+            tensor_tensor(out=power[:, :, 0, :], in0=sq0[:, 0, :, :], in1=sq0[:, 1, :, :], op=ALU.add)
+            for first, step in EIGHTHS:
+                tensor_tensor(out=power_eighths[:, first:8:step, :, tb:4 * tb], in0=squares[:, 0, first:8:step, :, :],
+                              in1=squares[:, 1, first:8:step, :, :], op=ALU.add)
+            th_view = th[:].rearrange("p f g t -> p g f t")
+            for sig in range(2):
+                of_sig = power[:, :, 2 * sig:2 * sig + 2, :]
+                tensor_tensor(out=of_sig, in0=of_sig, in1=th_view, op=ALU.subtract)
+            for sig in range(2):
+                of_sig = power[:, :, 2 * sig:2 * sig + 2, :]
+                nc.scalar.activation(out=of_sig, in_=of_sig, func=AF.Square, scale=1.0 / math.sqrt(128.0 * MEAN),
+                                     accum_out=d2_sums[:, sig, b:b + 1])
+
+        def blocks_of(b):
+            return range(BATCHES[b][0], BATCHES[b][0] + BATCHES[b][1])
+
+        for b in range(2):
+            for i in blocks_of(b):
+                network(i)
+                inputs(i)
+            for i in blocks_of(b):
+                matrices(i)
+        for b in range(len(BATCHES)):
+            transforms(b)
+            compare(b)
+            if b + 2 < len(BATCHES):
+                for i in blocks_of(b + 2):
+                    network(i)
+                    inputs(i)
+                for i in blocks_of(b + 2):
+                    matrices(i)
+
+        r0 = keep.tile([P, 2, TILES], F32)
+        for sig in range(2):
+            for t in range(TILES):
+                x_squares = stage.tile([P, N], F32)
+                nc.scalar.activation(out=x_squares[:], in_=x_rows[:, sig, t, :], func=AF.Square, accum_out=r0[:, sig, t:t + 1])
+
+        sums = keep.tile([P, P], F32)
+        nc.vector.memset(sums[:], 0.0)
+        r0_sums = keep.tile([P, 2], F32)
+        r0_squares = keep.tile([P, TILES], F32)
+        for sig in range(2):
+            nc.scalar.activation(out=r0_squares[:], in_=r0[:, sig, :], func=AF.Square, scale=1.0 / math.sqrt(MEAN),
+                                 accum_out=r0_sums[:, sig:sig + 1])
+        d2_total = keep.tile([P, 2], F32)
+        nc.vector.tensor_reduce(out=d2_total[:], in_=d2_sums[:], axis=AX.X, op=ALU.add)
+        tensor_tensor(out=sums[:, 0:2], in0=d2_total[:], in1=r0_sums[:], op=ALU.subtract)
+        sums_t = ps_spec.tile([P, P], F32, tag="spec")
+        nc.tensor.transpose(sums_t[:], sums[:], ident[:])
+        err = keep.tile([P, 1], F32)
+        nc.vector.tensor_reduce(out=err[:], in_=sums_t[:], axis=AX.X, op=ALU.add)
+        nc.sync.dma_start(out=out_1.rearrange("(a b) -> a b", a=1), in_=err[0:1, 0:1])
+        nc.sync.dma_start(out=out_3.rearrange("(a b) -> a b", a=1), in_=err[1:2, 0:1])

@@ -23,10 +23,11 @@ TILES = B // P
 BLK = 4
 NBLK = TILES // BLK
 G = 64
+L = 32
 FAST = ((0, 1), (1, 0), (1, 1))
+VECTOR_COPIES = (4, 1, 1)
 BATCHES = ((0, 1), (1, 2), (3, 2), (5, 2), (7, 1))
-SHARED = 3
-EIGHTHS = ((0, 2), (1, 4), (3, 4))
+SHARED = 2
 RHO = math.sqrt(0.5)
 MEAN = 2.0 * B * LAGS
 
@@ -41,7 +42,9 @@ def tile_qdtssolveronnx_pa_kernel(tc, h1, w_hid2, b_hid2, w_out, b_out, norm_roo
         keep = ctx.enter_context(tc.tile_pool(name="keep", bufs=1))
         h1_pool = ctx.enter_context(tc.tile_pool(name="h1_pool", bufs=3))
         stage = ctx.enter_context(tc.tile_pool(name="stage", bufs=2))
-        z_pool = ctx.enter_context(tc.tile_pool(name="z_pool", bufs=3))
+        x_pool = ctx.enter_context(tc.tile_pool(name="x_pool", bufs=4))
+        z_pool = ctx.enter_context(tc.tile_pool(name="z_pool", bufs=6))
+        sq_pool = ctx.enter_context(tc.tile_pool(name="sq_pool", bufs=3))
         batch_pool = ctx.enter_context(tc.tile_pool(name="batch_pool", bufs=2))
         fft = ctx.enter_context(tc.tile_pool(name="fft", bufs=1))
         ps_in = ctx.enter_context(tc.psum_pool(name="ps_in", bufs=1))
@@ -49,7 +52,7 @@ def tile_qdtssolveronnx_pa_kernel(tc, h1, w_hid2, b_hid2, w_out, b_out, norm_roo
         ps_x = ctx.enter_context(tc.psum_pool(name="ps_x", bufs=1))
         ps_spec = ctx.enter_context(tc.psum_pool(name="ps_spec", bufs=4))
 
-        w1_sb = keep.tile([P, 4, H], BF16)
+        w1_sb = h1_pool.tile([P, BLK, H], BF16, name="w1_sb", tag="h1_sb")
         nc.sync.dma_start(out=w1_sb[:], in_=w_hid2.rearrange("(p c) k -> p c k", c=4))
         h1_rows = h1.rearrange("(p t) k -> p t k", t=TILES)
         h1_tiles = {}
@@ -59,113 +62,63 @@ def tile_qdtssolveronnx_pa_kernel(tc, h1, w_hid2, b_hid2, w_out, b_out, norm_roo
             nc.sync.dma_start(out=h1_sb[:], in_=h1_rows[:, BLK * i:BLK * (i + 1), :])
             h1_tiles[i] = h1_sb
 
-        b1_bf = keep.tile([P, 4], BF16)
-        b2_bf = keep.tile([P, 1], BF16)
-        nr_bf = keep.tile([P, TILES], BF16)
+        b1 = keep.tile([P, 4], BF16)
+        b2 = keep.tile([P, 1], BF16)
+        nr = keep.tile([P, TILES], BF16)
         with nc.allow_non_contiguous_dma(reason="three short vectors, a few bytes a partition"):
-            nc.scalar.dma_start(out=b1_bf[:], in_=b_hid2.rearrange("(p c) -> p c", c=4))
-            nc.scalar.dma_start(out=b2_bf[:], in_=b_out.rearrange("(p o) -> p o", o=1))
-            nc.scalar.dma_start(out=nr_bf[:], in_=norm_root.rearrange("(p t) o -> p (t o)", t=TILES))
-        t_pad = keep.tile([P, TILES, N], BF16)
-        nc.vector.memset(t_pad[:], 0.0)
+            nc.scalar.dma_start(out=b1[:], in_=b_hid2.rearrange("(p c) -> p c", c=4))
+            nc.scalar.dma_start(out=b2[:], in_=b_out.rearrange("(p o) -> p o", o=1))
+            nc.scalar.dma_start(out=nr[:], in_=norm_root.rearrange("(p t) o -> p (t o)", t=TILES))
         ident = keep.tile([P, P], F32)
         make_identity(nc, ident[:])
-        ident_bf = keep.tile([P, P], BF16)
-        make_identity(nc, ident_bf[:])
         load_h1(0)
         w2_sb = keep.tile([P, H], BF16)
         nc.sync.dma_start(out=w2_sb[:], in_=w_out)
         load_h1(1)
-        nc.sync.dma_start(out=t_pad[:, :, 0:LAGS], in_=T.rearrange("(p t) c -> p t c", t=TILES))
+        ident_bf = keep.tile([P, P], BF16)
+        make_identity(nc, ident_bf[:])
 
-        def sines(phase, width, name):
-            nc.vector.tensor_single_scalar(out=phase, in_=phase, scalar=511, op=ALU.bitwise_and)
-            angle = fft.tile([P, width], F32, name=name + "_angle", tag="mid")
-            nc.vector.tensor_scalar(out=angle[:], in0=phase, scalar1=-256.0, scalar2=None, op0=ALU.add)
-            edge = fft.tile([P, width], F32, name=name + "_edge", tag="cross")
-            nc.vector.tensor_scalar(out=edge[:], in0=angle[:], scalar1=-256.0, scalar2=256.0, op0=ALU.is_equal, op1=ALU.mult)
-            nc.vector.tensor_tensor(out=angle[:], in0=angle[:], in1=edge[:], op=ALU.add)
-            table = keep.tile([P, width], F32, name=name + "_table")
-            nc.scalar.activation(out=table[:], in_=angle[:], func=AF.Sin, scale=math.pi / 256.0)
-            return table
-
-        COS = 256 + 128
-
-        W_TW = 4 * 56
-        row_phase = keep.tile([P, W_TW + N], I32)
-        tw_phase = row_phase[:, 0:W_TW].rearrange("p (k j h) -> p k j h", k=4, h=7)
-        for h in range(1, 8):
-            nc.gpsimd.iota(tw_phase[:, :, :, h - 1], pattern=[[128, 4], [8 * h, 8]], base=COS, channel_multiplier=0)
-        LAST_FREQ = 4 * (N - 1) + 1
-        nc.gpsimd.iota(row_phase[:, W_TW:W_TW + N], pattern=[[-LAST_FREQ, N]], base=LAGS * LAST_FREQ + COS, channel_multiplier=0)
-        row_table = sines(row_phase[:], W_TW + N, "row")
-        twiddle = row_table[:, 0:W_TW].rearrange("p (k j h) -> p k j h", k=4, h=7)
-        last_col = keep.tile([P, N], F32)
-        nc.vector.tensor_scalar(out=last_col[:], in0=row_table[:, W_TW:W_TW + N], scalar1=2.0, scalar2=None, op0=ALU.mult)
-
-        p_index = keep.tile([P, 2], I32)
-        nc.gpsimd.iota(p_index[:, 0:1], pattern=[[0, 1]], base=0, channel_multiplier=1)
-        nc.gpsimd.iota(p_index[:, 1:2], pattern=[[0, 1]], base=LAGS, channel_multiplier=-1)
-        p_float = keep.tile([P, 2], F32)
-        nc.vector.tensor_copy(out=p_float[:], in_=p_index[:])
-        freq = keep.tile([P, 2, G], I32)
-        nc.gpsimd.iota(freq[:], pattern=[[4, 2], [8, G]], base=1, channel_multiplier=0)
-        mat_phase = keep.tile([P, 4 * G + 4], I32)
-        for hf in range(2):
-            nc.gpsimd.iota(mat_phase[:, 4 * G + 2 * hf:4 * G + 2 * hf + 2], pattern=[[128, 2]], base=COS, channel_multiplier=1 + 4 * hf)
-        nc.vector.tensor_scalar(out=mat_phase[:, 0:G], in0=freq[:, 0, :], scalar1=p_float[:, 0:1], scalar2=float(COS),
-                                op0=ALU.mult, op1=ALU.add)
-        nc.vector.tensor_scalar(out=mat_phase[:, G:2 * G], in0=freq[:, 0, :], scalar1=p_float[:, 0:1], scalar2=256.0,
-                                op0=ALU.mult, op1=ALU.add)
-        nc.vector.tensor_scalar(out=mat_phase[:, 2 * G:4 * G], in0=freq[:].rearrange("p f g -> p (f g)"), scalar1=p_float[:, 1:2],
-                                scalar2=float(COS), op0=ALU.mult, op1=ALU.add)
-        mat_table = sines(mat_phase[:], 4 * G + 4, "mat")
-        x_matrix = mat_table[:, 0:2 * G]
-        t_matrix = keep.tile([P, 2 * G], F32)
-        nc.vector.tensor_scalar(out=t_matrix[:], in0=mat_table[:, 2 * G:4 * G], scalar1=2.0, scalar2=None, op0=ALU.mult)
-        twist = mat_table[:, 4 * G:4 * G + 4]
-
-        b1 = keep.tile([P, 4], F32)
-        nc.vector.tensor_copy(out=b1[:], in_=b1_bf[:])
-        b2 = keep.tile([P, 1], F32)
-        nc.vector.tensor_copy(out=b2[:], in_=b2_bf[:])
-        nr = keep.tile([P, TILES], F32)
-        nc.vector.tensor_copy(out=nr[:], in_=nr_bf[:])
-
-        w1_grouped = keep.tile([P, 4 * P, 4], BF16, align_bytes=64)
+        w1_grouped = stage.tile([P, 4 * P, 4], BF16, name="w1_grouped", tag="h1_grouped", align_bytes=64)
         w1_grouped32 = w1_grouped[:].bitcast(F32)
         w1_words = w1_sb[:].bitcast(F32)
         for a in range(2):
-            w1_t = ps_in.tile([P, 2, 2, P], F32, tag="in")
+            w1_t = ps_h2.tile([P, 2, 2, P], F32, tag="h2")
             for u in range(2):
                 for c in range(2):
                     nc.tensor.transpose(w1_t[:, u, c, :], w1_words[:, 2 * a + c, u:2 * P:2], ident[:])
-            nc.vector.tensor_copy(out=w1_grouped32[:, 2 * P * a:2 * P * (a + 1), :], in_=w1_t[:].rearrange("q u c m -> q (c m) u"))
+            (nc.vector.tensor_copy, nc.scalar.copy)[a](out=w1_grouped32[:, 2 * P * a:2 * P * (a + 1), :],
+                                                       in_=w1_t[:].rearrange("q u c m -> q (c m) u"))
         w1_codes = keep.tile([P, 4 * P], U32, align_bytes=64)
         w1_scales = keep.tile([P, 4 * P], U8, align_bytes=64)
         nc.vector.quantize_mx(out=w1_codes[:].bitcast(FP8X4), scales=w1_scales[:], in_=w1_grouped[:].rearrange("q n f -> q (n f)"))
-        w2_grouped = keep.tile([P, P, 4], BF16, align_bytes=64)
-        w2_words = w2_sb[:].bitcast(F32).rearrange("p (m u) -> p u m", u=2)
-        w2_t = ps_in.tile([P, 2, P], F32, tag="in")
-        for u in range(2):
-            nc.tensor.transpose(w2_t[:, u, :], w2_words[:, u, :], ident[:])
-        nc.vector.tensor_copy(out=w2_grouped[:].bitcast(F32), in_=w2_t[:].rearrange("q u n -> q n u"))
         w2_codes = keep.tile([P, P], U32, align_bytes=64)
         w2_scales = keep.tile([P, P], U8, align_bytes=64)
-        nc.vector.quantize_mx(out=w2_codes[:].bitcast(FP8X4), scales=w2_scales[:], in_=w2_grouped[:].rearrange("q n f -> q (n f)"))
 
-        x_rows = keep.tile([P, 2, TILES, N], F32)
+        def second_weights():
+            w2_grouped = keep.tile([P, P, 4], BF16, align_bytes=64)
+            w2_words = w2_sb[:].bitcast(F32).rearrange("p (m u) -> p u m", u=2)
+            w2_t = ps_x.tile([P, 2, P], F32, tag="x")
+            for u in range(2):
+                nc.tensor.transpose(w2_t[:, u, :], w2_words[:, u, :], ident[:])
+            nc.vector.tensor_copy(out=w2_grouped[:].bitcast(F32), in_=w2_t[:].rearrange("q u n -> q n u"))
+            nc.vector.quantize_mx(out=w2_codes[:].bitcast(FP8X4), scales=w2_scales[:], in_=w2_grouped[:].rearrange("q n f -> q (n f)"))
+
+        nr_all = keep.tile([P, TILES * P], BF16)
+
+        def spread_norm_root(i):
+            nr_t = ps_x.tile([P, BLK * P], BF16, tag="x")
+            for t in range(BLK):
+                at = BLK * i + t
+                nc.tensor.transpose(nr_t[:, P * t:P * (t + 1)], nr[:, at:at + 1].to_broadcast([P, P]), ident_bf[:])
+            nc.scalar.copy(out=nr_all[:, BLK * P * i:BLK * P * (i + 1)], in_=nr_t[:])
+
+        x_rows = {}
         x_out = (out_0.rearrange("(p t) j -> p t j", t=TILES), out_2.rearrange("(p t) j -> p t j", t=TILES))
-        d2_sums = keep.tile([P, 2, len(BATCHES)], F32)
-        per_batch = {}
         x_cols = {}
+        xc_cols = {}
+        h2_grouped = {}
 
-        def place(i):
-            b = [k for k, (first, count) in enumerate(BATCHES) if first <= i < first + count][0]
-            at = BLK * (i - BATCHES[b][0])
-            return b, BLK * BATCHES[b][1], slice(at, at + BLK)
-
-        def network(i):
+        def first_layer(i):
             shared = i < SHARED
             if i + 2 < NBLK:
                 load_h1(i + 2)
@@ -177,14 +130,11 @@ def tile_qdtssolveronnx_pa_kernel(tc, h1, w_hid2, b_hid2, w_out, b_out, norm_roo
                 for u in range(2):
                     for t in range(2):
                         nc.tensor.transpose(h1_t[:, u, t, :], h1_words[:, 2 * a + t, u:2 * P:2], ident[:])
-                if shared:
-                    nc.vector.tensor_copy(out=h1_grouped32[:, 2 * P * a:2 * P * (a + 1), :], in_=h1_t[:].rearrange("q u t p -> q (t p) u"))
-                else:
-                    nc.scalar.copy(out=h1_grouped32[:, 2 * P * a:2 * P * (a + 1), :], in_=h1_t[:].rearrange("q u t p -> q (t p) u"))
+                copy = nc.vector.tensor_copy if shared and a == 0 else nc.scalar.copy
+                copy(out=h1_grouped32[:, 2 * P * a:2 * P * (a + 1), :], in_=h1_t[:].rearrange("q u t p -> q (t p) u"))
             h1_codes = stage.tile([P, BLK * P], U32, align_bytes=64)
             h1_scales = stage.tile([P, BLK * P], U8, align_bytes=64)
             nc.vector.quantize_mx(out=h1_codes[:].bitcast(FP8X4), scales=h1_scales[:], in_=h1_grouped[:].rearrange("q n f -> q (n f)"))
-
             h2_planes = stage.tile([P, 4, BLK * P], BF16)
             for c in range(4):
                 h2_acc = ps_h2.tile([P, BLK * P], F32, tag="h2")
@@ -196,70 +146,142 @@ def tile_qdtssolveronnx_pa_kernel(tc, h1, w_hid2, b_hid2, w_out, b_out, norm_roo
                                             op0=ALU.add, op1=ALU.max)
                 else:
                     nc.scalar.activation(out=h2_planes[:, c, :], in_=h2_acc[:], func=AF.Relu, bias=b1[:, c:c + 1], scale=1.0)
-            h2_grouped = stage.tile([P, BLK * P, 4], BF16, align_bytes=64)
-            grouped_runs = h2_grouped[:].rearrange("m (a i) c -> m a c i", i=4)
-            plane_runs = h2_planes[:].rearrange("m c (a i) -> m a c i", i=4)
-            if shared:
-                nc.vector.tensor_copy(out=grouped_runs, in_=plane_runs)
-            else:
-                nc.scalar.copy(out=grouped_runs, in_=plane_runs)
+            h2_grouped[i] = stage.tile([P, BLK * P, 4], BF16, name="h2_grouped_new", align_bytes=64)
+            nc.vector.tensor_copy(out=h2_grouped[i][:].rearrange("m (a i) c -> m a c i", i=4),
+                                  in_=h2_planes[:].rearrange("m c (a i) -> m a c i", i=4))
+
+        def second_layer(i):
             h2_codes = stage.tile([P, BLK * P], U32, align_bytes=64)
             h2_scales = stage.tile([P, BLK * P], U8, align_bytes=64)
-            nc.vector.quantize_mx(out=h2_codes[:].bitcast(FP8X4), scales=h2_scales[:], in_=h2_grouped[:].rearrange("m n f -> m (n f)"))
-
+            nc.vector.quantize_mx(out=h2_codes[:].bitcast(FP8X4), scales=h2_scales[:], in_=h2_grouped[i][:].rearrange("m n f -> m (n f)"))
             y_acc = ps_x.tile([P, BLK * P], F32, tag="x")
             nc.tensor.matmul_mx(out=y_acc[:], lhsT=w2_codes[:].bitcast(FP8X4), lhsT_scale=w2_scales[:],
                                 rhs=h2_codes[:].bitcast(FP8X4), rhs_scale=h2_scales[:], start=True, stop=True)
-            y_cols = stage.tile([P, BLK * P], F32)
-            nc.scalar.activation(out=y_cols[:], in_=y_acc[:], func=AF.Identity, bias=b2[:, 0:1], scale=1.0)
-            y_rows = ps_x.tile([P, BLK, P], F32, tag="x")
+            x_cols[i] = x_pool.tile([P, BLK, P], F32, name="x_cols_new")
+            xc_cols[i] = stage.tile([P, BLK, P], F32, name="xc_cols_new")
+            mul_add(out=x_cols[i][:].rearrange("p t n -> p (t n)"), in0=y_acc[:], scalar=b2[:, 0:1],
+                    in1=nr_all[:, BLK * P * i:BLK * P * (i + 1)], op0=ALU.add, op1=ALU.mult)
+            nc.vector.tensor_scalar(out=xc_cols[i][:], in0=x_cols[i][:], scalar1=-2.0, scalar2=2.0, op0=ALU.max, op1=ALU.min)
+            x_t = ps_x.tile([P, BLK, P], F32, tag="x")
             for t in range(BLK):
-                nc.tensor.transpose(y_rows[:, t, :], y_cols[:, P * t:P * (t + 1)], ident[:])
+                nc.tensor.transpose(x_t[:, t, :], x_cols[i][:, t, :], ident[:])
             tiles = slice(BLK * i, BLK * (i + 1))
-            for t in range(BLK):
-                nc.scalar.activation(out=x_rows[:, 0, BLK * i + t, :], in_=y_rows[:, t, :], func=AF.Copy,
-                                     scale=nr[:, BLK * i + t:BLK * i + t + 1])
-            nc.vector.tensor_scalar(out=x_rows[:, 1, tiles, :], in0=x_rows[:, 0, tiles, :], scalar1=-2.0, scalar2=2.0,
+            x_rows[i] = x_pool.tile([P, 2, BLK, N], F32, name="x_rows_new")
+            nc.scalar.copy(out=x_rows[i][:, 0, :, :], in_=x_t[:])
+            nc.vector.tensor_scalar(out=x_rows[i][:, 1, :, :], in0=x_rows[i][:, 0, :, :], scalar1=-2.0, scalar2=2.0,
                                     op0=ALU.max, op1=ALU.min)
             for sig in range(2):
-                nc.sync.dma_start(out=x_out[sig][:, tiles, :], in_=x_rows[:, sig, tiles, :])
+                nc.sync.dma_start(out=x_out[sig][:, tiles, :], in_=x_rows[i][:, sig, :, :])
+
+        first_layer(0)
+        second_weights()
+        for i in range(2):
+            spread_norm_root(i)
+        second_layer(0)
+
+        t_pad = keep.tile([P, TILES, N], BF16)
+        nc.gpsimd.memset(t_pad[:], 0.0)
+        nc.sync.dma_start(out=t_pad[:, :, 0:LAGS], in_=T.rearrange("(p t) c -> p t c", t=TILES))
+
+        def sines(phase, width, name):
+            nc.vector.tensor_single_scalar(out=phase, in_=phase, scalar=511, op=ALU.bitwise_and)
+            angle = keep.tile([P, width], F32, name=name + "_angle")
+            nc.vector.tensor_scalar(out=angle[:], in0=phase, scalar1=-256.0, scalar2=None, op0=ALU.add)
+            edge = keep.tile([P, width], F32, name=name + "_edge")
+            nc.vector.tensor_scalar(out=edge[:], in0=angle[:], scalar1=-256.0, scalar2=256.0, op0=ALU.is_equal, op1=ALU.mult)
+            tensor_tensor(out=angle[:], in0=angle[:], in1=edge[:], op=ALU.add)
+            table = keep.tile([P, width], F32, name=name + "_table")
+            nc.scalar.activation(out=table[:], in_=angle[:], func=AF.Sin, scale=math.pi / 256.0)
+            return table
+
+        COS = 256 + 128
+
+        twist_phase = keep.tile([P, 8], I32)
+        for hf in range(2):
+            for e in range(2):
+                nc.gpsimd.iota(twist_phase[:, 4 * hf + e:4 * hf + e + 3:2], pattern=[[128, 2]], base=COS,
+                               channel_multiplier=8 * e + 4 * hf + 1)
+        parts = sines(twist_phase[:], 8, "twist")[:].rearrange("p (f s) -> p f s", f=2)
+        twist = keep.tile([P, 2, 4], F32)
+        for a in range(4):
+            quarter = slice(L * a, L * (a + 1))
+            nc.gpsimd.tensor_copy(out=twist[quarter, :, 0:4 - a], in_=parts[quarter, :, a:4])
+            if a > 0:
+                nc.gpsimd.tensor_copy(out=twist[quarter, :, 4 - a:4], in_=parts[quarter, :, 0:a])
+        ident_twice = keep.tile([P, 2 * P], F32)
+        for c in range(2):
+            nc.gpsimd.tensor_copy(out=ident_twice[:, P * c:P * (c + 1)], in_=ident[:])
+        turns = [ident_twice[:, P - L * w:2 * P - L * w] for w in range(4)]
+
+        x_matrix = keep.tile([P, 2 * G], F32)
+        t_matrix = keep.tile([P, 2 * G], F32)
+        last_col = keep.tile([P, N], F32)
+
+        def matrix_tables():
+            p_index = keep.tile([P, 2], I32)
+            nc.gpsimd.iota(p_index[:, 0:1], pattern=[[0, 1]], base=0, channel_multiplier=1)
+            nc.gpsimd.iota(p_index[:, 1:2], pattern=[[0, 1]], base=LAGS, channel_multiplier=-1)
+            p_float = keep.tile([P, 2], F32)
+            nc.vector.tensor_copy(out=p_float[:], in_=p_index[:])
+            freq = keep.tile([P, 2, G], I32)
+            nc.gpsimd.iota(freq[:], pattern=[[4, 2], [8, 2], [16, L]], base=1, channel_multiplier=0)
+            last_freq = 4 * (N - 1) + 1
+            phase = keep.tile([P, 6 * G], I32)
+            nc.gpsimd.iota(phase[:, 4 * G:4 * G + N], pattern=[[-last_freq, N]], base=LAGS * last_freq + COS, channel_multiplier=0)
+            nc.vector.tensor_scalar(out=phase[:, 0:G], in0=freq[:, 0, :], scalar1=p_float[:, 0:1], scalar2=float(COS),
+                                    op0=ALU.mult, op1=ALU.add)
+            nc.vector.tensor_scalar(out=phase[:, G:2 * G], in0=freq[:, 0, :], scalar1=p_float[:, 0:1], scalar2=256.0,
+                                    op0=ALU.mult, op1=ALU.add)
+            nc.vector.tensor_scalar(out=phase[:, 2 * G:4 * G], in0=freq[:].rearrange("p f g -> p (f g)"), scalar1=p_float[:, 1:2],
+                                    scalar2=float(COS), op0=ALU.mult, op1=ALU.add)
+            table = sines(phase[:], 6 * G, "matrix")
+            nc.vector.tensor_copy(out=x_matrix[:], in_=table[:, 0:2 * G])
+            nc.vector.tensor_scalar(out=t_matrix[:], in0=table[:, 2 * G:4 * G], scalar1=-2.0, scalar2=None, op0=ALU.mult)
+            nc.vector.tensor_scalar(out=last_col[:], in0=table[:, 4 * G:6 * G], scalar1=-2.0, scalar2=None, op0=ALU.mult)
+
+        r0 = keep.tile([P, 2, TILES], F32)
+        d2_sums = keep.tile([P, 2, NBLK], F32)
+        v = {}
+        sq = {}
+        th = {}
+        spectrum = {}
+
+        def place(i):
+            b = [k for k, (first, count) in enumerate(BATCHES) if first <= i < first + count][0]
+            at = BLK * (i - BATCHES[b][0])
+            return b, BLK * BATCHES[b][1], slice(at, at + BLK)
 
         def inputs(i):
             b, tb, sub = place(i)
-            if b not in per_batch:
-                v_new = batch_pool.tile([P, 2, G * 3 * tb], F32, name="v")
-                th_new = batch_pool.tile([P, 2, G, tb], F32, name="th")
-                sq0_new = batch_pool.tile([P, 2, G, tb], F32, name="sq0")
-                per_batch[b] = (v_new, th_new, sq0_new)
-            v_view = per_batch[b][0][:].rearrange("p r (n s t) -> p r n s t", s=3, t=tb)
-            cols = []
-            for sig in range(2):
-                sig_cols = ps_spec.tile([P, BLK, P], F32, tag="spec", name="sig_cols")
-                for t in range(BLK):
-                    nc.tensor.transpose(sig_cols[:, t, :], x_rows[:, sig, BLK * i + t, :], ident[:])
-                cols.append(sig_cols)
+            if b not in v:
+                v[b] = batch_pool.tile([P, L, 2, 2, 3 * tb], F32, name="v_new")
+            v_view = v[b][:].rearrange("p n r e (s t) -> p n r e s t", s=3)
+            cols = (x_cols[i], xc_cols[i])
             for s, (sig, hf) in enumerate(FAST):
-                for r in range(2):
+                twisted = []
+                for w in range(4):
                     z_cols = z_pool.tile([P, BLK, P], F32, name="z_cols")
-                    nc.scalar.activation(out=z_cols[:], in_=cols[sig][:], func=AF.Copy, scale=twist[:, 2 * hf + r:2 * hf + r + 1])
-                    z_rows = ps_spec.tile([P, BLK, P], F32, tag="spec", name="z_rows")
-                    for t in range(BLK):
-                        nc.tensor.transpose(z_rows[:, t, :], z_cols[:, t, :], ident[:])
-                    z_high = z_pool.tile([P, G, BLK], F32, name="z_high")
-                    nc.scalar.copy(out=z_high[:], in_=z_rows[:, :, G:N].rearrange("p t n -> p n t"))
-                    tensor_tensor(out=v_view[:, r, :, s, sub], in0=z_rows[:, :, 0:G].rearrange("p t n -> p n t"), in1=z_high[:], op=ALU.add)
-                if s == 0:
-                    x_cols[i] = stage.tile([P, BLK, P], F32, name="x_cols")
-                    nc.scalar.copy(out=x_cols[i][:], in_=cols[0][:])
+                    factor = twist[:, hf, w:w + 1]
+                    if w < VECTOR_COPIES[s]:
+                        nc.vector.tensor_scalar(out=z_cols[:], in0=cols[sig][:], scalar1=factor, scalar2=None, op0=ALU.mult)
+                    else:
+                        nc.scalar.activation(out=z_cols[:], in_=cols[sig][:], func=AF.Copy, scale=factor)
+                    twisted.append(z_cols)
+                v_rows = ps_spec.tile([P, BLK, P], F32, tag="spec", name="v_rows")
+                for t in range(BLK):
+                    for w in range(4):
+                        nc.tensor.matmul(out=v_rows[:, t, :], lhsT=twisted[w][:, t, :], rhs=turns[w], is_transpose=True,
+                                         start=w == 0, stop=w == 3)
+                nc.scalar.copy(out=v_view[:, :, :, :, s, sub].rearrange("p n r e t -> p (r e) n t"),
+                               in_=v_rows[:].rearrange("p t (k n) -> p k n t", n=L))
 
         def matrices(i):
-            b, tb, sub = place(i)
-            v, th, sq0 = per_batch[b]
+            sq[i] = sq_pool.tile([P, BLK, 2, 2, 2, G], F32, name="sq_new")
+            th[i] = sq_pool.tile([P, BLK, 2 * G], F32, name="th_new")
             spec0 = ps_spec.tile([P, BLK, P], F32, tag="spec")
             for t in range(BLK):
-                nc.tensor.matmul(out=spec0[:, t, :], lhsT=x_cols[i][:, t, :], rhs=x_matrix, start=True, stop=True)
-            nc.scalar.activation(out=sq0[:, :, :, sub].rearrange("p r g t -> p (r g) t"), in_=spec0[:].rearrange("p t c -> p c t"),
-                                 func=AF.Square)
+                nc.tensor.matmul(out=spec0[:, t, :], lhsT=x_cols[i][:, t, :], rhs=x_matrix[:], start=True, stop=True)
+            nc.scalar.activation(out=sq[i][:, :, :, 0, 0, :], in_=spec0[:].rearrange("p t (r g) -> p t r g", r=2), func=AF.Square)
             t_t = ps_spec.tile([P, BLK, P], BF16, tag="spec")
             for t in range(BLK):
                 nc.tensor.transpose(t_t[:, t, :], t_pad[:, BLK * i + t, :], ident_bf[:])
@@ -272,125 +294,131 @@ def tile_qdtssolveronnx_pa_kernel(tc, h1, w_hid2, b_hid2, w_out, b_out, norm_roo
                     nc.tensor.matmul(out=th_acc[:, t, 0:P - 1], lhsT=t_cols[:, t, :], rhs=t_matrix[:, 0:P - 1], start=True, stop=True)
                 else:
                     nc.tensor.matmul(out=th_acc[:, t, :], lhsT=t_cols[:, t, :], rhs=t_matrix[:], start=True, stop=True)
-            nc.scalar.copy(out=th[:, :, :, sub].rearrange("p f g t -> p (f g) t"), in_=th_acc[:].rearrange("p t c -> p c t"))
+            nc.scalar.copy(out=th[i][:], in_=th_acc[:])
             if i == NBLK - 1:
                 products = stage.tile([P, N], F32)
                 tensor_tensor(out=products[:], in0=t_pad[:, TILES - 1, :], in1=last_col[:], op=ALU.mult)
-                nc.vector.tensor_reduce(out=th[:, 1, G - 1, tb - 1:tb], in_=products[:], axis=AX.X, op=ALU.add)
+                nc.vector.tensor_reduce(out=th[i][:, BLK - 1, N - 1:N], in_=products[:], axis=AX.X, op=ALU.add)
+
+        def lag_zero(i):
+            for sig in range(2):
+                for t in range(BLK):
+                    x_squares = stage.tile([P, N], F32)
+                    nc.scalar.activation(out=x_squares[:], in_=x_rows[i][:, sig, t, :], func=AF.Square,
+                                         accum_out=r0[:, sig, BLK * i + t:BLK * i + t + 1])
+
+        def turned_sums(out, k1, k2, x, y):
+            sums = out[:, :, 2 * k1:2 * k2 + 2:2 * (k2 - k1) + 1, :]
+            diffs = out[:, :, 2 * k1 + 1:2 * k2 + 1:2 * (k2 - k1) - 1, :]
+            tensor_tensor(out=sums, in0=x, in1=y[:, :, ::-1, :], op=ALU.add)
+            tensor_tensor(out=diffs, in0=x[:, :, ::-1, :], in1=y, op=ALU.subtract)
+
+        def join(a, b, out, n, q, groups):
+            a_k, out_k = (ap.rearrange("p g (k r) q -> p g k (r q)", r=2) for ap in (a, out))
+
+            def turned(k):
+                t = math.sin(math.pi * k / n) / math.cos(math.pi * k / n)
+                d = fft.tile([P, groups, 4, q], F32, name="d", tag="d", bufs=3)
+                for g in range(groups):
+                    outer = b[:, g, 2 * k:2 * (n - k) + 2:2 * (n - 2 * k) + 1, :]
+                    inner = b[:, g, 2 * k + 1:2 * (n - k) + 1:2 * (n - 2 * k) - 1, :]
+                    mul_add(out=d[:, g, 0:4:3, :], in0=inner, scalar=t, in1=outer, op0=ALU.mult, op1=ALU.add)
+                    mul_add(out=d[:, g, 1:3, :], in0=outer, scalar=-t, in1=inner, op0=ALU.mult, op1=ALU.add)
+                return d
+
+            def joined(k, d):
+                c = math.cos(math.pi * k / n)
+                for g in range(groups):
+                    d_pair = d[:, g, :, :].rearrange("p (k r) q -> p k (r q)", r=2)
+                    a_pair = a_k[:, g, k:n - k + 1:n - 2 * k, :]
+                    mul_add(out=out_k[:, g, k:2 * n - k + 1:2 * (n - k), :], in0=d_pair, scalar=c, in1=a_pair, op0=ALU.mult, op1=ALU.add)
+                    mul_add(out=out_k[:, g, n - k:n + k + 1:2 * k, :], in0=d_pair[:, ::-1, :], scalar=-c, in1=a_pair[:, ::-1, :],
+                            op0=ALU.mult, op1=ALU.add)
+
+            half = n // 2
+            ahead = turned(1)
+            tensor_tensor(out=out_k[:, :, 0, :], in0=a_k[:, :, 0, :], in1=b[:, :, 0:2, :].rearrange("p g r q -> p g (r q)"), op=ALU.add)
+            tensor_tensor(out=out_k[:, :, n, :], in0=a_k[:, :, 0, :], in1=b[:, :, 0:2, :].rearrange("p g r q -> p g (r q)"), op=ALU.subtract)
+            for k in range(1, half):
+                d = ahead
+                if k + 1 < half:
+                    ahead = turned(k + 1)
+                else:
+                    turned_sums(out, half, 3 * half, a[:, :, n:n + 2, :], b[:, :, n:n + 2, :])
+                joined(k, d)
 
         def transforms(b):
-            q = 3 * BLK * BATCHES[b][1]
-            x8 = 8 * q
-            v = per_batch[b][0]
-            src = v
-            for l, m in ((8, 1), (1, 8)):
-                y = m * q
+            q = 6 * BLK * BATCHES[b][1]
+            x = v[b][:].rearrange("p (m h) r e z -> p m (h r e z)", m=8)
+            fours = fft.tile([P, 2, 4, 4, 2, q], F32, tag="front")
+            add4, sub4 = fours[:, 0, :, :, :, :], fours[:, 1, :, :, :, :]
+            flat = "p m g r q -> p m (g r q)"
+            tensor_tensor(out=add4.rearrange(flat), in0=x[:, 0:4, :], in1=x[:, 4:8, :], op=ALU.add)
+            tensor_tensor(out=sub4.rearrange(flat), in0=x[:, 0:4, :], in1=x[:, 4:8, :], op=ALU.subtract)
+            add2 = fft.tile([P, 2, 4, 2, q], F32, tag="add2")
+            sub2 = fft.tile([P, 2, 4, 2, q], F32, tag="sub2")
+            diag = fft.tile([P, 2, 4, 2, q], F32, tag="diag")
+            eighths = fft.tile([P, 4, 16, q], F32, tag="mid", bufs=2)
+            tensor_tensor(out=add2[:].rearrange(flat), in0=add4[:, 0:2, :, :, :].rearrange(flat), in1=add4[:, 2:4, :, :, :].rearrange(flat), op=ALU.add)
+            tensor_tensor(out=diag[:, :, :, 0, :], in0=sub4[:, 1:4:2, :, 0, :], in1=sub4[:, 1:4:2, :, 1, :], op=ALU.add)
+            tensor_tensor(out=sub2[:].rearrange(flat), in0=add4[:, 0:2, :, :, :].rearrange(flat), in1=add4[:, 2:4, :, :, :].rearrange(flat), op=ALU.subtract)
+            tensor_tensor(out=diag[:, :, :, 1, :], in0=sub4[:, 1:4:2, :, 1, :], in1=sub4[:, 1:4:2, :, 0, :], op=ALU.subtract)
+            tensor_tensor(out=eighths[:, :, 0:2, :], in0=add2[:, 0, :, :, :], in1=add2[:, 1, :, :, :], op=ALU.add)
+            tensor_tensor(out=eighths[:, :, 8:10, :], in0=add2[:, 0, :, :, :], in1=add2[:, 1, :, :, :], op=ALU.subtract)
+            straight = fft.tile([P, 4, 4, q], F32, tag="straight")
+            turned_sums(straight[:], 0, 1, sub4[:, 0, :, :, :], sub4[:, 2, :, :, :])
+            slanted = fft.tile([P, 4, 4, q], F32, tag="add2")
+            turned_sums(slanted[:], 0, 1, diag[:, 0, :, :, :], diag[:, 1, :, :, :])
+            turned_sums(eighths[:], 2, 6, sub2[:, 0, :, :, :], sub2[:, 1, :, :, :])
+            mul_add(out=eighths[:, :, 2:4, :], in0=slanted[:, :, 0:2, :], scalar=RHO, in1=straight[:, :, 0:2, :], op0=ALU.mult, op1=ALU.add)
+            mul_add(out=eighths[:, :, 10:12, :], in0=slanted[:, :, 0:2, :], scalar=-RHO, in1=straight[:, :, 0:2, :], op0=ALU.mult, op1=ALU.add)
+            for k, sign in ((3, 1.0), (7, -1.0)):
+                mul_add(out=eighths[:, :, 2 * k, :], in0=slanted[:, :, 3, :], scalar=sign * RHO, in1=straight[:, :, 2, :], op0=ALU.mult, op1=ALU.add)
+                mul_add(out=eighths[:, :, 2 * k + 1, :], in0=slanted[:, :, 2, :], scalar=-sign * RHO, in1=straight[:, :, 3, :], op0=ALU.mult, op1=ALU.add)
+            sixteenths = fft.tile([P, 2, L, q], F32, tag="front")
+            join(eighths[:, 0:2, :, :], eighths[:, 2:4, :, :], sixteenths[:], 8, q, 2)
+            spectrum[b] = fft.tile([P, 1, 2 * L, q], F32, name="spectrum_new", tag="mid", bufs=2)
+            join(sixteenths[:, 0:1, :, :], sixteenths[:, 1:2, :, :], spectrum[b][:], 16, q, 1)
 
-                def jy(ap):
-                    return ap.rearrange("p (j y) -> p j y", j=l)
-
-                def rjy(ap):
-                    return ap.rearrange("p r (j y) -> p r j y", j=l)
-
-                x = src[:].rearrange("p r (h x) -> p r h x", h=8)
-                add4 = fft.tile([P, 2, 4, x8], F32, tag="add4")
-                sub4 = fft.tile([P, 2, 4, x8], F32, tag="sub4")
-                tensor_tensor(out=add4[:], in0=x[:, :, 0:4, :], in1=x[:, :, 4:8, :], op=ALU.add)
-                tensor_tensor(out=sub4[:], in0=x[:, :, 0:4, :], in1=x[:, :, 4:8, :], op=ALU.subtract)
-                dst_tile = fft.tile([P, 2, G * q], F32, tag="mid", name="mid") if l > 1 else v
-                dst = dst_tile[:].rearrange("p r (j h y) -> p r j h y", j=l, h=8)
-                add2 = fft.tile([P, 2, 2, x8], F32, tag="add2")
-                sub2 = fft.tile([P, 2, 2, x8], F32, tag="sub2")
-                tensor_tensor(out=add2[:], in0=add4[:, :, 0:2, :], in1=add4[:, :, 2:4, :], op=ALU.add)
-                tensor_tensor(out=sub2[:], in0=add4[:, :, 0:2, :], in1=add4[:, :, 2:4, :], op=ALU.subtract)
-                tensor_tensor(out=dst[:, :, :, 0, :], in0=rjy(add2[:, :, 0, :]), in1=rjy(add2[:, :, 1, :]), op=ALU.add)
-                tensor_tensor(out=dst[:, :, :, 4, :], in0=rjy(add2[:, :, 0, :]), in1=rjy(add2[:, :, 1, :]), op=ALU.subtract)
-                tensor_tensor(out=dst[:, 0, :, 2, :], in0=jy(sub2[:, 0, 0, :]), in1=jy(sub2[:, 1, 1, :]), op=ALU.add)
-                tensor_tensor(out=dst[:, 1, :, 2, :], in0=jy(sub2[:, 1, 0, :]), in1=jy(sub2[:, 0, 1, :]), op=ALU.subtract)
-                tensor_tensor(out=dst[:, 0, :, 6, :], in0=jy(sub2[:, 0, 0, :]), in1=jy(sub2[:, 1, 1, :]), op=ALU.subtract)
-                tensor_tensor(out=dst[:, 1, :, 6, :], in0=jy(sub2[:, 1, 0, :]), in1=jy(sub2[:, 0, 1, :]), op=ALU.add)
-                plus = fft.tile([P, 2, x8], F32, tag="plus")
-                minus = fft.tile([P, 2, x8], F32, tag="minus")
-                tensor_tensor(out=plus[:], in0=sub4[:, 0, 1:4:2, :], in1=sub4[:, 1, 1:4:2, :], op=ALU.add)
-                tensor_tensor(out=minus[:], in0=sub4[:, 1, 1:4:2, :], in1=sub4[:, 0, 1:4:2, :], op=ALU.subtract)
-                e02p = fft.tile([P, 2, x8], F32, tag="e02p")
-                e02m = fft.tile([P, 2, x8], F32, tag="e02m")
-                e13p = fft.tile([P, 2, x8], F32, tag="e13p")
-                e13m = fft.tile([P, 2, x8], F32, tag="e13m")
-                tensor_tensor(out=e02p[:, 0, :], in0=sub4[:, 0, 0, :], in1=sub4[:, 1, 2, :], op=ALU.add)
-                tensor_tensor(out=e02p[:, 1, :], in0=sub4[:, 1, 0, :], in1=sub4[:, 0, 2, :], op=ALU.subtract)
-                tensor_tensor(out=e13p[:, 0, :], in0=plus[:, 0, :], in1=minus[:, 1, :], op=ALU.add)
-                tensor_tensor(out=e13p[:, 1, :], in0=minus[:, 0, :], in1=plus[:, 1, :], op=ALU.subtract)
+        def compare(i):
+            b, tb, sub = place(i)
+            view = spectrum[b][:, 0, :, :].rearrange("p (k r) (e s t) -> p r e k s t", r=2, e=2, s=3)
+            for s, (sig, hf) in enumerate(FAST):
                 for r in range(2):
-                    mul_add(out=dst[:, r, :, 1, :], in0=jy(e13p[:, r, :]), scalar=RHO, in1=jy(e02p[:, r, :]), op0=ALU.mult, op1=ALU.add)
-                    mul_add(out=dst[:, r, :, 5, :], in0=jy(e13p[:, r, :]), scalar=-RHO, in1=jy(e02p[:, r, :]), op0=ALU.mult, op1=ALU.add)
-                tensor_tensor(out=e02m[:, 0, :], in0=sub4[:, 0, 0, :], in1=sub4[:, 1, 2, :], op=ALU.subtract)
-                tensor_tensor(out=e02m[:, 1, :], in0=sub4[:, 1, 0, :], in1=sub4[:, 0, 2, :], op=ALU.add)
-                tensor_tensor(out=e13m[:, 0, :], in0=plus[:, 0, :], in1=minus[:, 1, :], op=ALU.subtract)
-                tensor_tensor(out=e13m[:, 1, :], in0=minus[:, 0, :], in1=plus[:, 1, :], op=ALU.add)
-                mul_add(out=dst[:, 0, :, 3, :], in0=jy(e13m[:, 1, :]), scalar=RHO, in1=jy(e02m[:, 0, :]), op0=ALU.mult, op1=ALU.add)
-                mul_add(out=dst[:, 1, :, 3, :], in0=jy(e13m[:, 0, :]), scalar=-RHO, in1=jy(e02m[:, 1, :]), op0=ALU.mult, op1=ALU.add)
-                mul_add(out=dst[:, 0, :, 7, :], in0=jy(e13m[:, 1, :]), scalar=-RHO, in1=jy(e02m[:, 0, :]), op0=ALU.mult, op1=ALU.add)
-                mul_add(out=dst[:, 1, :, 7, :], in0=jy(e13m[:, 0, :]), scalar=RHO, in1=jy(e02m[:, 1, :]), op0=ALU.mult, op1=ALU.add)
-                if l > 1:
-                    shape = [P, l - 1, 7, y]
-                    cross = fft.tile([P, 2, l - 1, 7, y], F32, tag="cross")
-                    for r in range(2):
-                        tensor_tensor(out=cross[:, r, :, :, :], in0=dst[:, r, 1:l, 1:8, :],
-                                      in1=twiddle[:, 1 + 2 * r, 1:l, :].unsqueeze(3).to_broadcast(shape), op=ALU.mult)
-                    for r in range(2):
-                        tensor_tensor(out=dst[:, r, 1:l, 1:8, :], in0=dst[:, r, 1:l, 1:8, :],
-                                      in1=twiddle[:, 0, 1:l, :].unsqueeze(3).to_broadcast(shape), op=ALU.mult)
-                    for r in range(2):
-                        tensor_tensor(out=dst[:, r, 1:l, 1:8, :], in0=dst[:, r, 1:l, 1:8, :], in1=cross[:, 1 - r, :, :, :], op=ALU.add)
-                src = dst_tile
-            spectrum = v[:].rearrange("p r (h y) -> p r h y", h=8)
-            for first, step in EIGHTHS:
-                nc.scalar.activation(out=spectrum[:, :, first:8:step, :], in_=spectrum[:, :, first:8:step, :], func=AF.Square)
-
-        def compare(b):
-            v, th, sq0 = per_batch[b]
-            tb = BLK * BATCHES[b][1]
-            squares = v[:].rearrange("p r (h k z) -> p r h k z", h=8, k=8)
-            power = fft.tile([P, G, 4, tb], F32, tag="power")
-            power_eighths = power[:].rearrange("p (h k) s t -> p h k (s t)", h=8)
-            tensor_tensor(out=power[:, :, 0, :], in0=sq0[:, 0, :, :], in1=sq0[:, 1, :, :], op=ALU.add)
-            for first, step in EIGHTHS:
-                tensor_tensor(out=power_eighths[:, first:8:step, :, tb:4 * tb], in0=squares[:, 0, first:8:step, :, :],
-                              in1=squares[:, 1, first:8:step, :, :], op=ALU.add)
-            th_view = th[:].rearrange("p f g t -> p g f t")
+                    nc.scalar.activation(out=sq[i][:, :, r, sig, hf, :].rearrange("p t (e k) -> p e k t", e=2), in_=view[:, r, :, :, s, sub],
+                                         func=AF.Square)
             for sig in range(2):
-                of_sig = power[:, :, 2 * sig:2 * sig + 2, :]
-                tensor_tensor(out=of_sig, in0=of_sig, in1=th_view, op=ALU.subtract)
-            for sig in range(2):
-                of_sig = power[:, :, 2 * sig:2 * sig + 2, :]
-                nc.scalar.activation(out=of_sig, in_=of_sig, func=AF.Square, scale=1.0 / math.sqrt(128.0 * MEAN),
-                                     accum_out=d2_sums[:, sig, b:b + 1])
+                diff = ps_spec.tile([P, BLK, P], F32, tag="spec", name="diff")
+                for t in range(BLK):
+                    for r in range(2):
+                        nc.tensor.matmul(out=diff[:, t, :], lhsT=sq[i][:, t, r, sig, :, :].rearrange("p f g -> p (f g)"), rhs=ident[:],
+                                         is_transpose=True, start=r == 0, stop=False)
+                    nc.tensor.matmul(out=diff[:, t, :], lhsT=th[i][:, t, :], rhs=ident[:], is_transpose=True, start=False, stop=True)
+                squared = stage.tile([P, BLK, P], F32)
+                nc.scalar.activation(out=squared[:], in_=diff[:], func=AF.Square, scale=1.0 / math.sqrt(128.0 * MEAN),
+                                     accum_out=d2_sums[:, sig, i:i + 1])
 
         def blocks_of(b):
             return range(BATCHES[b][0], BATCHES[b][0] + BATCHES[b][1])
 
-        for b in range(2):
-            for i in blocks_of(b):
-                network(i)
-                inputs(i)
-            for i in blocks_of(b):
-                matrices(i)
-        for b in range(len(BATCHES)):
-            transforms(b)
-            compare(b)
-            if b + 2 < len(BATCHES):
-                for i in blocks_of(b + 2):
-                    network(i)
+        for b in range(len(BATCHES) + 1):
+            if b < len(BATCHES):
+                for i in blocks_of(b):
+                    if i > 0:
+                        if i + 1 < NBLK:
+                            spread_norm_root(i + 1)
+                        first_layer(i)
+                        second_layer(i)
                     inputs(i)
-                for i in blocks_of(b + 2):
+                if b == 0:
+                    matrix_tables()
+            if b > 0:
+                for i in blocks_of(b - 1):
                     matrices(i)
-
-        r0 = keep.tile([P, 2, TILES], F32)
-        for sig in range(2):
-            for t in range(TILES):
-                x_squares = stage.tile([P, N], F32)
-                nc.scalar.activation(out=x_squares[:], in_=x_rows[:, sig, t, :], func=AF.Square, accum_out=r0[:, sig, t:t + 1])
+                    lag_zero(i)
+                transforms(b - 1)
+                for i in blocks_of(b - 1):
+                    compare(i)
 
         sums = keep.tile([P, P], F32)
         nc.vector.memset(sums[:], 0.0)

@@ -25,7 +25,7 @@ NBLK = TILES // BLK
 G = 64
 L = 32
 FAST = ((0, 1), (1, 0), (1, 1))
-VECTOR_COPIES = (4, 1, 1)
+VECTOR_COPIES = (2, 1, 1)
 BATCHES = ((0, 1), (1, 2), (3, 2), (5, 2), (7, 1))
 SHARED = 2
 RHO = math.sqrt(0.5)
@@ -54,26 +54,30 @@ def tile_qdtssolveronnx_pa_kernel(tc, h1, w_hid2, b_hid2, w_out, b_out, norm_roo
 
         w1_sb = h1_pool.tile([P, BLK, H], BF16, name="w1_sb", tag="h1_sb")
         nc.sync.dma_start(out=w1_sb[:], in_=w_hid2.rearrange("(p c) k -> p c k", c=4))
-        h1_rows = h1.rearrange("(p t) k -> p t k", t=TILES)
+        h1_rows = h1.rearrange("(i p t) k -> i p t k", p=P, t=BLK)
         h1_tiles = {}
 
         def load_h1(i):
             h1_sb = h1_pool.tile([P, BLK, H], BF16, name="h1_sb")
-            nc.sync.dma_start(out=h1_sb[:], in_=h1_rows[:, BLK * i:BLK * (i + 1), :])
+            nc.sync.dma_start(out=h1_sb[:], in_=h1_rows[i])
             h1_tiles[i] = h1_sb
 
         b1 = keep.tile([P, 4], BF16)
         b2 = keep.tile([P, 1], BF16)
-        nr = keep.tile([P, TILES], BF16)
-        with nc.allow_non_contiguous_dma(reason="three short vectors, a few bytes a partition"):
+        with nc.allow_non_contiguous_dma(reason="two short vectors, a few bytes a partition"):
             nc.scalar.dma_start(out=b1[:], in_=b_hid2.rearrange("(p c) -> p c", c=4))
             nc.scalar.dma_start(out=b2[:], in_=b_out.rearrange("(p o) -> p o", o=1))
-            nc.scalar.dma_start(out=nr[:], in_=norm_root.rearrange("(p t) o -> p (t o)", t=TILES))
+        zero = keep.tile([P, 1], F32)
+        nc.vector.memset(zero[:], 0.0)
+        first_sine = keep.tile([P, 1], F32)
+        nc.scalar.activation(out=first_sine[:], in_=zero[:], func=AF.Sin)
         ident = keep.tile([P, P], F32)
         make_identity(nc, ident[:])
         load_h1(0)
         w2_sb = keep.tile([P, H], BF16)
         nc.sync.dma_start(out=w2_sb[:], in_=w_out)
+        nr_all = keep.tile([P, B], BF16)
+        nc.sync.dma_start(out=nr_all[:], in_=norm_root.rearrange("r o -> (r o)").partition_broadcast(P))
         load_h1(1)
         ident_bf = keep.tile([P, P], BF16)
         make_identity(nc, ident_bf[:])
@@ -103,17 +107,8 @@ def tile_qdtssolveronnx_pa_kernel(tc, h1, w_hid2, b_hid2, w_out, b_out, norm_roo
             nc.vector.tensor_copy(out=w2_grouped[:].bitcast(F32), in_=w2_t[:].rearrange("q u n -> q n u"))
             nc.vector.quantize_mx(out=w2_codes[:].bitcast(FP8X4), scales=w2_scales[:], in_=w2_grouped[:].rearrange("q n f -> q (n f)"))
 
-        nr_all = keep.tile([P, TILES * P], BF16)
-
-        def spread_norm_root(i):
-            nr_t = ps_x.tile([P, BLK * P], BF16, tag="x")
-            for t in range(BLK):
-                at = BLK * i + t
-                nc.tensor.transpose(nr_t[:, P * t:P * (t + 1)], nr[:, at:at + 1].to_broadcast([P, P]), ident_bf[:])
-            nc.scalar.copy(out=nr_all[:, BLK * P * i:BLK * P * (i + 1)], in_=nr_t[:])
-
         x_rows = {}
-        x_out = (out_0.rearrange("(p t) j -> p t j", t=TILES), out_2.rearrange("(p t) j -> p t j", t=TILES))
+        x_out = [out.rearrange("(i p t) j -> i p t j", p=P, t=BLK) for out in (out_0, out_2)]
         x_cols = {}
         xc_cols = {}
         h2_grouped = {}
@@ -159,29 +154,28 @@ def tile_qdtssolveronnx_pa_kernel(tc, h1, w_hid2, b_hid2, w_out, b_out, norm_roo
                                 rhs=h2_codes[:].bitcast(FP8X4), rhs_scale=h2_scales[:], start=True, stop=True)
             x_cols[i] = x_pool.tile([P, BLK, P], F32, name="x_cols_new")
             xc_cols[i] = stage.tile([P, BLK, P], F32, name="xc_cols_new")
-            mul_add(out=x_cols[i][:].rearrange("p t n -> p (t n)"), in0=y_acc[:], scalar=b2[:, 0:1],
-                    in1=nr_all[:, BLK * P * i:BLK * P * (i + 1)], op0=ALU.add, op1=ALU.mult)
+            mul_add(out=x_cols[i][:], in0=y_acc[:].rearrange("j (t p) -> j t p", t=BLK), scalar=b2[:, 0:1],
+                    in1=nr_all[:, BLK * P * i:BLK * P * (i + 1)].rearrange("j (p t) -> j t p", t=BLK), op0=ALU.add, op1=ALU.mult)
             nc.vector.tensor_scalar(out=xc_cols[i][:], in0=x_cols[i][:], scalar1=-2.0, scalar2=2.0, op0=ALU.max, op1=ALU.min)
             x_t = ps_x.tile([P, BLK, P], F32, tag="x")
             for t in range(BLK):
                 nc.tensor.transpose(x_t[:, t, :], x_cols[i][:, t, :], ident[:])
-            tiles = slice(BLK * i, BLK * (i + 1))
             x_rows[i] = x_pool.tile([P, 2, BLK, N], F32, name="x_rows_new")
             nc.scalar.copy(out=x_rows[i][:, 0, :, :], in_=x_t[:])
             nc.vector.tensor_scalar(out=x_rows[i][:, 1, :, :], in0=x_rows[i][:, 0, :, :], scalar1=-2.0, scalar2=2.0,
                                     op0=ALU.max, op1=ALU.min)
             for sig in range(2):
-                nc.sync.dma_start(out=x_out[sig][:, tiles, :], in_=x_rows[i][:, sig, :, :])
+                nc.sync.dma_start(out=x_out[sig][i], in_=x_rows[i][:, sig, :, :])
 
         first_layer(0)
         second_weights()
-        for i in range(2):
-            spread_norm_root(i)
         second_layer(0)
 
         t_pad = keep.tile([P, TILES, N], BF16)
         nc.gpsimd.memset(t_pad[:], 0.0)
-        nc.sync.dma_start(out=t_pad[:, :, 0:LAGS], in_=T.rearrange("(p t) c -> p t c", t=TILES))
+        t_rows = T.rearrange("(i p t) c -> i p t c", p=P, t=BLK)
+        for i in range(NBLK):
+            nc.sync.dma_start(out=t_pad[:, BLK * i:BLK * (i + 1), 0:LAGS], in_=t_rows[i])
 
         def sines(phase, width, name):
             nc.vector.tensor_single_scalar(out=phase, in_=phase, scalar=511, op=ALU.bitwise_and)
@@ -241,7 +235,7 @@ def tile_qdtssolveronnx_pa_kernel(tc, h1, w_hid2, b_hid2, w_out, b_out, norm_roo
 
         r0 = keep.tile([P, 2, TILES], F32)
         d2_sums = keep.tile([P, 2, NBLK], F32)
-        v = {}
+        fours = {}
         sq = {}
         th = {}
         spectrum = {}
@@ -253,9 +247,9 @@ def tile_qdtssolveronnx_pa_kernel(tc, h1, w_hid2, b_hid2, w_out, b_out, norm_roo
 
         def inputs(i):
             b, tb, sub = place(i)
-            if b not in v:
-                v[b] = batch_pool.tile([P, L, 2, 2, 3 * tb], F32, name="v_new")
-            v_view = v[b][:].rearrange("p n r e (s t) -> p n r e s t", s=3)
+            if b not in fours:
+                fours[b] = batch_pool.tile([P, 2, L // 2, 2, 2, 3 * tb], F32, name="fours_new")
+            fours_view = fours[b][:].rearrange("p f n r e (s t) -> p f n r e s t", s=3)
             cols = (x_cols[i], xc_cols[i])
             for s, (sig, hf) in enumerate(FAST):
                 twisted = []
@@ -272,8 +266,13 @@ def tile_qdtssolveronnx_pa_kernel(tc, h1, w_hid2, b_hid2, w_out, b_out, norm_roo
                     for w in range(4):
                         nc.tensor.matmul(out=v_rows[:, t, :], lhsT=twisted[w][:, t, :], rhs=turns[w], is_transpose=True,
                                          start=w == 0, stop=w == 3)
-                nc.scalar.copy(out=v_view[:, :, :, :, s, sub].rearrange("p n r e t -> p (r e) n t"),
-                               in_=v_rows[:].rearrange("p t (k n) -> p k n t", n=L))
+                v_parts = v_rows[:].rearrange("p t (k n) -> p k n t", n=L)
+                v_high = z_pool.tile([P, L // 2, 4, BLK], F32, name="v_high", bufs=2)
+                high = v_high[:].rearrange("p n k t -> p k n t")
+                nc.scalar.copy(out=high, in_=v_parts[:, :, L // 2:L, :])
+                for f, op in enumerate((ALU.add, ALU.subtract)):
+                    tensor_tensor(out=fours_view[:, f, :, :, :, s, sub].rearrange("p n r e t -> p (r e) n t"),
+                                  in0=v_parts[:, :, 0:L // 2, :], in1=high, op=op)
 
         def matrices(i):
             sq[i] = sq_pool.tile([P, BLK, 2, 2, 2, G], F32, name="sq_new")
@@ -313,12 +312,12 @@ def tile_qdtssolveronnx_pa_kernel(tc, h1, w_hid2, b_hid2, w_out, b_out, norm_roo
             tensor_tensor(out=sums, in0=x, in1=y[:, :, ::-1, :], op=ALU.add)
             tensor_tensor(out=diffs, in0=x[:, :, ::-1, :], in1=y, op=ALU.subtract)
 
-        def join(a, b, out, n, q, groups):
-            a_k, out_k = (ap.rearrange("p g (k r) q -> p g k (r q)", r=2) for ap in (a, out))
+        def join(a, b, out, n, q, groups, order):
+            a_k, b_k, out_k = (ap.rearrange("p g (k r) q -> p g k (r q)", r=2) for ap in (a, b, out))
 
             def turned(k):
                 t = math.sin(math.pi * k / n) / math.cos(math.pi * k / n)
-                d = fft.tile([P, groups, 4, q], F32, name="d", tag="d", bufs=3)
+                d = fft.tile([P, groups, 4, q], F32, name="d", tag="d", bufs=4)
                 for g in range(groups):
                     outer = b[:, g, 2 * k:2 * (n - k) + 2:2 * (n - 2 * k) + 1, :]
                     inner = b[:, g, 2 * k + 1:2 * (n - k) + 1:2 * (n - 2 * k) - 1, :]
@@ -336,25 +335,19 @@ def tile_qdtssolveronnx_pa_kernel(tc, h1, w_hid2, b_hid2, w_out, b_out, norm_roo
                             op0=ALU.mult, op1=ALU.add)
 
             half = n // 2
-            ahead = turned(1)
-            tensor_tensor(out=out_k[:, :, 0, :], in0=a_k[:, :, 0, :], in1=b[:, :, 0:2, :].rearrange("p g r q -> p g (r q)"), op=ALU.add)
-            tensor_tensor(out=out_k[:, :, n, :], in0=a_k[:, :, 0, :], in1=b[:, :, 0:2, :].rearrange("p g r q -> p g (r q)"), op=ALU.subtract)
-            for k in range(1, half):
-                d = ahead
-                if k + 1 < half:
-                    ahead = turned(k + 1)
-                else:
-                    turned_sums(out, half, 3 * half, a[:, :, n:n + 2, :], b[:, :, n:n + 2, :])
-                joined(k, d)
+            made = [turned(k) for k in order[0:2]]
+            tensor_tensor(out=out_k[:, :, 0, :], in0=a_k[:, :, 0, :], in1=b_k[:, :, 0, :], op=ALU.add)
+            tensor_tensor(out=out_k[:, :, n, :], in0=a_k[:, :, 0, :], in1=b_k[:, :, 0, :], op=ALU.subtract)
+            turned_sums(out, half, 3 * half, a[:, :, n:n + 2, :], b[:, :, n:n + 2, :])
+            for at, k in enumerate(order):
+                if at + 2 < len(order):
+                    made.append(turned(order[at + 2]))
+                joined(k, made[at])
 
         def transforms(b):
             q = 6 * BLK * BATCHES[b][1]
-            x = v[b][:].rearrange("p (m h) r e z -> p m (h r e z)", m=8)
-            fours = fft.tile([P, 2, 4, 4, 2, q], F32, tag="front")
-            add4, sub4 = fours[:, 0, :, :, :, :], fours[:, 1, :, :, :, :]
+            add4, sub4 = (fours[b][:, f, :, :, :, :].rearrange("p (m h) r e z -> p m h r (e z)", h=4) for f in range(2))
             flat = "p m g r q -> p m (g r q)"
-            tensor_tensor(out=add4.rearrange(flat), in0=x[:, 0:4, :], in1=x[:, 4:8, :], op=ALU.add)
-            tensor_tensor(out=sub4.rearrange(flat), in0=x[:, 0:4, :], in1=x[:, 4:8, :], op=ALU.subtract)
             add2 = fft.tile([P, 2, 4, 2, q], F32, tag="add2")
             sub2 = fft.tile([P, 2, 4, 2, q], F32, tag="sub2")
             diag = fft.tile([P, 2, 4, 2, q], F32, tag="diag")
@@ -375,18 +368,21 @@ def tile_qdtssolveronnx_pa_kernel(tc, h1, w_hid2, b_hid2, w_out, b_out, norm_roo
             for k, sign in ((3, 1.0), (7, -1.0)):
                 mul_add(out=eighths[:, :, 2 * k, :], in0=slanted[:, :, 3, :], scalar=sign * RHO, in1=straight[:, :, 2, :], op0=ALU.mult, op1=ALU.add)
                 mul_add(out=eighths[:, :, 2 * k + 1, :], in0=slanted[:, :, 2, :], scalar=-sign * RHO, in1=straight[:, :, 3, :], op0=ALU.mult, op1=ALU.add)
-            sixteenths = fft.tile([P, 2, L, q], F32, tag="front")
-            join(eighths[:, 0:2, :, :], eighths[:, 2:4, :, :], sixteenths[:], 8, q, 2)
+            sixteenths = fft.tile([P, 2, L, q], F32, tag="sixteenths")
+            join(eighths[:, 0:2, :, :], eighths[:, 2:4, :, :], sixteenths[:], 8, q, 2, (2, 1, 3))
             spectrum[b] = fft.tile([P, 1, 2 * L, q], F32, name="spectrum_new", tag="mid", bufs=2)
-            join(sixteenths[:, 0:1, :, :], sixteenths[:, 1:2, :, :], spectrum[b][:], 16, q, 1)
+            join(sixteenths[:, 0:1, :, :], sixteenths[:, 1:2, :, :], spectrum[b][:], 16, q, 1, (4, 2, 6, 1, 7, 3, 5))
 
         def compare(i):
             b, tb, sub = place(i)
             view = spectrum[b][:, 0, :, :].rearrange("p (k r) (e s t) -> p r e k s t", r=2, e=2, s=3)
             for s, (sig, hf) in enumerate(FAST):
                 for r in range(2):
-                    nc.scalar.activation(out=sq[i][:, :, r, sig, hf, :].rearrange("p t (e k) -> p e k t", e=2), in_=view[:, r, :, :, s, sub],
-                                         func=AF.Square)
+                    squares, part = sq[i][:, :, r, sig, hf, :].rearrange("p t (e k) -> p e k t", e=2), view[:, r, :, :, s, sub]
+                    if r == 1 and i == NBLK - 1:
+                        tensor_tensor(out=squares, in0=part, in1=part, op=ALU.mult)
+                    else:
+                        nc.scalar.activation(out=squares, in_=part, func=AF.Square)
             for sig in range(2):
                 diff = ps_spec.tile([P, BLK, P], F32, tag="spec", name="diff")
                 for t in range(BLK):
@@ -401,21 +397,25 @@ def tile_qdtssolveronnx_pa_kernel(tc, h1, w_hid2, b_hid2, w_out, b_out, norm_roo
         def blocks_of(b):
             return range(BATCHES[b][0], BATCHES[b][0] + BATCHES[b][1])
 
-        for b in range(len(BATCHES) + 1):
-            if b < len(BATCHES):
+        last = len(BATCHES) - 1
+        for b in range(last + 2):
+            if b <= last:
                 for i in blocks_of(b):
                     if i > 0:
-                        if i + 1 < NBLK:
-                            spread_norm_root(i + 1)
                         first_layer(i)
                         second_layer(i)
                     inputs(i)
                 if b == 0:
                     matrix_tables()
+                if b == last:
+                    for i in blocks_of(b):
+                        matrices(i)
+                        lag_zero(i)
             if b > 0:
-                for i in blocks_of(b - 1):
-                    matrices(i)
-                    lag_zero(i)
+                if b <= last:
+                    for i in blocks_of(b - 1):
+                        matrices(i)
+                        lag_zero(i)
                 transforms(b - 1)
                 for i in blocks_of(b - 1):
                     compare(i)

@@ -25,7 +25,8 @@ NBLK = TILES // BLK
 G = 64
 L = 32
 FAST = ((0, 1), (1, 0), (1, 1))
-VECTOR_COPIES = (2, 1, 1)
+VECTOR_COPIES = (1, 1, 1)
+FIRST_COPIES = 3
 BATCHES = ((0, 1), (1, 2), (3, 2), (5, 2), (7, 1))
 SHARED = 2
 RHO = math.sqrt(0.5)
@@ -45,12 +46,14 @@ def tile_qdtssolveronnx_pa_kernel(tc, h1, w_hid2, b_hid2, w_out, b_out, norm_roo
         x_pool = ctx.enter_context(tc.tile_pool(name="x_pool", bufs=4))
         z_pool = ctx.enter_context(tc.tile_pool(name="z_pool", bufs=6))
         sq_pool = ctx.enter_context(tc.tile_pool(name="sq_pool", bufs=3))
+        th_pool = ctx.enter_context(tc.tile_pool(name="th_pool", bufs=6))
         batch_pool = ctx.enter_context(tc.tile_pool(name="batch_pool", bufs=2))
         fft = ctx.enter_context(tc.tile_pool(name="fft", bufs=1))
         ps_in = ctx.enter_context(tc.psum_pool(name="ps_in", bufs=1))
         ps_h2 = ctx.enter_context(tc.psum_pool(name="ps_h2", bufs=2))
         ps_x = ctx.enter_context(tc.psum_pool(name="ps_x", bufs=1))
-        ps_spec = ctx.enter_context(tc.psum_pool(name="ps_spec", bufs=4))
+        ps_spec = ctx.enter_context(tc.psum_pool(name="ps_spec", bufs=3))
+        ps_t = ctx.enter_context(tc.psum_pool(name="ps_t", bufs=1))
 
         w1_sb = h1_pool.tile([P, BLK, H], BF16, name="w1_sb", tag="h1_sb")
         nc.sync.dma_start(out=w1_sb[:], in_=w_hid2.rearrange("(p c) k -> p c k", c=4))
@@ -179,12 +182,12 @@ def tile_qdtssolveronnx_pa_kernel(tc, h1, w_hid2, b_hid2, w_out, b_out, norm_roo
 
         def sines(phase, width, name):
             nc.vector.tensor_single_scalar(out=phase, in_=phase, scalar=511, op=ALU.bitwise_and)
-            angle = keep.tile([P, width], F32, name=name + "_angle")
+            angle = fft.tile([P, width], F32, name=name + "_angle", tag="add2")
             nc.vector.tensor_scalar(out=angle[:], in0=phase, scalar1=-256.0, scalar2=None, op0=ALU.add)
-            edge = keep.tile([P, width], F32, name=name + "_edge")
+            edge = fft.tile([P, width], F32, name=name + "_edge", tag="sub2")
             nc.vector.tensor_scalar(out=edge[:], in0=angle[:], scalar1=-256.0, scalar2=256.0, op0=ALU.is_equal, op1=ALU.mult)
             tensor_tensor(out=angle[:], in0=angle[:], in1=edge[:], op=ALU.add)
-            table = keep.tile([P, width], F32, name=name + "_table")
+            table = fft.tile([P, width], F32, name=name + "_table", tag="straight")
             nc.scalar.activation(out=table[:], in_=angle[:], func=AF.Sin, scale=math.pi / 256.0)
             return table
 
@@ -220,7 +223,7 @@ def tile_qdtssolveronnx_pa_kernel(tc, h1, w_hid2, b_hid2, w_out, b_out, norm_roo
             freq = keep.tile([P, 2, G], I32)
             nc.gpsimd.iota(freq[:], pattern=[[4, 2], [8, 2], [16, L]], base=1, channel_multiplier=0)
             last_freq = 4 * (N - 1) + 1
-            phase = keep.tile([P, 6 * G], I32)
+            phase = fft.tile([P, 6 * G], I32, tag="diag")
             nc.gpsimd.iota(phase[:, 4 * G:4 * G + N], pattern=[[-last_freq, N]], base=LAGS * last_freq + COS, channel_multiplier=0)
             nc.vector.tensor_scalar(out=phase[:, 0:G], in0=freq[:, 0, :], scalar1=p_float[:, 0:1], scalar2=float(COS),
                                     op0=ALU.mult, op1=ALU.add)
@@ -256,7 +259,7 @@ def tile_qdtssolveronnx_pa_kernel(tc, h1, w_hid2, b_hid2, w_out, b_out, norm_roo
                 for w in range(4):
                     z_cols = z_pool.tile([P, BLK, P], F32, name="z_cols")
                     factor = twist[:, hf, w:w + 1]
-                    if w < VECTOR_COPIES[s]:
+                    if w < (VECTOR_COPIES[s] if i > 0 else FIRST_COPIES):
                         nc.vector.tensor_scalar(out=z_cols[:], in0=cols[sig][:], scalar1=factor, scalar2=None, op0=ALU.mult)
                     else:
                         nc.scalar.activation(out=z_cols[:], in_=cols[sig][:], func=AF.Copy, scale=factor)
@@ -276,17 +279,19 @@ def tile_qdtssolveronnx_pa_kernel(tc, h1, w_hid2, b_hid2, w_out, b_out, norm_roo
 
         def matrices(i):
             sq[i] = sq_pool.tile([P, BLK, 2, 2, 2, G], F32, name="sq_new")
-            th[i] = sq_pool.tile([P, BLK, 2 * G], F32, name="th_new")
             spec0 = ps_spec.tile([P, BLK, P], F32, tag="spec")
             for t in range(BLK):
                 nc.tensor.matmul(out=spec0[:, t, :], lhsT=x_cols[i][:, t, :], rhs=x_matrix[:], start=True, stop=True)
             nc.scalar.activation(out=sq[i][:, :, :, 0, 0, :], in_=spec0[:].rearrange("p t (r g) -> p t r g", r=2), func=AF.Square)
-            t_t = ps_spec.tile([P, BLK, P], BF16, tag="spec")
+
+        def targets(i):
+            th[i] = th_pool.tile([P, BLK, 2 * G], F32, name="th_new")
+            t_t = ps_t.tile([P, BLK, P], BF16, tag="t")
             for t in range(BLK):
                 nc.tensor.transpose(t_t[:, t, :], t_pad[:, BLK * i + t, :], ident_bf[:])
             t_cols = stage.tile([P, BLK, P], F32)
             nc.scalar.copy(out=t_cols[:], in_=t_t[:])
-            th_acc = ps_spec.tile([P, BLK, P], F32, tag="spec")
+            th_acc = ps_t.tile([P, BLK, P], F32, tag="t")
             for t in range(BLK):
                 if BLK * i + t == TILES - 1:
                     nc.tensor.transpose(th_acc[:, t, :], t_cols[:, t, :], ident[:])
@@ -418,6 +423,7 @@ def tile_qdtssolveronnx_pa_kernel(tc, h1, w_hid2, b_hid2, w_out, b_out, norm_roo
                         lag_zero(i)
                 transforms(b - 1)
                 for i in blocks_of(b - 1):
+                    targets(i)
                     compare(i)
 
         sums = keep.tile([P, P], F32)

@@ -25,7 +25,7 @@ NBLK = TILES // BLK
 G = 64
 L = 32
 FAST = ((0, 1), (1, 0), (1, 1))
-VECTOR_COPIES = (1, 1, 1)
+VECTOR_COPIES = (3, 1, 1)
 FIRST_COPIES = 3
 BATCHES = ((0, 1), (1, 2), (3, 2), (5, 2), (7, 1))
 SHARED = 2
@@ -238,7 +238,7 @@ def tile_qdtssolveronnx_pa_kernel(tc, h1, w_hid2, b_hid2, w_out, b_out, norm_roo
 
         r0 = keep.tile([P, 2, TILES], F32)
         d2_sums = keep.tile([P, 2, NBLK], F32)
-        fours = {}
+        v = {}
         sq = {}
         th = {}
         spectrum = {}
@@ -250,9 +250,9 @@ def tile_qdtssolveronnx_pa_kernel(tc, h1, w_hid2, b_hid2, w_out, b_out, norm_roo
 
         def inputs(i):
             b, tb, sub = place(i)
-            if b not in fours:
-                fours[b] = batch_pool.tile([P, 2, L // 2, 2, 2, 3 * tb], F32, name="fours_new")
-            fours_view = fours[b][:].rearrange("p f n r e (s t) -> p f n r e s t", s=3)
+            if b not in v:
+                v[b] = batch_pool.tile([P, L, 2, 2, 3 * tb], F32, name="v_new")
+            v_view = v[b][:].rearrange("p n r e (s t) -> p n r e s t", s=3)
             cols = (x_cols[i], xc_cols[i])
             for s, (sig, hf) in enumerate(FAST):
                 twisted = []
@@ -269,13 +269,8 @@ def tile_qdtssolveronnx_pa_kernel(tc, h1, w_hid2, b_hid2, w_out, b_out, norm_roo
                     for w in range(4):
                         nc.tensor.matmul(out=v_rows[:, t, :], lhsT=twisted[w][:, t, :], rhs=turns[w], is_transpose=True,
                                          start=w == 0, stop=w == 3)
-                v_parts = v_rows[:].rearrange("p t (k n) -> p k n t", n=L)
-                v_high = z_pool.tile([P, L // 2, 4, BLK], F32, name="v_high", bufs=2)
-                high = v_high[:].rearrange("p n k t -> p k n t")
-                nc.scalar.copy(out=high, in_=v_parts[:, :, L // 2:L, :])
-                for f, op in enumerate((ALU.add, ALU.subtract)):
-                    tensor_tensor(out=fours_view[:, f, :, :, :, s, sub].rearrange("p n r e t -> p (r e) n t"),
-                                  in0=v_parts[:, :, 0:L // 2, :], in1=high, op=op)
+                nc.scalar.copy(out=v_view[:, :, :, :, s, sub].rearrange("p n r e t -> p (r e) n t"),
+                               in_=v_rows[:].rearrange("p t (k n) -> p k n t", n=L))
 
         def matrices(i):
             sq[i] = sq_pool.tile([P, BLK, 2, 2, 2, G], F32, name="sq_new")
@@ -351,7 +346,11 @@ def tile_qdtssolveronnx_pa_kernel(tc, h1, w_hid2, b_hid2, w_out, b_out, norm_roo
 
         def transforms(b):
             q = 6 * BLK * BATCHES[b][1]
-            add4, sub4 = (fours[b][:, f, :, :, :, :].rearrange("p (m h) r e z -> p m h r (e z)", h=4) for f in range(2))
+            x = v[b][:].rearrange("p (m h) r e z -> p m (h r e z)", m=8)
+            fours = fft.tile([P, 2, 4, 4, 2, q], F32, tag="sixteenths")
+            add4, sub4 = fours[:, 0, :, :, :, :], fours[:, 1, :, :, :, :]
+            tensor_tensor(out=add4.rearrange("p m g r q -> p m (g r q)"), in0=x[:, 0:4, :], in1=x[:, 4:8, :], op=ALU.add)
+            tensor_tensor(out=sub4.rearrange("p m g r q -> p m (g r q)"), in0=x[:, 0:4, :], in1=x[:, 4:8, :], op=ALU.subtract)
             flat = "p m g r q -> p m (g r q)"
             add2 = fft.tile([P, 2, 4, 2, q], F32, tag="add2")
             sub2 = fft.tile([P, 2, 4, 2, q], F32, tag="sub2")
@@ -400,31 +399,31 @@ def tile_qdtssolveronnx_pa_kernel(tc, h1, w_hid2, b_hid2, w_out, b_out, norm_roo
                                      accum_out=d2_sums[:, sig, i:i + 1])
 
         def blocks_of(b):
-            return range(BATCHES[b][0], BATCHES[b][0] + BATCHES[b][1])
+            return range(BATCHES[b][0], BATCHES[b][0] + BATCHES[b][1]) if 0 <= b < len(BATCHES) else range(0)
 
         last = len(BATCHES) - 1
-        for b in range(last + 2):
-            if b <= last:
+        for b in range(last + 3):
+            for i in blocks_of(b):
+                if i > 0:
+                    first_layer(i)
+                    second_layer(i)
+                inputs(i)
+            if b == 0:
+                matrix_tables()
+            for i in blocks_of(b - 2):
+                compare(i)
+            if b == last:
                 for i in blocks_of(b):
-                    if i > 0:
-                        first_layer(i)
-                        second_layer(i)
-                    inputs(i)
-                if b == 0:
-                    matrix_tables()
-                if b == last:
-                    for i in blocks_of(b):
-                        matrices(i)
-                        lag_zero(i)
-            if b > 0:
-                if b <= last:
-                    for i in blocks_of(b - 1):
-                        matrices(i)
-                        lag_zero(i)
-                transforms(b - 1)
+                    matrices(i)
+                    lag_zero(i)
+            if b <= last:
                 for i in blocks_of(b - 1):
-                    targets(i)
-                    compare(i)
+                    matrices(i)
+                    lag_zero(i)
+            for i in blocks_of(b - 1):
+                targets(i)
+            if 0 < b < last + 2:
+                transforms(b - 1)
 
         sums = keep.tile([P, P], F32)
         nc.vector.memset(sums[:], 0.0)

@@ -237,7 +237,12 @@ def tile_qdtssolveronnx_pa_kernel(tc, h1, w_hid2, b_hid2, w_out, b_out, norm_roo
             nc.vector.tensor_scalar(out=last_col[:], in0=table[:, 4 * G:6 * G], scalar1=-2.0, scalar2=None, op0=ALU.mult)
 
         r0 = keep.tile([P, 2, TILES], F32)
-        d2_sums = keep.tile([P, 2, NBLK], F32)
+        d2_sums = keep.tile([P, 2, NBLK - 1], F32)
+        shares = []
+        for name in ("shares_before", "shares_last"):
+            share = keep.tile([P, P], F32, name=name)
+            nc.gpsimd.memset(share[:], 0.0)
+            shares.append(share)
         v = {}
         sq = {}
         th = {}
@@ -395,8 +400,8 @@ def tile_qdtssolveronnx_pa_kernel(tc, h1, w_hid2, b_hid2, w_out, b_out, norm_roo
                                          is_transpose=True, start=r == 0, stop=False)
                     nc.tensor.matmul(out=diff[:, t, :], lhsT=th[i][:, t, :], rhs=ident[:], is_transpose=True, start=False, stop=True)
                 squared = stage.tile([P, BLK, P], F32)
-                nc.scalar.activation(out=squared[:], in_=diff[:], func=AF.Square, scale=1.0 / math.sqrt(128.0 * MEAN),
-                                     accum_out=d2_sums[:, sig, i:i + 1])
+                into = d2_sums[:, sig, i:i + 1] if i < NBLK - 1 else shares[1][:, sig:sig + 1]
+                nc.scalar.activation(out=squared[:], in_=diff[:], func=AF.Square, scale=1.0 / math.sqrt(128.0 * MEAN), accum_out=into)
 
         def blocks_of(b):
             return range(BATCHES[b][0], BATCHES[b][0] + BATCHES[b][1]) if 0 <= b < len(BATCHES) else range(0)
@@ -425,8 +430,6 @@ def tile_qdtssolveronnx_pa_kernel(tc, h1, w_hid2, b_hid2, w_out, b_out, norm_roo
             if 0 < b < last + 2:
                 transforms(b - 1)
 
-        sums = keep.tile([P, P], F32)
-        nc.vector.memset(sums[:], 0.0)
         r0_sums = keep.tile([P, 2], F32)
         r0_squares = keep.tile([P, TILES], F32)
         for sig in range(2):
@@ -434,10 +437,11 @@ def tile_qdtssolveronnx_pa_kernel(tc, h1, w_hid2, b_hid2, w_out, b_out, norm_roo
                                  accum_out=r0_sums[:, sig:sig + 1])
         d2_total = keep.tile([P, 2], F32)
         nc.vector.tensor_reduce(out=d2_total[:], in_=d2_sums[:], axis=AX.X, op=ALU.add)
-        tensor_tensor(out=sums[:, 0:2], in0=d2_total[:], in1=r0_sums[:], op=ALU.subtract)
-        sums_t = ps_spec.tile([P, P], F32, tag="spec")
-        nc.tensor.transpose(sums_t[:], sums[:], ident[:])
+        tensor_tensor(out=shares[0][:, 0:2], in0=d2_total[:], in1=r0_sums[:], op=ALU.subtract)
+        shares_t = ps_spec.tile([P, P], F32, tag="spec")
+        for at in range(2):
+            nc.tensor.matmul(out=shares_t[:], lhsT=shares[at][:], rhs=ident[:], is_transpose=True, start=at == 0, stop=at == 1)
         err = keep.tile([P, 1], F32)
-        nc.vector.tensor_reduce(out=err[:], in_=sums_t[:], axis=AX.X, op=ALU.add)
+        nc.vector.tensor_reduce(out=err[:], in_=shares_t[:], axis=AX.X, op=ALU.add)
         nc.sync.dma_start(out=out_1.rearrange("(a b) -> a b", a=1), in_=err[0:1, 0:1])
         nc.sync.dma_start(out=out_3.rearrange("(a b) -> a b", a=1), in_=err[1:2, 0:1])

@@ -205,10 +205,14 @@ def tile_qdtssolveronnx_pa_kernel(tc, h1, w_hid2, b_hid2, w_out, b_out, norm_roo
             nc.gpsimd.tensor_copy(out=twist[quarter, :, 0:4 - a], in_=parts[quarter, :, a:4])
             if a > 0:
                 nc.gpsimd.tensor_copy(out=twist[quarter, :, 4 - a:4], in_=parts[quarter, :, 0:a])
-        ident_twice = keep.tile([P, 2 * P], F32)
+        ident_twice = fft.tile([P, 2 * P], F32, tag="diag")
         for c in range(2):
             nc.gpsimd.tensor_copy(out=ident_twice[:, P * c:P * (c + 1)], in_=ident[:])
-        turns = [ident_twice[:, P - L * w:2 * P - L * w] for w in range(4)]
+        turn_matrices = keep.tile([P, 4, P], F32)
+        for w in range(4):
+            nc.gpsimd.tensor_copy(out=turn_matrices[:, w, :].rearrange("p (r n e) -> p r n e", r=2, e=2),
+                                  in_=ident_twice[:, P - L * w:2 * P - L * w].rearrange("p (r e n) -> p r n e", r=2, e=2))
+        turns = [turn_matrices[:, w, :] for w in range(4)]
 
         x_matrix = keep.tile([P, 2 * G], F32)
         t_matrix = keep.tile([P, 2 * G], F32)
@@ -221,8 +225,11 @@ def tile_qdtssolveronnx_pa_kernel(tc, h1, w_hid2, b_hid2, w_out, b_out, norm_roo
             p_float = keep.tile([P, 2], F32)
             nc.vector.tensor_copy(out=p_float[:], in_=p_index[:])
             freq = keep.tile([P, 2, G], I32)
-            nc.gpsimd.iota(freq[:], pattern=[[4, 2], [8, 2], [16, L]], base=1, channel_multiplier=0)
-            last_freq = 4 * (N - 1) + 1
+            for hf in range(2):
+                nc.gpsimd.iota(freq[:, hf, 0:L], pattern=[[16, L // 2], [8, 2]], base=4 * hf + 1, channel_multiplier=0)
+                nc.gpsimd.iota(freq[:, hf, L:G], pattern=[[-16, L // 2], [8, 2]], base=16 * L + 4 * hf + 1, channel_multiplier=0)
+                nc.gpsimd.iota(freq[:, hf, L:L + 2], pattern=[[8, 2]], base=8 * L + 4 * hf + 1, channel_multiplier=0)
+            last_freq = 16 * (L - L // 2 + 1) + 8 + 4 + 1
             phase = fft.tile([P, 6 * G], I32, tag="diag")
             nc.gpsimd.iota(phase[:, 4 * G:4 * G + N], pattern=[[-last_freq, N]], base=LAGS * last_freq + COS, channel_multiplier=0)
             nc.vector.tensor_scalar(out=phase[:, 0:G], in0=freq[:, 0, :], scalar1=p_float[:, 0:1], scalar2=float(COS),
@@ -256,8 +263,8 @@ def tile_qdtssolveronnx_pa_kernel(tc, h1, w_hid2, b_hid2, w_out, b_out, norm_roo
         def inputs(i):
             b, tb, sub = place(i)
             if b not in v:
-                v[b] = batch_pool.tile([P, L, 2, 2, 3 * tb], F32, name="v_new")
-            v_view = v[b][:].rearrange("p n r e (s t) -> p n r e s t", s=3)
+                v[b] = batch_pool.tile([P, 2, 2 * L, 3 * tb], F32, name="v_new")
+            v_view = v[b][:].rearrange("p r x (h t) -> p r x h t", h=3)
             cols = (x_cols[i], xc_cols[i])
             for s, (sig, hf) in enumerate(FAST):
                 twisted = []
@@ -274,8 +281,7 @@ def tile_qdtssolveronnx_pa_kernel(tc, h1, w_hid2, b_hid2, w_out, b_out, norm_roo
                     for w in range(4):
                         nc.tensor.matmul(out=v_rows[:, t, :], lhsT=twisted[w][:, t, :], rhs=turns[w], is_transpose=True,
                                          start=w == 0, stop=w == 3)
-                nc.scalar.copy(out=v_view[:, :, :, :, s, sub].rearrange("p n r e t -> p (r e) n t"),
-                               in_=v_rows[:].rearrange("p t (k n) -> p k n t", n=L))
+                nc.scalar.copy(out=v_view[:, :, :, s, sub], in_=v_rows[:].rearrange("p t (r x) -> p r x t", r=2))
 
         def matrices(i):
             sq[i] = sq_pool.tile([P, BLK, 2, 2, 2, G], F32, name="sq_new")
@@ -311,87 +317,92 @@ def tile_qdtssolveronnx_pa_kernel(tc, h1, w_hid2, b_hid2, w_out, b_out, norm_roo
                     nc.scalar.activation(out=x_squares[:], in_=x_rows[i][:, sig, t, :], func=AF.Square,
                                          accum_out=r0[:, sig, BLK * i + t:BLK * i + t + 1])
 
-        def turned_sums(out, k1, k2, x, y):
-            sums = out[:, :, 2 * k1:2 * k2 + 2:2 * (k2 - k1) + 1, :]
-            diffs = out[:, :, 2 * k1 + 1:2 * k2 + 1:2 * (k2 - k1) - 1, :]
-            tensor_tensor(out=sums, in0=x, in1=y[:, :, ::-1, :], op=ALU.add)
-            tensor_tensor(out=diffs, in0=x[:, :, ::-1, :], in1=y, op=ALU.subtract)
+        def turned(out, x, y):
+            tensor_tensor(out=out[:, :, 0:2, :], in0=x, in1=y[:, :, ::-1, :], op=ALU.add)
+            tensor_tensor(out=out[:, :, 2:4, :], in0=x[:, :, ::-1, :], in1=y, op=ALU.subtract)
 
-        def join(a, b, out, n, q, groups, order):
-            a_k, b_k, out_k = (ap.rearrange("p g (k r) q -> p g k (r q)", r=2) for ap in (a, b, out))
-
-            def turned(k):
+        def join(a, b, n, fours, order, put):
+            def slanted(k):
                 t = math.sin(math.pi * k / n) / math.cos(math.pi * k / n)
-                d = fft.tile([P, groups, 4, q], F32, name="d", tag="d", bufs=4)
-                for g in range(groups):
-                    outer = b[:, g, 2 * k:2 * (n - k) + 2:2 * (n - 2 * k) + 1, :]
-                    inner = b[:, g, 2 * k + 1:2 * (n - k) + 1:2 * (n - 2 * k) - 1, :]
-                    mul_add(out=d[:, g, 0:4:3, :], in0=inner, scalar=t, in1=outer, op0=ALU.mult, op1=ALU.add)
-                    mul_add(out=d[:, g, 1:3, :], in0=outer, scalar=-t, in1=inner, op0=ALU.mult, op1=ALU.add)
+                d = fft.tile([P, a.shape[1], 4, a.shape[3]], F32, name="d", tag="d", bufs=4)
+                first, second = b[:, :, fours[k]:fours[k] + 2, :], b[:, :, fours[k] + 2:fours[k] + 4, :]
+                mul_add(out=d[:, :, 0:2, :], in0=second, scalar=t, in1=first, op0=ALU.mult, op1=ALU.add)
+                mul_add(out=d[:, :, 2:4, :], in0=first, scalar=-t, in1=second, op0=ALU.mult, op1=ALU.add)
                 return d
 
             def joined(k, d):
                 c = math.cos(math.pi * k / n)
-                for g in range(groups):
-                    d_pair = d[:, g, :, :].rearrange("p (k r) q -> p k (r q)", r=2)
-                    a_pair = a_k[:, g, k:n - k + 1:n - 2 * k, :]
-                    mul_add(out=out_k[:, g, k:2 * n - k + 1:2 * (n - k), :], in0=d_pair, scalar=c, in1=a_pair, op0=ALU.mult, op1=ALU.add)
-                    mul_add(out=out_k[:, g, n - k:n + k + 1:2 * k, :], in0=d_pair[:, ::-1, :], scalar=-c, in1=a_pair[:, ::-1, :],
+                for at, factor in ((k, c), (n + k, -c)):
+                    out, step = put(at)
+                    mul_add(out=out, in0=d[:, :, ::step, :], scalar=factor, in1=a[:, :, fours[k]:fours[k] + 4, :][:, :, ::step, :],
                             op0=ALU.mult, op1=ALU.add)
 
-            half = n // 2
-            made = [turned(k) for k in order[0:2]]
-            tensor_tensor(out=out_k[:, :, 0, :], in0=a_k[:, :, 0, :], in1=b_k[:, :, 0, :], op=ALU.add)
-            tensor_tensor(out=out_k[:, :, n, :], in0=a_k[:, :, 0, :], in1=b_k[:, :, 0, :], op=ALU.subtract)
-            turned_sums(out, half, 3 * half, a[:, :, n:n + 2, :], b[:, :, n:n + 2, :])
+            made = [slanted(k) for k in order[0:2]]
+            out = put(0)[0]
+            tensor_tensor(out=out[0], in0=a[:, :, 0:2, :], in1=b[:, :, 0:2, :], op=ALU.add)
+            tensor_tensor(out=out[1], in0=a[:, :, 0:2, :], in1=b[:, :, 0:2, :], op=ALU.subtract)
+            turned(put(n // 2)[0], a[:, :, 2:4, :], b[:, :, 2:4, :])
             for at, k in enumerate(order):
                 if at + 2 < len(order):
-                    made.append(turned(order[at + 2]))
+                    made.append(slanted(order[at + 2]))
                 joined(k, made[at])
 
         def transforms(b):
-            q = 6 * BLK * BATCHES[b][1]
-            x = v[b][:].rearrange("p (m h) r e z -> p m (h r e z)", m=8)
-            fours = fft.tile([P, 2, 4, 4, 2, q], F32, tag="sixteenths")
-            add4, sub4 = fours[:, 0, :, :, :, :], fours[:, 1, :, :, :, :]
-            tensor_tensor(out=add4.rearrange("p m g r q -> p m (g r q)"), in0=x[:, 0:4, :], in1=x[:, 4:8, :], op=ALU.add)
-            tensor_tensor(out=sub4.rearrange("p m g r q -> p m (g r q)"), in0=x[:, 0:4, :], in1=x[:, 4:8, :], op=ALU.subtract)
-            flat = "p m g r q -> p m (g r q)"
-            add2 = fft.tile([P, 2, 4, 2, q], F32, tag="add2")
-            sub2 = fft.tile([P, 2, 4, 2, q], F32, tag="sub2")
-            diag = fft.tile([P, 2, 4, 2, q], F32, tag="diag")
-            eighths = fft.tile([P, 4, 16, q], F32, tag="mid", bufs=2)
-            tensor_tensor(out=add2[:].rearrange(flat), in0=add4[:, 0:2, :, :, :].rearrange(flat), in1=add4[:, 2:4, :, :, :].rearrange(flat), op=ALU.add)
-            tensor_tensor(out=diag[:, :, :, 0, :], in0=sub4[:, 1:4:2, :, 0, :], in1=sub4[:, 1:4:2, :, 1, :], op=ALU.add)
-            tensor_tensor(out=sub2[:].rearrange(flat), in0=add4[:, 0:2, :, :, :].rearrange(flat), in1=add4[:, 2:4, :, :, :].rearrange(flat), op=ALU.subtract)
-            tensor_tensor(out=diag[:, :, :, 1, :], in0=sub4[:, 1:4:2, :, 1, :], in1=sub4[:, 1:4:2, :, 0, :], op=ALU.subtract)
-            tensor_tensor(out=eighths[:, :, 0:2, :], in0=add2[:, 0, :, :, :], in1=add2[:, 1, :, :, :], op=ALU.add)
-            tensor_tensor(out=eighths[:, :, 8:10, :], in0=add2[:, 0, :, :, :], in1=add2[:, 1, :, :, :], op=ALU.subtract)
-            straight = fft.tile([P, 4, 4, q], F32, tag="straight")
-            turned_sums(straight[:], 0, 1, sub4[:, 0, :, :, :], sub4[:, 2, :, :, :])
-            slanted = fft.tile([P, 4, 4, q], F32, tag="add2")
-            turned_sums(slanted[:], 0, 1, diag[:, 0, :, :, :], diag[:, 1, :, :, :])
-            turned_sums(eighths[:], 2, 6, sub2[:, 0, :, :, :], sub2[:, 1, :, :, :])
-            mul_add(out=eighths[:, :, 2:4, :], in0=slanted[:, :, 0:2, :], scalar=RHO, in1=straight[:, :, 0:2, :], op0=ALU.mult, op1=ALU.add)
-            mul_add(out=eighths[:, :, 10:12, :], in0=slanted[:, :, 0:2, :], scalar=-RHO, in1=straight[:, :, 0:2, :], op0=ALU.mult, op1=ALU.add)
-            for k, sign in ((3, 1.0), (7, -1.0)):
-                mul_add(out=eighths[:, :, 2 * k, :], in0=slanted[:, :, 3, :], scalar=sign * RHO, in1=straight[:, :, 2, :], op0=ALU.mult, op1=ALU.add)
-                mul_add(out=eighths[:, :, 2 * k + 1, :], in0=slanted[:, :, 2, :], scalar=-sign * RHO, in1=straight[:, :, 3, :], op0=ALU.mult, op1=ALU.add)
-            sixteenths = fft.tile([P, 2, L, q], F32, tag="sixteenths")
-            join(eighths[:, 0:2, :, :], eighths[:, 2:4, :, :], sixteenths[:], 8, q, 2, (2, 1, 3))
-            spectrum[b] = fft.tile([P, 1, 2 * L, q], F32, name="spectrum_new", tag="mid", bufs=2)
-            join(sixteenths[:, 0:1, :, :], sixteenths[:, 1:2, :, :], spectrum[b][:], 16, q, 1, (4, 2, 6, 1, 7, 3, 5))
+            z = 6 * BLK * BATCHES[b][1]
+            x = v[b][:].rearrange("p r (m g e) z -> p r m g (e z)", m=8, e=2)
+            halved = fft.tile([P, 2, 4, 8, z], F32, tag="sixteenths")
+            add4, sub4 = halved[:, 0, :, :, :], halved[:, 1, :, :, :]
+            for out, op in ((add4, ALU.add), (sub4, ALU.subtract)):
+                tensor_tensor(out=out.rearrange("p g (r m) z -> p r m g z", r=2), in0=x[:, :, 0:4, :, :], in1=x[:, :, 4:8, :, :], op=op)
+            add2 = fft.tile([P, 4, 4, z], F32, tag="add2")
+            sub2 = fft.tile([P, 4, 4, z], F32, tag="sub2")
+            diag = fft.tile([P, 4, 4, z], F32, tag="diag")
+            straight = fft.tile([P, 4, 4, z], F32, tag="straight")
+            eighths = fft.tile([P, 4, 16, z], F32, tag="mid", bufs=2)
+            pairs = add4.rearrange("p g (r m) z -> p (g r) m z", r=2)
+            tensor_tensor(out=add2[:].rearrange("p g (r m) z -> p (g r) m z", r=2), in0=pairs[:, :, 0:2, :], in1=pairs[:, :, 2:4, :], op=ALU.add)
+            tensor_tensor(out=diag[:, :, 0:2, :], in0=sub4[:, :, 1:4:2, :], in1=sub4[:, :, 5:8:2, :], op=ALU.add)
+            tensor_tensor(out=sub2[:].rearrange("p g (r m) z -> p (g r) m z", r=2), in0=pairs[:, :, 0:2, :], in1=pairs[:, :, 2:4, :], op=ALU.subtract)
+            tensor_tensor(out=diag[:, :, 2:4, :], in0=sub4[:, :, 5:2:-2, :], in1=sub4[:, :, 1:8:6, :], op=ALU.subtract)
+            tensor_tensor(out=eighths[:, :, 0:2, :], in0=add2[:, :, 0:4:2, :], in1=add2[:, :, 1:4:2, :], op=ALU.add)
+            tensor_tensor(out=eighths[:, :, 2:4, :], in0=add2[:, :, 0:4:2, :], in1=add2[:, :, 1:4:2, :], op=ALU.subtract)
+            turned(straight[:], sub4[:, :, 0:8:4, :], sub4[:, :, 2:8:4, :])
+            slant = fft.tile([P, 4, 4, z], F32, tag="add2")
+            tensor_tensor(out=slant[:, :, 0:4:2, :], in0=diag[:, :, 0:4:2, :], in1=diag[:, :, 3::-2, :], op=ALU.subtract)
+            tensor_tensor(out=slant[:, :, 1:4:2, :], in0=diag[:, :, 0:4:2, :], in1=diag[:, :, 3::-2, :], op=ALU.add)
+            turned(eighths[:, :, 4:8, :], sub2[:, :, 0:4:2, :], sub2[:, :, 1:4:2, :])
+            for at, sign in ((8, 1.0), (12, -1.0)):
+                mul_add(out=eighths[:, :, at:at + 3, :], in0=slant[:, :, 0:3, :], scalar=sign * RHO, in1=straight[:, :, 0:3, :], op0=ALU.mult, op1=ALU.add)
+                mul_add(out=eighths[:, :, at + 3, :], in0=slant[:, :, 3, :], scalar=-sign * RHO, in1=straight[:, :, 3, :], op0=ALU.mult, op1=ALU.add)
+            sixteenths = fft.tile([P, 2, L, z], F32, tag="sixteenths")
+            fours = {4: 4, 2: 8, 10: 12, 1: 16, 9: 20, 5: 24, 13: 28}
+
+            def into_sixteenths(k):
+                if k == 0:
+                    return (sixteenths[:, :, 0:2, :], sixteenths[:, :, 2:4, :]), 1
+                return sixteenths[:, :, fours[k]:fours[k] + 4, :], 1
+
+            join(eighths[:, 0:2, :, :], eighths[:, 2:4, :, :], 8, {2: 4, 1: 8, 5: 12}, (2, 1, 5), into_sixteenths)
+            planes = fft.tile([P, 1, 4, L // 2, z], F32, name="planes", tag="mid", bufs=2)
+            spectrum[b] = planes
+
+            def into_planes(k):
+                if k == 0:
+                    return (planes[:, :, 0:4:2, 0, :], planes[:, :, 1:4:2, 0, :]), 1
+                return (planes[:, :, :, k, :], 1) if k < L // 2 else (planes[:, :, :, L - k, :], -1)
+
+            join(sixteenths[:, 0:1, :, :], sixteenths[:, 1:2, :, :], 16, fours, (4, 2, 10, 1, 9, 5, 13), into_planes)
 
         def compare(i):
             b, tb, sub = place(i)
-            view = spectrum[b][:, 0, :, :].rearrange("p (k r) (e s t) -> p r e k s t", r=2, e=2, s=3)
+            view = spectrum[b][:, 0, :, :, :].rearrange("p c k (e s t) -> p s (c k e) t", e=2, s=3)
             for s, (sig, hf) in enumerate(FAST):
-                for r in range(2):
-                    squares, part = sq[i][:, :, r, sig, hf, :].rearrange("p t (e k) -> p e k t", e=2), view[:, r, :, :, s, sub]
-                    if r == 1 and i == NBLK - 1:
-                        tensor_tensor(out=squares, in0=part, in1=part, op=ALU.mult)
-                    else:
-                        nc.scalar.activation(out=squares, in_=part, func=AF.Square)
+                squares = sq[i][:, :, :, sig, hf, :].rearrange("p t r x -> p r x t")
+                part = view[:, s, :, sub].rearrange("p (r x) t -> p r x t", r=2)
+                if i == NBLK - 1 and s == 1:
+                    tensor_tensor(out=squares, in0=part, in1=part, op=ALU.mult)
+                else:
+                    nc.scalar.activation(out=squares, in_=part, func=AF.Square)
             for sig in range(2):
                 diff = ps_spec.tile([P, BLK, P], F32, tag="spec", name="diff")
                 for t in range(BLK):

@@ -278,37 +278,65 @@ def tile_qdtssolveronnx_pa_kernel(tc, h1, w_hid2, b_hid2, w_out, b_out, norm_roo
                     twisted.append(z_cols)
                 v_rows = ps_spec.tile([P, BLK, P], F32, tag="spec", name="v_rows")
                 for t in range(BLK):
+                    if t == 2 and plain_pairs:
+                        next_pair()
                     for w in range(4):
                         nc.tensor.matmul(out=v_rows[:, t, :], lhsT=twisted[w][:, t, :], rhs=turns[w], is_transpose=True,
                                          start=w == 0, stop=w == 3)
                 nc.scalar.copy(out=v_view[:, :, :, s, sub], in_=v_rows[:].rearrange("p t (r x) -> p r x t", r=2))
 
+        plain_pairs = []
+
+        def next_pair():
+            pair = plain_pairs[0]
+            plain_pairs[:] = plain_pairs[1:]
+            pair()
+
         def matrices(i):
-            sq[i] = sq_pool.tile([P, BLK, 2, 2, 2, G], F32, name="sq_new")
-            spec0 = ps_spec.tile([P, BLK, P], F32, tag="spec")
-            for t in range(BLK):
-                nc.tensor.matmul(out=spec0[:, t, :], lhsT=x_cols[i][:, t, :], rhs=x_matrix[:], start=True, stop=True)
-            nc.scalar.activation(out=sq[i][:, :, :, 0, 0, :], in_=spec0[:].rearrange("p t (r g) -> p t r g", r=2), func=AF.Square)
+            held = []
+
+            def pair(first):
+                if first == 0:
+                    sq[i] = sq_pool.tile([P, BLK, 2, 2, 2, G], F32, name="sq_new")
+                    held.append(ps_spec.tile([P, BLK, P], F32, tag="spec", name="spec0"))
+                for t in range(first, first + 2):
+                    nc.tensor.matmul(out=held[0][:, t, :], lhsT=x_cols[i][:, t, :], rhs=x_matrix[:], start=True, stop=True)
+                if first == 2:
+                    nc.scalar.activation(out=sq[i][:, :, :, 0, 0, :], in_=held[0][:].rearrange("p t (r g) -> p t r g", r=2), func=AF.Square)
+
+            plain_pairs.extend([lambda: pair(0), lambda: pair(2)])
 
         def targets(i):
-            th[i] = th_pool.tile([P, BLK, 2 * G], F32, name="th_new")
-            t_t = ps_t.tile([P, BLK, P], BF16, tag="t")
-            for t in range(BLK):
-                nc.tensor.transpose(t_t[:, t, :], t_pad[:, BLK * i + t, :], ident_bf[:])
-            t_cols = stage.tile([P, BLK, P], F32)
-            nc.scalar.copy(out=t_cols[:], in_=t_t[:])
-            th_acc = ps_t.tile([P, BLK, P], F32, tag="t")
-            for t in range(BLK):
-                if BLK * i + t == TILES - 1:
-                    nc.tensor.transpose(th_acc[:, t, :], t_cols[:, t, :], ident[:])
-                    nc.tensor.matmul(out=th_acc[:, t, 0:P - 1], lhsT=t_cols[:, t, :], rhs=t_matrix[:, 0:P - 1], start=True, stop=True)
-                else:
-                    nc.tensor.matmul(out=th_acc[:, t, :], lhsT=t_cols[:, t, :], rhs=t_matrix[:], start=True, stop=True)
-            nc.scalar.copy(out=th[i][:], in_=th_acc[:])
-            if i == NBLK - 1:
-                products = stage.tile([P, N], F32)
-                tensor_tensor(out=products[:], in0=t_pad[:, TILES - 1, :], in1=last_col[:], op=ALU.mult)
-                nc.vector.tensor_reduce(out=th[i][:, BLK - 1, N - 1:N], in_=products[:], axis=AX.X, op=ALU.add)
+            held = []
+
+            def turn():
+                t_t = ps_t.tile([P, BLK, P], BF16, tag="t")
+                for t in range(BLK):
+                    nc.tensor.transpose(t_t[:, t, :], t_pad[:, BLK * i + t, :], ident_bf[:])
+                t_cols = stage.tile([P, BLK, P], F32)
+                nc.scalar.copy(out=t_cols[:], in_=t_t[:])
+                held.append(t_cols)
+
+            def pair(first):
+                if first == 0:
+                    th[i] = th_pool.tile([P, BLK, 2 * G], F32, name="th_new")
+                    held.append(ps_t.tile([P, BLK, P], F32, tag="t", name="th_acc"))
+                t_cols, th_acc = held
+                for t in range(first, first + 2):
+                    if BLK * i + t == TILES - 1:
+                        nc.tensor.transpose(th_acc[:, t, :], t_cols[:, t, :], ident[:])
+                        nc.tensor.matmul(out=th_acc[:, t, 0:P - 1], lhsT=t_cols[:, t, :], rhs=t_matrix[:, 0:P - 1], start=True, stop=True)
+                    else:
+                        nc.tensor.matmul(out=th_acc[:, t, :], lhsT=t_cols[:, t, :], rhs=t_matrix[:], start=True, stop=True)
+                if first == 2:
+                    nc.scalar.copy(out=th[i][:], in_=th_acc[:])
+                    if i == NBLK - 1:
+                        products = stage.tile([P, N], F32)
+                        tensor_tensor(out=products[:], in0=t_pad[:, TILES - 1, :], in1=last_col[:], op=ALU.mult)
+                        nc.vector.tensor_reduce(out=th[i][:, BLK - 1, N - 1:N], in_=products[:], axis=AX.X, op=ALU.add)
+
+            turn()
+            plain_pairs.extend([lambda: pair(0), lambda: pair(2)])
 
         def lag_zero(i):
             for sig in range(2):
@@ -419,6 +447,9 @@ def tile_qdtssolveronnx_pa_kernel(tc, h1, w_hid2, b_hid2, w_out, b_out, norm_roo
 
         last = len(BATCHES) - 1
         for b in range(last + 3):
+            for i in blocks_of(b - 1) if b <= last else range(0):
+                matrices(i)
+                targets(i)
             for i in blocks_of(b):
                 if i > 0:
                     first_layer(i)
@@ -428,16 +459,15 @@ def tile_qdtssolveronnx_pa_kernel(tc, h1, w_hid2, b_hid2, w_out, b_out, norm_roo
                 matrix_tables()
             for i in blocks_of(b - 2):
                 compare(i)
-            if b == last:
-                for i in blocks_of(b):
-                    matrices(i)
-                    lag_zero(i)
+            for i in blocks_of(b) if b == last else range(0):
+                matrices(i)
+                targets(i)
+                lag_zero(i)
             if b <= last:
                 for i in blocks_of(b - 1):
-                    matrices(i)
                     lag_zero(i)
-            for i in blocks_of(b - 1):
-                targets(i)
+            while plain_pairs:
+                next_pair()
             if 0 < b < last + 2:
                 transforms(b - 1)
 

@@ -49,20 +49,22 @@ def tile_qdtssolveronnx_pa_kernel(tc, h1, w_hid2, b_hid2, w_out, b_out, norm_roo
         th_pool = ctx.enter_context(tc.tile_pool(name="th_pool", bufs=6))
         batch_pool = ctx.enter_context(tc.tile_pool(name="batch_pool", bufs=2))
         fft = ctx.enter_context(tc.tile_pool(name="fft", bufs=1))
-        ps_in = ctx.enter_context(tc.psum_pool(name="ps_in", bufs=1))
-        ps_h2 = ctx.enter_context(tc.psum_pool(name="ps_h2", bufs=2))
+        ps_h2 = ctx.enter_context(tc.psum_pool(name="ps_h2", bufs=3))
         ps_x = ctx.enter_context(tc.psum_pool(name="ps_x", bufs=1))
         ps_spec = ctx.enter_context(tc.psum_pool(name="ps_spec", bufs=3))
         ps_t = ctx.enter_context(tc.psum_pool(name="ps_t", bufs=1))
 
         w1_sb = h1_pool.tile([P, BLK, H], BF16, name="w1_sb", tag="h1_sb")
-        nc.sync.dma_start(out=w1_sb[:], in_=w_hid2.rearrange("(p c) k -> p c k", c=4))
+        w1_rows = w_hid2.rearrange("(p c) k -> p c k", c=4)
+        for a in range(2):
+            nc.sync.dma_start(out=w1_sb[:, 2 * a:2 * a + 2, :], in_=w1_rows[:, 2 * a:2 * a + 2, :])
         h1_rows = h1.rearrange("(i p t) k -> i p t k", p=P, t=BLK)
         h1_tiles = {}
 
         def load_h1(i):
             h1_sb = h1_pool.tile([P, BLK, H], BF16, name="h1_sb")
-            nc.sync.dma_start(out=h1_sb[:], in_=h1_rows[i])
+            for half in ((slice(0, 2), slice(2, 4)) if i == 0 else (slice(0, 4),)):
+                nc.sync.dma_start(out=h1_sb[:, half, :], in_=h1_rows[i][:, half, :])
             h1_tiles[i] = h1_sb
 
         b1 = keep.tile([P, 4], BF16)
@@ -116,63 +118,88 @@ def tile_qdtssolveronnx_pa_kernel(tc, h1, w_hid2, b_hid2, w_out, b_out, norm_roo
         xc_cols = {}
         h2_grouped = {}
 
-        def first_layer(i):
-            shared = i < SHARED
-            if i + 2 < NBLK:
-                load_h1(i + 2)
-            h1_words = h1_tiles[i][:].bitcast(F32)
-            h1_grouped = stage.tile([P, BLK * P, 4], BF16, align_bytes=64)
-            h1_grouped32 = h1_grouped[:].bitcast(F32)
-            for a in range(2):
-                h1_t = ps_in.tile([P, 2, 2, P], F32, tag="in")
-                for u in range(2):
-                    for t in range(2):
-                        nc.tensor.transpose(h1_t[:, u, t, :], h1_words[:, 2 * a + t, u:2 * P:2], ident[:])
-                copy = nc.vector.tensor_copy if shared and a == 0 else nc.scalar.copy
-                copy(out=h1_grouped32[:, 2 * P * a:2 * P * (a + 1), :], in_=h1_t[:].rearrange("q u t p -> q (t p) u"))
-            h1_codes = stage.tile([P, BLK * P], U32, align_bytes=64)
-            h1_scales = stage.tile([P, BLK * P], U8, align_bytes=64)
-            nc.vector.quantize_mx(out=h1_codes[:].bitcast(FP8X4), scales=h1_scales[:], in_=h1_grouped[:].rearrange("q n f -> q (n f)"))
-            h2_planes = stage.tile([P, 4, BLK * P], BF16)
-            for c in range(4):
-                h2_acc = ps_h2.tile([P, BLK * P], F32, tag="h2")
-                nc.tensor.matmul_mx(out=h2_acc[:], lhsT=w1_codes[:, P * c:P * (c + 1)].bitcast(FP8X4),
-                                    lhsT_scale=w1_scales[:, P * c:P * (c + 1)],
-                                    rhs=h1_codes[:].bitcast(FP8X4), rhs_scale=h1_scales[:], start=True, stop=True)
-                if shared and c % 2 == 1:
-                    nc.vector.tensor_scalar(out=h2_planes[:, c, :], in0=h2_acc[:], scalar1=b1[:, c:c + 1], scalar2=0.0,
-                                            op0=ALU.add, op1=ALU.max)
-                else:
-                    nc.scalar.activation(out=h2_planes[:, c, :], in_=h2_acc[:], func=AF.Relu, bias=b1[:, c:c + 1], scale=1.0)
-            h2_grouped[i] = stage.tile([P, BLK * P, 4], BF16, name="h2_grouped_new", align_bytes=64)
-            nc.vector.tensor_copy(out=h2_grouped[i][:].rearrange("m (a i) c -> m a c i", i=4),
-                                  in_=h2_planes[:].rearrange("m c (a i) -> m a c i", i=4))
+        h1_grouped = {}
+        h1_codes = {}
+        h2_planes = {}
+        h2_codes = {}
+        held = {}
 
-        def second_layer(i):
-            h2_codes = stage.tile([P, BLK * P], U32, align_bytes=64)
-            h2_scales = stage.tile([P, BLK * P], U8, align_bytes=64)
-            nc.vector.quantize_mx(out=h2_codes[:].bitcast(FP8X4), scales=h2_scales[:], in_=h2_grouped[i][:].rearrange("m n f -> m (n f)"))
+        def turn_h1(i, a):
+            h1_words = h1_tiles[i][:].bitcast(F32)
+            if a == 0:
+                h1_grouped[i] = stage.tile([P, BLK * P, 4], BF16, name="h1_grouped_new", tag="h1_grouped", align_bytes=64)
+            h1_t = ps_h2.tile([P, 2, 2, P], F32, tag="h2")
+            for u in range(2):
+                for t in range(2):
+                    nc.tensor.transpose(h1_t[:, u, t, :], h1_words[:, 2 * a + t, u:2 * P:2], ident[:])
+            held["h1", i, a] = h1_t
+
+        def group_h1(i, a):
+            copy = nc.vector.tensor_copy if i < SHARED and a == 0 else nc.scalar.copy
+            copy(out=h1_grouped[i][:].bitcast(F32)[:, 2 * P * a:2 * P * (a + 1), :], in_=held["h1", i, a][:].rearrange("q u t p -> q (t p) u"))
+
+        def quantize_h1(i):
+            codes = stage.tile([P, BLK * P], U32, name="h1_codes_new", align_bytes=64)
+            scales = stage.tile([P, BLK * P], U8, name="h1_scales_new", align_bytes=64)
+            nc.vector.quantize_mx(out=codes[:].bitcast(FP8X4), scales=scales[:], in_=h1_grouped[i][:].rearrange("q n f -> q (n f)"))
+            h1_codes[i] = codes, scales
+
+        def hidden(i, c):
+            codes, scales = h1_codes[i]
+            h2_acc = ps_h2.tile([P, BLK * P], F32, tag="h2")
+            nc.tensor.matmul_mx(out=h2_acc[:], lhsT=w1_codes[:, P * c:P * (c + 1)].bitcast(FP8X4), lhsT_scale=w1_scales[:, P * c:P * (c + 1)],
+                                rhs=codes[:].bitcast(FP8X4), rhs_scale=scales[:], start=True, stop=True)
+            held["h2", i, c] = h2_acc
+
+        def relu(i, c):
+            if c == 0:
+                h2_planes[i] = stage.tile([P, 4, BLK * P], BF16, name="h2_planes_new")
+            h2_acc = held["h2", i, c]
+            if i < SHARED and c % 2 == 1:
+                nc.vector.tensor_scalar(out=h2_planes[i][:, c, :], in0=h2_acc[:], scalar1=b1[:, c:c + 1], scalar2=0.0, op0=ALU.add, op1=ALU.max)
+            else:
+                nc.scalar.activation(out=h2_planes[i][:, c, :], in_=h2_acc[:], func=AF.Relu, bias=b1[:, c:c + 1], scale=1.0)
+
+        def group_h2(i):
+            h2_grouped[i] = stage.tile([P, BLK * P, 4], BF16, name="h2_grouped_new", align_bytes=64)
+            nc.vector.tensor_copy(out=h2_grouped[i][:].rearrange("m (a i) c -> m a c i", i=4), in_=h2_planes[i][:].rearrange("m c (a i) -> m a c i", i=4))
+
+        def quantize_h2(i):
+            codes = stage.tile([P, BLK * P], U32, name="h2_codes_new", align_bytes=64)
+            scales = stage.tile([P, BLK * P], U8, name="h2_scales_new", align_bytes=64)
+            nc.vector.quantize_mx(out=codes[:].bitcast(FP8X4), scales=scales[:], in_=h2_grouped[i][:].rearrange("m n f -> m (n f)"))
+            h2_codes[i] = codes, scales
+
+        def product(i):
+            codes, scales = h2_codes[i]
             y_acc = ps_x.tile([P, BLK * P], F32, tag="x")
             nc.tensor.matmul_mx(out=y_acc[:], lhsT=w2_codes[:].bitcast(FP8X4), lhsT_scale=w2_scales[:],
-                                rhs=h2_codes[:].bitcast(FP8X4), rhs_scale=h2_scales[:], start=True, stop=True)
+                                rhs=codes[:].bitcast(FP8X4), rhs_scale=scales[:], start=True, stop=True)
+            held["y", i] = y_acc
+
+        def columns(i):
             x_cols[i] = x_pool.tile([P, BLK, P], F32, name="x_cols_new")
-            xc_cols[i] = stage.tile([P, BLK, P], F32, name="xc_cols_new")
-            mul_add(out=x_cols[i][:], in0=y_acc[:].rearrange("j (t p) -> j t p", t=BLK), scalar=b2[:, 0:1],
+            mul_add(out=x_cols[i][:], in0=held["y", i][:].rearrange("j (t p) -> j t p", t=BLK), scalar=b2[:, 0:1],
                     in1=nr_all[:, BLK * P * i:BLK * P * (i + 1)].rearrange("j (p t) -> j t p", t=BLK), op0=ALU.add, op1=ALU.mult)
+
+        def clip_columns(i):
+            xc_cols[i] = stage.tile([P, BLK, P], F32, name="xc_cols_new")
             nc.vector.tensor_scalar(out=xc_cols[i][:], in0=x_cols[i][:], scalar1=-2.0, scalar2=2.0, op0=ALU.max, op1=ALU.min)
+
+        def turn_x(i):
             x_t = ps_x.tile([P, BLK, P], F32, tag="x")
             for t in range(BLK):
                 nc.tensor.transpose(x_t[:, t, :], x_cols[i][:, t, :], ident[:])
+            held["x", i] = x_t
+
+        def rows(i):
             x_rows[i] = x_pool.tile([P, 2, BLK, N], F32, name="x_rows_new")
-            nc.scalar.copy(out=x_rows[i][:, 0, :, :], in_=x_t[:])
-            nc.vector.tensor_scalar(out=x_rows[i][:, 1, :, :], in0=x_rows[i][:, 0, :, :], scalar1=-2.0, scalar2=2.0,
-                                    op0=ALU.max, op1=ALU.min)
+            nc.scalar.copy(out=x_rows[i][:, 0, :, :], in_=held["x", i][:])
+
+        def clip_rows(i):
+            nc.vector.tensor_scalar(out=x_rows[i][:, 1, :, :], in0=x_rows[i][:, 0, :, :], scalar1=-2.0, scalar2=2.0, op0=ALU.max, op1=ALU.min)
             for sig in range(2):
                 nc.sync.dma_start(out=x_out[sig][i], in_=x_rows[i][:, sig, :, :])
-
-        first_layer(0)
-        second_weights()
-        second_layer(0)
 
         t_pad = keep.tile([P, TILES, N], BF16)
         nc.gpsimd.memset(t_pad[:], 0.0)
@@ -260,30 +287,31 @@ def tile_qdtssolveronnx_pa_kernel(tc, h1, w_hid2, b_hid2, w_out, b_out, norm_roo
             at = BLK * (i - BATCHES[b][0])
             return b, BLK * BATCHES[b][1], slice(at, at + BLK)
 
-        def inputs(i):
+        def twist_copy(i, s, w):
+            sig, hf = FAST[s]
+            z_cols = z_pool.tile([P, BLK, P], F32, name="z_cols")
+            x, factor = (x_cols[i], xc_cols[i])[sig], twist[:, hf, w:w + 1]
+            if i < NBLK - 1 and w < (VECTOR_COPIES[s] if i > 0 else FIRST_COPIES):
+                nc.vector.tensor_scalar(out=z_cols[:], in0=x[:], scalar1=factor, scalar2=None, op0=ALU.mult)
+            else:
+                nc.scalar.activation(out=z_cols[:], in_=x[:], func=AF.Copy, scale=factor)
+            held["z", i, s, w] = z_cols
+
+        def fold(i, s):
+            v_rows = ps_spec.tile([P, BLK, P], F32, tag="spec", name="v_rows")
+            for t in range(BLK):
+                if t == 2 and plain_pairs:
+                    next_pair()
+                for w in range(4):
+                    nc.tensor.matmul(out=v_rows[:, t, :], lhsT=held["z", i, s, w][:, t, :], rhs=turns[w], is_transpose=True, start=w == 0, stop=w == 3)
+            held["v", i, s] = v_rows
+
+        def folded(i, s):
             b, tb, sub = place(i)
             if b not in v:
                 v[b] = batch_pool.tile([P, 2, 2 * L, 3 * tb], F32, name="v_new")
             v_view = v[b][:].rearrange("p r x (h t) -> p r x h t", h=3)
-            cols = (x_cols[i], xc_cols[i])
-            for s, (sig, hf) in enumerate(FAST):
-                twisted = []
-                for w in range(4):
-                    z_cols = z_pool.tile([P, BLK, P], F32, name="z_cols")
-                    factor = twist[:, hf, w:w + 1]
-                    if w < (VECTOR_COPIES[s] if i > 0 else FIRST_COPIES):
-                        nc.vector.tensor_scalar(out=z_cols[:], in0=cols[sig][:], scalar1=factor, scalar2=None, op0=ALU.mult)
-                    else:
-                        nc.scalar.activation(out=z_cols[:], in_=cols[sig][:], func=AF.Copy, scale=factor)
-                    twisted.append(z_cols)
-                v_rows = ps_spec.tile([P, BLK, P], F32, tag="spec", name="v_rows")
-                for t in range(BLK):
-                    if t == 2 and plain_pairs:
-                        next_pair()
-                    for w in range(4):
-                        nc.tensor.matmul(out=v_rows[:, t, :], lhsT=twisted[w][:, t, :], rhs=turns[w], is_transpose=True,
-                                         start=w == 0, stop=w == 3)
-                nc.scalar.copy(out=v_view[:, :, :, s, sub], in_=v_rows[:].rearrange("p t (r x) -> p r x t", r=2))
+            nc.scalar.copy(out=v_view[:, :, :, s, sub], in_=held["v", i, s][:].rearrange("p t (r x) -> p r x t", r=2))
 
         plain_pairs = []
 
@@ -332,18 +360,18 @@ def tile_qdtssolveronnx_pa_kernel(tc, h1, w_hid2, b_hid2, w_out, b_out, norm_roo
                     nc.scalar.copy(out=th[i][:], in_=th_acc[:])
                     if i == NBLK - 1:
                         products = stage.tile([P, N], F32)
-                        tensor_tensor(out=products[:], in0=t_pad[:, TILES - 1, :], in1=last_col[:], op=ALU.mult)
-                        nc.vector.tensor_reduce(out=th[i][:, BLK - 1, N - 1:N], in_=products[:], axis=AX.X, op=ALU.add)
+                        nc.gpsimd.tensor_tensor(out=products[:], in0=t_pad[:, TILES - 1, :], in1=last_col[:], op=ALU.mult)
+                        summed = stage.tile([P, N], F32)
+                        nc.scalar.activation(out=summed[:], in_=products[:], func=AF.Copy, accum_out=th[i][:, BLK - 1, N - 1:N])
 
             turn()
             plain_pairs.extend([lambda: pair(0), lambda: pair(2)])
 
-        def lag_zero(i):
-            for sig in range(2):
-                for t in range(BLK):
-                    x_squares = stage.tile([P, N], F32)
-                    nc.scalar.activation(out=x_squares[:], in_=x_rows[i][:, sig, t, :], func=AF.Square,
-                                         accum_out=r0[:, sig, BLK * i + t:BLK * i + t + 1])
+        def lag_zero(i, sig):
+            for t in range(BLK):
+                x_squares = stage.tile([P, N], F32)
+                nc.scalar.activation(out=x_squares[:], in_=x_rows[i][:, sig, t, :], func=AF.Square,
+                                     accum_out=r0[:, sig, BLK * i + t:BLK * i + t + 1])
 
         def turned(out, x, y):
             tensor_tensor(out=out[:, :, 0:2, :], in0=x, in1=y[:, :, ::-1, :], op=ALU.add)
@@ -421,53 +449,135 @@ def tile_qdtssolveronnx_pa_kernel(tc, h1, w_hid2, b_hid2, w_out, b_out, norm_roo
 
             join(sixteenths[:, 0:1, :, :], sixteenths[:, 1:2, :, :], 16, fours, (4, 2, 10, 1, 9, 5, 13), into_planes)
 
-        def compare(i):
+        def squares(i, s):
             b, tb, sub = place(i)
+            sig, hf = FAST[s]
             view = spectrum[b][:, 0, :, :, :].rearrange("p c k (e s t) -> p s (c k e) t", e=2, s=3)
-            for s, (sig, hf) in enumerate(FAST):
-                squares = sq[i][:, :, :, sig, hf, :].rearrange("p t r x -> p r x t")
-                part = view[:, s, :, sub].rearrange("p (r x) t -> p r x t", r=2)
-                if i == NBLK - 1 and s == 1:
-                    tensor_tensor(out=squares, in0=part, in1=part, op=ALU.mult)
-                else:
-                    nc.scalar.activation(out=squares, in_=part, func=AF.Square)
-            for sig in range(2):
-                diff = ps_spec.tile([P, BLK, P], F32, tag="spec", name="diff")
-                for t in range(BLK):
-                    for r in range(2):
-                        nc.tensor.matmul(out=diff[:, t, :], lhsT=sq[i][:, t, r, sig, :, :].rearrange("p f g -> p (f g)"), rhs=ident[:],
-                                         is_transpose=True, start=r == 0, stop=False)
-                    nc.tensor.matmul(out=diff[:, t, :], lhsT=th[i][:, t, :], rhs=ident[:], is_transpose=True, start=False, stop=True)
-                squared = stage.tile([P, BLK, P], F32)
-                into = d2_sums[:, sig, i:i + 1] if i < NBLK - 1 else shares[1][:, sig:sig + 1]
-                nc.scalar.activation(out=squared[:], in_=diff[:], func=AF.Square, scale=1.0 / math.sqrt(128.0 * MEAN), accum_out=into)
+            out = sq[i][:, :, :, sig, hf, :].rearrange("p t r x -> p r x t")
+            part = view[:, s, :, sub].rearrange("p (r x) t -> p r x t", r=2)
+            if i == NBLK - 1 and s == 1:
+                tensor_tensor(out=out, in0=part, in1=part, op=ALU.mult)
+            else:
+                nc.scalar.activation(out=out, in_=part, func=AF.Square)
+
+        def differences(i, sig):
+            diff = ps_spec.tile([P, BLK, P], F32, tag="spec", name="diff")
+            for t in range(BLK):
+                for r in range(2):
+                    nc.tensor.matmul(out=diff[:, t, :], lhsT=sq[i][:, t, r, sig, :, :].rearrange("p f g -> p (f g)"), rhs=ident[:],
+                                     is_transpose=True, start=r == 0, stop=False)
+                nc.tensor.matmul(out=diff[:, t, :], lhsT=th[i][:, t, :], rhs=ident[:], is_transpose=True, start=False, stop=True)
+            held["d", i, sig] = diff
+
+        def errors(i, sig):
+            squared = stage.tile([P, BLK, P], F32)
+            into = d2_sums[:, sig, i:i + 1] if i < NBLK - 1 else shares[1][:, sig:sig + 1]
+            nc.scalar.activation(out=squared[:], in_=held["d", i, sig][:], func=AF.Square, scale=1.0 / math.sqrt(128.0 * MEAN), accum_out=into)
+
+        matrix_tables()
 
         def blocks_of(b):
             return range(BATCHES[b][0], BATCHES[b][0] + BATCHES[b][1]) if 0 <= b < len(BATCHES) else range(0)
 
         last = len(BATCHES) - 1
+
+        def front_a(f):
+            if f < NBLK:
+                if f + 2 < NBLK:
+                    load_h1(f + 2)
+                turn_h1(f, 0)
+                group_h1(f, 0)
+
+        def front_b(f):
+            if f < NBLK:
+                turn_h1(f, 1)
+                group_h1(f, 1)
+                quantize_h1(f)
+
+        def front_c(f, c):
+            if f < NBLK:
+                for cc in (c, c + 1):
+                    hidden(f, cc)
+                    relu(f, cc)
+                if c == 2:
+                    group_h2(f)
+                    quantize_h2(f)
+
+        def front_d(f):
+            if f < NBLK:
+                product(f)
+                columns(f)
+                clip_columns(f)
+
+        def front_e(f):
+            if f < NBLK:
+                turn_x(f)
+                rows(f)
+                clip_rows(f)
+
+        def do_fold(i, s):
+            fold(i, s)
+            folded(i, s)
+
+        def twists(f):
+            if f < NBLK:
+                for s in range(3):
+                    for w in range(4):
+                        twist_copy(f, s, w)
+
+        def compare(i, sig):
+            for s in range(3):
+                if FAST[s][0] == sig:
+                    squares(i, s)
+            differences(i, sig)
+            errors(i, sig)
+
+        front_a(0)
+        front_b(0)
+        front_c(0, 0)
+        front_c(0, 2)
+        second_weights()
+        front_d(0)
+        front_e(0)
+        twists(0)
         for b in range(last + 3):
-            for i in blocks_of(b - 1) if b <= last else range(0):
-                matrices(i)
-                targets(i)
-            for i in blocks_of(b):
-                if i > 0:
-                    first_layer(i)
-                    second_layer(i)
-                inputs(i)
-            if b == 0:
-                matrix_tables()
-            for i in blocks_of(b - 2):
-                compare(i)
-            for i in blocks_of(b) if b == last else range(0):
-                matrices(i)
-                targets(i)
-                lag_zero(i)
-            if b <= last:
-                for i in blocks_of(b - 1):
-                    lag_zero(i)
+            for j in blocks_of(b - 1) if b <= last else range(0):
+                matrices(j)
+                targets(j)
+            todo = [j for j in blocks_of(b - 2)]
+            here = [i for i in blocks_of(b)]
+            for n, i in enumerate(here):
+                mine = todo[n * len(todo) // len(here):(n + 1) * len(todo) // len(here)]
+                f = i + 1
+                front_a(f)
+                front_b(f)
+                front_c(f, 0)
+                front_c(f, 2)
+                do_fold(i, 0)
+                do_fold(i, 1)
+                do_fold(i, 2)
+                for j in mine:
+                    compare(j, 0)
+                front_d(f)
+                for j in mine:
+                    compare(j, 1)
+                twists(f)
+                front_e(f)
+            if not here:
+                for j in todo:
+                    compare(j, 0)
+                    compare(j, 1)
+            for j in blocks_of(b) if b == last else range(0):
+                matrices(j)
+                targets(j)
+                lag_zero(j, 0)
+                lag_zero(j, 1)
             while plain_pairs:
                 next_pair()
+            if b <= last:
+                for j in blocks_of(b - 1):
+                    lag_zero(j, 0)
+                    lag_zero(j, 1)
             if 0 < b < last + 2:
                 transforms(b - 1)
 

@@ -44,9 +44,9 @@ def tile_qdtssolveronnx_pa_kernel(tc, h1, w_hid2, b_hid2, w_out, b_out, norm_roo
         h1_pool = ctx.enter_context(tc.tile_pool(name="h1_pool", bufs=3))
         stage = ctx.enter_context(tc.tile_pool(name="stage", bufs=2))
         x_pool = ctx.enter_context(tc.tile_pool(name="x_pool", bufs=4))
-        z_pool = ctx.enter_context(tc.tile_pool(name="z_pool", bufs=6))
+        z_pool = ctx.enter_context(tc.tile_pool(name="z_pool", bufs=12))
         sq_pool = ctx.enter_context(tc.tile_pool(name="sq_pool", bufs=3))
-        th_pool = ctx.enter_context(tc.tile_pool(name="th_pool", bufs=6))
+        th_pool = ctx.enter_context(tc.tile_pool(name="th_pool", bufs=4))
         batch_pool = ctx.enter_context(tc.tile_pool(name="batch_pool", bufs=2))
         fft = ctx.enter_context(tc.tile_pool(name="fft", bufs=1))
         ps_h2 = ctx.enter_context(tc.psum_pool(name="ps_h2", bufs=3))
@@ -60,12 +60,15 @@ def tile_qdtssolveronnx_pa_kernel(tc, h1, w_hid2, b_hid2, w_out, b_out, norm_roo
             nc.sync.dma_start(out=w1_sb[:, 2 * a:2 * a + 2, :], in_=w1_rows[:, 2 * a:2 * a + 2, :])
         h1_rows = h1.rearrange("(i p t) k -> i p t k", p=P, t=BLK)
         h1_tiles = {}
+        roots = {}
 
         def load_h1(i):
             h1_sb = h1_pool.tile([P, BLK, H], BF16, name="h1_sb")
             for half in ((slice(0, 2), slice(2, 4)) if i == 0 else (slice(0, 4),)):
                 nc.sync.dma_start(out=h1_sb[:, half, :], in_=h1_rows[i][:, half, :])
             h1_tiles[i] = h1_sb
+            roots[i] = h1_pool.tile([P, BLK * P], BF16, name="roots_new", bufs=4)
+            nc.sync.dma_start(out=roots[i][:], in_=norm_root.rearrange("(i r) o -> i (r o)", i=NBLK)[i].partition_broadcast(P))
 
         b1 = keep.tile([P, 4], BF16)
         b2 = keep.tile([P, 1], BF16)
@@ -81,8 +84,6 @@ def tile_qdtssolveronnx_pa_kernel(tc, h1, w_hid2, b_hid2, w_out, b_out, norm_roo
         load_h1(0)
         w2_sb = keep.tile([P, H], BF16)
         nc.sync.dma_start(out=w2_sb[:], in_=w_out)
-        nr_all = keep.tile([P, B], BF16)
-        nc.sync.dma_start(out=nr_all[:], in_=norm_root.rearrange("r o -> (r o)").partition_broadcast(P))
         load_h1(1)
         ident_bf = keep.tile([P, P], BF16)
         make_identity(nc, ident_bf[:])
@@ -180,7 +181,7 @@ def tile_qdtssolveronnx_pa_kernel(tc, h1, w_hid2, b_hid2, w_out, b_out, norm_roo
         def columns(i):
             x_cols[i] = x_pool.tile([P, BLK, P], F32, name="x_cols_new")
             mul_add(out=x_cols[i][:], in0=held["y", i][:].rearrange("j (t p) -> j t p", t=BLK), scalar=b2[:, 0:1],
-                    in1=nr_all[:, BLK * P * i:BLK * P * (i + 1)].rearrange("j (p t) -> j t p", t=BLK), op0=ALU.add, op1=ALU.mult)
+                    in1=roots[i][:].rearrange("j (p t) -> j t p", t=BLK), op0=ALU.add, op1=ALU.mult)
 
         def clip_columns(i):
             xc_cols[i] = stage.tile([P, BLK, P], F32, name="xc_cols_new")
@@ -201,11 +202,13 @@ def tile_qdtssolveronnx_pa_kernel(tc, h1, w_hid2, b_hid2, w_out, b_out, norm_roo
             for sig in range(2):
                 nc.sync.dma_start(out=x_out[sig][i], in_=x_rows[i][:, sig, :, :])
 
-        t_pad = keep.tile([P, TILES, N], BF16)
-        nc.gpsimd.memset(t_pad[:], 0.0)
+        t_pads = {}
         t_rows = T.rearrange("(i p t) c -> i p t c", p=P, t=BLK)
-        for i in range(NBLK):
-            nc.sync.dma_start(out=t_pad[:, BLK * i:BLK * (i + 1), 0:LAGS], in_=t_rows[i])
+
+        def load_targets(i):
+            t_pads[i] = h1_pool.tile([P, BLK, N], BF16, name="t_pad_new", bufs=4)
+            nc.gpsimd.memset(t_pads[i][:], 0.0)
+            nc.sync.dma_start(out=t_pads[i][:, :, 0:LAGS], in_=t_rows[i])
 
         def sines(phase, width, name):
             nc.vector.tensor_single_scalar(out=phase, in_=phase, scalar=511, op=ALU.bitwise_and)
@@ -253,8 +256,8 @@ def tile_qdtssolveronnx_pa_kernel(tc, h1, w_hid2, b_hid2, w_out, b_out, norm_roo
             nc.vector.tensor_copy(out=p_float[:], in_=p_index[:])
             freq = keep.tile([P, 2, G], I32)
             for hf in range(2):
-                nc.gpsimd.iota(freq[:, hf, 0:L], pattern=[[16, L // 2], [8, 2]], base=4 * hf + 1, channel_multiplier=0)
-                nc.gpsimd.iota(freq[:, hf, L:G], pattern=[[-16, L // 2], [8, 2]], base=16 * L + 4 * hf + 1, channel_multiplier=0)
+                nc.gpsimd.iota(freq[:, hf, 0:L], pattern=[[16, 2], [32, L // 4], [8, 2]], base=4 * hf + 1, channel_multiplier=0)
+                nc.gpsimd.iota(freq[:, hf, L:G], pattern=[[-16, 2], [-32, L // 4], [8, 2]], base=16 * L + 4 * hf + 1, channel_multiplier=0)
                 nc.gpsimd.iota(freq[:, hf, L:L + 2], pattern=[[8, 2]], base=8 * L + 4 * hf + 1, channel_multiplier=0)
             last_freq = 16 * (L - L // 2 + 1) + 8 + 4 + 1
             phase = fft.tile([P, 6 * G], I32, tag="diag")
@@ -338,9 +341,10 @@ def tile_qdtssolveronnx_pa_kernel(tc, h1, w_hid2, b_hid2, w_out, b_out, norm_roo
             held = []
 
             def turn():
+                load_targets(i)
                 t_t = ps_t.tile([P, BLK, P], BF16, tag="t")
                 for t in range(BLK):
-                    nc.tensor.transpose(t_t[:, t, :], t_pad[:, BLK * i + t, :], ident_bf[:])
+                    nc.tensor.transpose(t_t[:, t, :], t_pads[i][:, t, :], ident_bf[:])
                 t_cols = stage.tile([P, BLK, P], F32)
                 nc.scalar.copy(out=t_cols[:], in_=t_t[:])
                 held.append(t_cols)
@@ -360,7 +364,7 @@ def tile_qdtssolveronnx_pa_kernel(tc, h1, w_hid2, b_hid2, w_out, b_out, norm_roo
                     nc.scalar.copy(out=th[i][:], in_=th_acc[:])
                     if i == NBLK - 1:
                         products = stage.tile([P, N], F32)
-                        nc.gpsimd.tensor_tensor(out=products[:], in0=t_pad[:, TILES - 1, :], in1=last_col[:], op=ALU.mult)
+                        nc.gpsimd.tensor_tensor(out=products[:], in0=t_pads[i][:, BLK - 1, :], in1=last_col[:], op=ALU.mult)
                         summed = stage.tile([P, N], F32)
                         nc.scalar.activation(out=summed[:], in_=products[:], func=AF.Copy, accum_out=th[i][:, BLK - 1, N - 1:N])
 
@@ -445,20 +449,27 @@ def tile_qdtssolveronnx_pa_kernel(tc, h1, w_hid2, b_hid2, w_out, b_out, norm_roo
             def into_planes(k):
                 if k == 0:
                     return (planes[:, :, 0:4:2, 0, :], planes[:, :, 1:4:2, 0, :]), 1
-                return (planes[:, :, :, k, :], 1) if k < L // 2 else (planes[:, :, :, L - k, :], -1)
+                k, step = (k, 1) if k < L // 2 else (L - k, -1)
+                return planes[:, :, :, k // 2 + L // 4 * (k % 2), :], step
 
             join(sixteenths[:, 0:1, :, :], sixteenths[:, 1:2, :, :], 16, fours, (4, 2, 10, 1, 9, 5, 13), into_planes)
 
-        def squares(i, s):
+        def squares(i, s, first=0, last=L // 2):
             b, tb, sub = place(i)
             sig, hf = FAST[s]
-            view = spectrum[b][:, 0, :, :, :].rearrange("p c k (e s t) -> p s (c k e) t", e=2, s=3)
-            out = sq[i][:, :, :, sig, hf, :].rearrange("p t r x -> p r x t")
-            part = view[:, s, :, sub].rearrange("p (r x) t -> p r x t", r=2)
-            if i == NBLK - 1 and s == 1:
-                tensor_tensor(out=out, in0=part, in1=part, op=ALU.mult)
-            else:
+            view = spectrum[b][:, 0, :, first:last, :].rearrange("p c k (e s t) -> p s c (k e) t", e=2, s=3)
+            if last - first == L // 2:
+                out = sq[i][:, :, :, sig, hf, :].rearrange("p t r x -> p r x t")
+                part = spectrum[b][:, 0, :, :, :].rearrange("p c k (e s t) -> p s (c k e) t", e=2, s=3)[:, s, :, sub].rearrange("p (r x) t -> p r x t", r=2)
                 nc.scalar.activation(out=out, in_=part, func=AF.Square)
+                return
+            for r in range(2):
+                out = sq[i][:, :, r, sig, hf, :].rearrange("p t (c x) -> p c x t", c=2)[:, :, 2 * first:2 * last, :]
+                part = view[:, s, 2 * r:2 * r + 2, :, sub]
+                if i == NBLK - 1 and s == 1 and first > 0:
+                    tensor_tensor(out=out, in0=part, in1=part, op=ALU.mult)
+                else:
+                    nc.scalar.activation(out=out, in_=part, func=AF.Square)
 
         def differences(i, sig):
             diff = ps_spec.tile([P, BLK, P], F32, tag="spec", name="diff")
@@ -528,7 +539,10 @@ def tile_qdtssolveronnx_pa_kernel(tc, h1, w_hid2, b_hid2, w_out, b_out, norm_roo
         def compare(i, sig):
             for s in range(3):
                 if FAST[s][0] == sig:
-                    squares(i, s)
+                    if i < NBLK - 1:
+                        squares(i, s)
+                    else:
+                        squares(i, s, L // 4, L // 2)
             differences(i, sig)
             errors(i, sig)
 
@@ -546,34 +560,44 @@ def tile_qdtssolveronnx_pa_kernel(tc, h1, w_hid2, b_hid2, w_out, b_out, norm_roo
                 targets(j)
             todo = [j for j in blocks_of(b - 2)]
             here = [i for i in blocks_of(b)]
-            for n, i in enumerate(here):
-                mine = todo[n * len(todo) // len(here):(n + 1) * len(todo) // len(here)]
-                f = i + 1
+            ahead = [f for f in blocks_of(b + 1)]
+            for f in ahead:
                 front_a(f)
                 front_b(f)
-                front_c(f, 0)
-                front_c(f, 2)
+            for c in (0, 2):
+                for f in ahead:
+                    front_c(f, c)
+            for n, i in enumerate(here):
                 do_fold(i, 0)
                 do_fold(i, 1)
                 do_fold(i, 2)
-                for j in mine:
-                    compare(j, 0)
+                if n < len(ahead):
+                    front_d(ahead[n])
+            for f in ahead[len(here):]:
                 front_d(f)
-                for j in mine:
-                    compare(j, 1)
+            for j in todo if here else []:
+                compare(j, 0)
+                compare(j, 1)
+            for f in ahead:
                 twists(f)
                 front_e(f)
-            if not here:
+            if b > last:
+                for j in blocks_of(last) if b == last + 1 else range(0):
+                    matrices(j)
+                    targets(j)
+                for j in todo if b == last + 2 else range(0):
+                    for s in range(3):
+                        squares(j, s, 0, L // 4)
                 for j in todo:
-                    compare(j, 0)
-                    compare(j, 1)
-            for j in blocks_of(b) if b == last else range(0):
-                matrices(j)
-                targets(j)
-                lag_zero(j, 0)
-                lag_zero(j, 1)
+                    for sig in range(2):
+                        compare(j, sig)
+                        if plain_pairs:
+                            next_pair()
             while plain_pairs:
                 next_pair()
+            if b == last + 1:
+                lag_zero(NBLK - 1, 0)
+                lag_zero(NBLK - 1, 1)
             if b <= last:
                 for j in blocks_of(b - 1):
                     lag_zero(j, 0)

@@ -26,9 +26,9 @@ G = 64
 L = 32
 FAST = ((0, 1), (1, 0), (1, 1))
 VECTOR_COPIES = (3, 1, 1)
-FIRST_COPIES = 3
+FIRST_COPIES = 4
 BATCHES = ((0, 1), (1, 2), (3, 2), (5, 2), (7, 1))
-SHARED = 2
+SHARED = 1
 RHO = math.sqrt(0.5)
 MEAN = 2.0 * B * LAGS
 
@@ -51,8 +51,8 @@ def tile_qdtssolveronnx_pa_kernel(tc, h1, w_hid2, b_hid2, w_out, b_out, norm_roo
         fft = ctx.enter_context(tc.tile_pool(name="fft", bufs=1))
         ps_h2 = ctx.enter_context(tc.psum_pool(name="ps_h2", bufs=3))
         ps_x = ctx.enter_context(tc.psum_pool(name="ps_x", bufs=1))
-        ps_spec = ctx.enter_context(tc.psum_pool(name="ps_spec", bufs=3))
-        ps_t = ctx.enter_context(tc.psum_pool(name="ps_t", bufs=1))
+        ps_spec = ctx.enter_context(tc.psum_pool(name="ps_spec", bufs=4))
+        ps_t = ps_spec
 
         w1_sb = h1_pool.tile([P, BLK, H], BF16, name="w1_sb", tag="h1_sb")
         w1_rows = w_hid2.rearrange("(p c) k -> p c k", c=4)
@@ -342,7 +342,7 @@ def tile_qdtssolveronnx_pa_kernel(tc, h1, w_hid2, b_hid2, w_out, b_out, norm_roo
 
             def turn():
                 load_targets(i)
-                t_t = ps_t.tile([P, BLK, P], BF16, tag="t")
+                t_t = ps_t.tile([P, BLK, P], BF16, tag="spec")
                 for t in range(BLK):
                     nc.tensor.transpose(t_t[:, t, :], t_pads[i][:, t, :], ident_bf[:])
                 t_cols = stage.tile([P, BLK, P], F32)
@@ -352,7 +352,7 @@ def tile_qdtssolveronnx_pa_kernel(tc, h1, w_hid2, b_hid2, w_out, b_out, norm_roo
             def pair(first):
                 if first == 0:
                     th[i] = th_pool.tile([P, BLK, 2 * G], F32, name="th_new")
-                    held.append(ps_t.tile([P, BLK, P], F32, tag="t", name="th_acc"))
+                    held.append(ps_t.tile([P, BLK, P], F32, tag="spec", name="th_acc"))
                 t_cols, th_acc = held
                 for t in range(first, first + 2):
                     if BLK * i + t == TILES - 1:

@@ -67,6 +67,8 @@ def tile_qdtssolveronnx_pa_kernel(tc, h1, w_hid2, b_hid2, w_out, b_out, norm_roo
             for half in ((slice(0, 2), slice(2, 4)) if i == 0 else (slice(0, 4),)):
                 nc.sync.dma_start(out=h1_sb[:, half, :], in_=h1_rows[i][:, half, :])
             h1_tiles[i] = h1_sb
+
+        def load_roots(i):
             roots[i] = h1_pool.tile([P, BLK * P], BF16, name="roots_new", bufs=4)
             nc.sync.dma_start(out=roots[i][:], in_=norm_root.rearrange("(i r) o -> i (r o)", i=NBLK)[i].partition_broadcast(P))
 
@@ -82,9 +84,10 @@ def tile_qdtssolveronnx_pa_kernel(tc, h1, w_hid2, b_hid2, w_out, b_out, norm_roo
         ident = keep.tile([P, P], F32)
         make_identity(nc, ident[:])
         load_h1(0)
+        load_h1(1)
         w2_sb = keep.tile([P, H], BF16)
         nc.sync.dma_start(out=w2_sb[:], in_=w_out)
-        load_h1(1)
+        load_roots(0)
         ident_bf = keep.tile([P, P], BF16)
         make_identity(nc, ident_bf[:])
 
@@ -474,6 +477,8 @@ def tile_qdtssolveronnx_pa_kernel(tc, h1, w_hid2, b_hid2, w_out, b_out, norm_roo
         def differences(i, sig):
             diff = ps_spec.tile([P, BLK, P], F32, tag="spec", name="diff")
             for t in range(BLK):
+                if t == 2 and plain_pairs:
+                    next_pair()
                 for r in range(2):
                     nc.tensor.matmul(out=diff[:, t, :], lhsT=sq[i][:, t, r, sig, :, :].rearrange("p f g -> p (f g)"), rhs=ident[:],
                                      is_transpose=True, start=r == 0, stop=False)
@@ -507,6 +512,8 @@ def tile_qdtssolveronnx_pa_kernel(tc, h1, w_hid2, b_hid2, w_out, b_out, norm_roo
 
         def front_c(f, c):
             if f < NBLK:
+                if f > 0 and c == 0:
+                    load_roots(f)
                 for cc in (c, c + 1):
                     hidden(f, cc)
                     relu(f, cc)

import math
from contextlib import ExitStack

import concourse.mybir as mybir
from concourse.masks import make_identity

F32 = mybir.dt.float32
BF16 = mybir.dt.bfloat16
I32 = mybir.dt.int32
U32 = mybir.dt.uint32
U8 = mybir.dt.uint8
FP8X4 = mybir.dt.float8_e4m3fn_x4
ALU = mybir.AluOpType
AF = mybir.ActivationFunctionType
AX = mybir.AxisListType

P = 128
B = 4096
H = 512
N = 128
LAGS = 127
TILES = B // P
BLK = 4
NBLK = TILES // BLK
G = 64
L = 32
FAST = ((0, 1), (1, 0), (1, 1))
VECTOR_COPIES = (3, 1, 1)
FIRST_COPIES = 4
BATCHES = ((0, 1), (1, 2), (3, 2), (5, 2), (7, 1))
SHARED = 1
RHO = math.sqrt(0.5)
MEAN = 2.0 * B * LAGS

FLOPS = 2 * B * H * (H + N) + 2 * 2 * B * (N * LAGS // 2)


def tile_qdtssolveronnx_pa_kernel(tc, h1, w_hid2, b_hid2, w_out, b_out, norm_root, T, out_0, out_1, out_2, out_3):
    nc = tc.nc
    tensor_tensor = nc.vector.tensor_tensor
    mul_add = nc.vector.scalar_tensor_tensor
    with ExitStack() as ctx:
        keep = ctx.enter_context(tc.tile_pool(name="keep", bufs=1))
        h1_pool = ctx.enter_context(tc.tile_pool(name="h1_pool", bufs=3))
        stage = ctx.enter_context(tc.tile_pool(name="stage", bufs=2))
        x_pool = ctx.enter_context(tc.tile_pool(name="x_pool", bufs=4))
        z_pool = ctx.enter_context(tc.tile_pool(name="z_pool", bufs=12))
        sq_pool = ctx.enter_context(tc.tile_pool(name="sq_pool", bufs=3))
        th_pool = ctx.enter_context(tc.tile_pool(name="th_pool", bufs=4))
        batch_pool = ctx.enter_context(tc.tile_pool(name="batch_pool", bufs=2))
        fft = ctx.enter_context(tc.tile_pool(name="fft", bufs=1))
        ps_h2 = ctx.enter_context(tc.psum_pool(name="ps_h2", bufs=3))
        ps_x = ctx.enter_context(tc.psum_pool(name="ps_x", bufs=1))
        ps_spec = ctx.enter_context(tc.psum_pool(name="ps_spec", bufs=4))
        ps_t = ps_spec

        w1_sb = h1_pool.tile([P, BLK, H], BF16, name="w1_sb", tag="h1_sb")
        w1_rows = w_hid2.rearrange("(p c) k -> p c k", c=4)
        for a in range(2):
            nc.sync.dma_start(out=w1_sb[:, 2 * a:2 * a + 2, :], in_=w1_rows[:, 2 * a:2 * a + 2, :])
        h1_rows = h1.rearrange("(i p t) k -> i p t k", p=P, t=BLK)
        h1_tiles = {}
        roots = {}

        def load_h1(i):
            h1_sb = h1_pool.tile([P, BLK, H], BF16, name="h1_sb")
            for half in ((slice(0, 2), slice(2, 4)) if i == 0 else (slice(0, 4),)):
                nc.sync.dma_start(out=h1_sb[:, half, :], in_=h1_rows[i][:, half, :])
            h1_tiles[i] = h1_sb

        def load_roots(i):
            roots[i] = h1_pool.tile([P, BLK * P], BF16, name="roots_new", bufs=4)
            nc.sync.dma_start(out=roots[i][:], in_=norm_root.rearrange("(i r) o -> i (r o)", i=NBLK)[i].partition_broadcast(P))

        b1 = keep.tile([P, 4], BF16)
        b2 = keep.tile([P, 1], BF16)
        with nc.allow_non_contiguous_dma(reason="two short vectors, a few bytes a partition"):
            nc.scalar.dma_start(out=b1[:], in_=b_hid2.rearrange("(p c) -> p c", c=4))
            nc.scalar.dma_start(out=b2[:], in_=b_out.rearrange("(p o) -> p o", o=1))
        zero = keep.tile([P, 1], F32)
        nc.vector.memset(zero[:], 0.0)
        first_sine = keep.tile([P, 1], F32)
        nc.scalar.activation(out=first_sine[:], in_=zero[:], func=AF.Sin)
        ident = keep.tile([P, P], F32)
        make_identity(nc, ident[:])
        load_h1(0)
        load_h1(1)
        w2_sb = keep.tile([P, H], BF16)
        nc.sync.dma_start(out=w2_sb[:], in_=w_out)
        load_roots(0)
        ident_bf = keep.tile([P, P], BF16)
        make_identity(nc, ident_bf[:])

        w1_grouped = stage.tile([P, 4 * P, 4], BF16, name="w1_grouped", tag="h1_grouped", align_bytes=64)
        w1_grouped32 = w1_grouped[:].bitcast(F32)
        w1_words = w1_sb[:].bitcast(F32)
        for a in range(2):
            w1_t = ps_h2.tile([P, 2, 2, P], F32, tag="h2")
            for u in range(2):
                for c in range(2):
                    nc.tensor.transpose(w1_t[:, u, c, :], w1_words[:, 2 * a + c, u:2 * P:2], ident[:])
            (nc.vector.tensor_copy, nc.scalar.copy)[a](out=w1_grouped32[:, 2 * P * a:2 * P * (a + 1), :],
                                                       in_=w1_t[:].rearrange("q u c m -> q (c m) u"))
        w1_codes = keep.tile([P, 4 * P], U32, align_bytes=64)
        w1_scales = keep.tile([P, 4 * P], U8, align_bytes=64)
        nc.vector.quantize_mx(out=w1_codes[:].bitcast(FP8X4), scales=w1_scales[:], in_=w1_grouped[:].rearrange("q n f -> q (n f)"))
        w2_codes = keep.tile([P, P], U32, align_bytes=64)
        w2_scales = keep.tile([P, P], U8, align_bytes=64)

        def second_weights():
            w2_grouped = keep.tile([P, P, 4], BF16, align_bytes=64)
            w2_words = w2_sb[:].bitcast(F32).rearrange("p (m u) -> p u m", u=2)
            w2_t = ps_x.tile([P, 2, P], F32, tag="x")
            for u in range(2):
                nc.tensor.transpose(w2_t[:, u, :], w2_words[:, u, :], ident[:])
            nc.vector.tensor_copy(out=w2_grouped[:].bitcast(F32), in_=w2_t[:].rearrange("q u n -> q n u"))
            nc.vector.quantize_mx(out=w2_codes[:].bitcast(FP8X4), scales=w2_scales[:], in_=w2_grouped[:].rearrange("q n f -> q (n f)"))

        x_rows = {}
        x_out = [out.rearrange("(i p t) j -> i p t j", p=P, t=BLK) for out in (out_0, out_2)]
        x_cols = {}
        xc_cols = {}
        h2_grouped = {}

        h1_grouped = {}
        h1_codes = {}
        h2_planes = {}
        h2_codes = {}
        held = {}

        def turn_h1(i, a):
            h1_words = h1_tiles[i][:].bitcast(F32)
            if a == 0:
                h1_grouped[i] = stage.tile([P, BLK * P, 4], BF16, name="h1_grouped_new", tag="h1_grouped", align_bytes=64)
            h1_t = ps_h2.tile([P, 2, 2, P], F32, tag="h2")
            for u in range(2):
                for t in range(2):
                    nc.tensor.transpose(h1_t[:, u, t, :], h1_words[:, 2 * a + t, u:2 * P:2], ident[:])
            held["h1", i, a] = h1_t

        def group_h1(i, a):
            copy = nc.vector.tensor_copy if i < SHARED and a == 0 else nc.scalar.copy
            copy(out=h1_grouped[i][:].bitcast(F32)[:, 2 * P * a:2 * P * (a + 1), :], in_=held["h1", i, a][:].rearrange("q u t p -> q (t p) u"))

        def quantize_h1(i):
            codes = stage.tile([P, BLK * P], U32, name="h1_codes_new", align_bytes=64)
            scales = stage.tile([P, BLK * P], U8, name="h1_scales_new", align_bytes=64)
            nc.vector.quantize_mx(out=codes[:].bitcast(FP8X4), scales=scales[:], in_=h1_grouped[i][:].rearrange("q n f -> q (n f)"))
            h1_codes[i] = codes, scales

        def hidden(i, c):
            codes, scales = h1_codes[i]
            h2_acc = ps_h2.tile([P, BLK * P], F32, tag="h2")
            nc.tensor.matmul_mx(out=h2_acc[:], lhsT=w1_codes[:, P * c:P * (c + 1)].bitcast(FP8X4), lhsT_scale=w1_scales[:, P * c:P * (c + 1)],
                                rhs=codes[:].bitcast(FP8X4), rhs_scale=scales[:], start=True, stop=True)
            held["h2", i, c] = h2_acc

        def relu(i, c):
            if c == 0:
                h2_planes[i] = stage.tile([P, 4, BLK * P], BF16, name="h2_planes_new")
            h2_acc = held["h2", i, c]
            if i < SHARED and c % 2 == 1:
                nc.vector.tensor_scalar(out=h2_planes[i][:, c, :], in0=h2_acc[:], scalar1=b1[:, c:c + 1], scalar2=0.0, op0=ALU.add, op1=ALU.max)
            else:
                nc.scalar.activation(out=h2_planes[i][:, c, :], in_=h2_acc[:], func=AF.Relu, bias=b1[:, c:c + 1], scale=1.0)

        def group_h2(i):
            h2_grouped[i] = stage.tile([P, BLK * P, 4], BF16, name="h2_grouped_new", align_bytes=64)
            nc.vector.tensor_copy(out=h2_grouped[i][:].rearrange("m (a i) c -> m a c i", i=4), in_=h2_planes[i][:].rearrange("m c (a i) -> m a c i", i=4))

        def quantize_h2(i):
            codes = stage.tile([P, BLK * P], U32, name="h2_codes_new", align_bytes=64)
            scales = stage.tile([P, BLK * P], U8, name="h2_scales_new", align_bytes=64)
            nc.vector.quantize_mx(out=codes[:].bitcast(FP8X4), scales=scales[:], in_=h2_grouped[i][:].rearrange("m n f -> m (n f)"))
            h2_codes[i] = codes, scales

        def product(i):
            codes, scales = h2_codes[i]
            y_acc = ps_x.tile([P, BLK * P], F32, tag="x")
            nc.tensor.matmul_mx(out=y_acc[:], lhsT=w2_codes[:].bitcast(FP8X4), lhsT_scale=w2_scales[:],
                                rhs=codes[:].bitcast(FP8X4), rhs_scale=scales[:], start=True, stop=True)
            held["y", i] = y_acc

        def columns(i):
            x_cols[i] = x_pool.tile([P, BLK, P], F32, name="x_cols_new")
            mul_add(out=x_cols[i][:], in0=held["y", i][:].rearrange("j (t p) -> j t p", t=BLK), scalar=b2[:, 0:1],
                    in1=roots[i][:].rearrange("j (p t) -> j t p", t=BLK), op0=ALU.add, op1=ALU.mult)

        def clip_columns(i):
            xc_cols[i] = stage.tile([P, BLK, P], F32, name="xc_cols_new")
            nc.vector.tensor_scalar(out=xc_cols[i][:], in0=x_cols[i][:], scalar1=-2.0, scalar2=2.0, op0=ALU.max, op1=ALU.min)

        def turn_x(i):
            x_t = ps_x.tile([P, BLK, P], F32, tag="x")
            for t in range(BLK):
                nc.tensor.transpose(x_t[:, t, :], x_cols[i][:, t, :], ident[:])
            held["x", i] = x_t

        def rows(i):
            x_rows[i] = x_pool.tile([P, 2, BLK, N], F32, name="x_rows_new")
            nc.scalar.copy(out=x_rows[i][:, 0, :, :], in_=held["x", i][:])

        def clip_rows(i):
            nc.vector.tensor_scalar(out=x_rows[i][:, 1, :, :], in0=x_rows[i][:, 0, :, :], scalar1=-2.0, scalar2=2.0, op0=ALU.max, op1=ALU.min)
            for sig in range(2):
                nc.sync.dma_start(out=x_out[sig][i], in_=x_rows[i][:, sig, :, :])

        t_pads = {}
        t_rows = T.rearrange("(i p t) c -> i p t c", p=P, t=BLK)

        def load_targets(i):
            t_pads[i] = h1_pool.tile([P, BLK, N], BF16, name="t_pad_new", bufs=4)
            nc.gpsimd.memset(t_pads[i][:], 0.0)
            nc.sync.dma_start(out=t_pads[i][:, :, 0:LAGS], in_=t_rows[i])

        def sines(phase, width, name):
            nc.vector.tensor_single_scalar(out=phase, in_=phase, scalar=511, op=ALU.bitwise_and)
            angle = fft.tile([P, width], F32, name=name + "_angle", tag="add2")
            nc.vector.tensor_scalar(out=angle[:], in0=phase, scalar1=-256.0, scalar2=None, op0=ALU.add)
            edge = fft.tile([P, width], F32, name=name + "_edge", tag="sub2")
            nc.vector.tensor_scalar(out=edge[:], in0=angle[:], scalar1=-256.0, scalar2=256.0, op0=ALU.is_equal, op1=ALU.mult)
            tensor_tensor(out=angle[:], in0=angle[:], in1=edge[:], op=ALU.add)
            table = fft.tile([P, width], F32, name=name + "_table", tag="straight")
            nc.scalar.activation(out=table[:], in_=angle[:], func=AF.Sin, scale=math.pi / 256.0)
            return table

        COS = 256 + 128

        twist_phase = keep.tile([P, 8], I32)
        for hf in range(2):
            for e in range(2):
                nc.gpsimd.iota(twist_phase[:, 4 * hf + e:4 * hf + e + 3:2], pattern=[[128, 2]], base=COS,
                               channel_multiplier=8 * e + 4 * hf + 1)
        parts = sines(twist_phase[:], 8, "twist")[:].rearrange("p (f s) -> p f s", f=2)
        twist = keep.tile([P, 2, 4], F32)
        for a in range(4):
            quarter = slice(L * a, L * (a + 1))
            nc.gpsimd.tensor_copy(out=twist[quarter, :, 0:4 - a], in_=parts[quarter, :, a:4])
            if a > 0:
                nc.gpsimd.tensor_copy(out=twist[quarter, :, 4 - a:4], in_=parts[quarter, :, 0:a])
        ident_twice = fft.tile([P, 2 * P], F32, tag="diag")
        for c in range(2):
            nc.gpsimd.tensor_copy(out=ident_twice[:, P * c:P * (c + 1)], in_=ident[:])
        turn_matrices = keep.tile([P, 4, P], F32)
        for w in range(4):
            nc.gpsimd.tensor_copy(out=turn_matrices[:, w, :].rearrange("p (r n e) -> p r n e", r=2, e=2),
                                  in_=ident_twice[:, P - L * w:2 * P - L * w].rearrange("p (r e n) -> p r n e", r=2, e=2))
        turns = [turn_matrices[:, w, :] for w in range(4)]

        x_matrix = keep.tile([P, 2 * G], F32)
        t_matrix = keep.tile([P, 2 * G], F32)
        last_col = keep.tile([P, N], F32)

        def matrix_tables():
            p_index = keep.tile([P, 2], I32)
            nc.gpsimd.iota(p_index[:, 0:1], pattern=[[0, 1]], base=0, channel_multiplier=1)
            nc.gpsimd.iota(p_index[:, 1:2], pattern=[[0, 1]], base=LAGS, channel_multiplier=-1)
            p_float = keep.tile([P, 2], F32)
            nc.vector.tensor_copy(out=p_float[:], in_=p_index[:])
            freq = keep.tile([P, 2, G], I32)
            for hf in range(2):
                nc.gpsimd.iota(freq[:, hf, 0:L], pattern=[[16, 2], [32, L // 4], [8, 2]], base=4 * hf + 1, channel_multiplier=0)
                nc.gpsimd.iota(freq[:, hf, L:G], pattern=[[-16, 2], [-32, L // 4], [8, 2]], base=16 * L + 4 * hf + 1, channel_multiplier=0)
                nc.gpsimd.iota(freq[:, hf, L:L + 2], pattern=[[8, 2]], base=8 * L + 4 * hf + 1, channel_multiplier=0)
            last_freq = 16 * (L - L // 2 + 1) + 8 + 4 + 1
            phase = fft.tile([P, 6 * G], I32, tag="diag")
            nc.gpsimd.iota(phase[:, 4 * G:4 * G + N], pattern=[[-last_freq, N]], base=LAGS * last_freq + COS, channel_multiplier=0)
            nc.vector.tensor_scalar(out=phase[:, 0:G], in0=freq[:, 0, :], scalar1=p_float[:, 0:1], scalar2=float(COS),
                                    op0=ALU.mult, op1=ALU.add)
            nc.vector.tensor_scalar(out=phase[:, G:2 * G], in0=freq[:, 0, :], scalar1=p_float[:, 0:1], scalar2=256.0,
                                    op0=ALU.mult, op1=ALU.add)
            nc.vector.tensor_scalar(out=phase[:, 2 * G:4 * G], in0=freq[:].rearrange("p f g -> p (f g)"), scalar1=p_float[:, 1:2],
                                    scalar2=float(COS), op0=ALU.mult, op1=ALU.add)
            table = sines(phase[:], 6 * G, "matrix")
            nc.vector.tensor_copy(out=x_matrix[:], in_=table[:, 0:2 * G])
            nc.vector.tensor_scalar(out=t_matrix[:], in0=table[:, 2 * G:4 * G], scalar1=-2.0, scalar2=None, op0=ALU.mult)
            nc.vector.tensor_scalar(out=last_col[:], in0=table[:, 4 * G:6 * G], scalar1=-2.0, scalar2=None, op0=ALU.mult)

        r0 = keep.tile([P, 2, TILES], F32)
        d2_sums = keep.tile([P, 2, NBLK - 1], F32)
        shares = []
        for name in ("shares_before", "shares_last"):
            share = keep.tile([P, P], F32, name=name)
            nc.gpsimd.memset(share[:], 0.0)
            shares.append(share)
        v = {}
        sq = {}
        th = {}
        spectrum = {}

        def place(i):
            b = [k for k, (first, count) in enumerate(BATCHES) if first <= i < first + count][0]
            at = BLK * (i - BATCHES[b][0])
            return b, BLK * BATCHES[b][1], slice(at, at + BLK)

        def twist_copy(i, s, w):
            sig, hf = FAST[s]
            z_cols = z_pool.tile([P, BLK, P], F32, name="z_cols")
            x, factor = (x_cols[i], xc_cols[i])[sig], twist[:, hf, w:w + 1]
            if i < NBLK - 1 and w < (VECTOR_COPIES[s] if i > 0 else FIRST_COPIES):
                nc.vector.tensor_scalar(out=z_cols[:], in0=x[:], scalar1=factor, scalar2=None, op0=ALU.mult)
            else:
                nc.scalar.activation(out=z_cols[:], in_=x[:], func=AF.Copy, scale=factor)
            held["z", i, s, w] = z_cols

        def fold(i, s):
            v_rows = ps_spec.tile([P, BLK, P], F32, tag="spec", name="v_rows")
            for t in range(BLK):
                if t == 2 and plain_pairs:
                    next_pair()
                for w in range(4):
                    nc.tensor.matmul(out=v_rows[:, t, :], lhsT=held["z", i, s, w][:, t, :], rhs=turns[w], is_transpose=True, start=w == 0, stop=w == 3)
            held["v", i, s] = v_rows

        def folded(i, s):
            b, tb, sub = place(i)
            if b not in v:
                v[b] = batch_pool.tile([P, 2, 2 * L, 3 * tb], F32, name="v_new")
            v_view = v[b][:].rearrange("p r x (h t) -> p r x h t", h=3)
            nc.scalar.copy(out=v_view[:, :, :, s, sub], in_=held["v", i, s][:].rearrange("p t (r x) -> p r x t", r=2))

        plain_pairs = []

        def next_pair():
            pair = plain_pairs[0]
            plain_pairs[:] = plain_pairs[1:]
            pair()

        def matrices(i):
            held = []

            def pair(first):
                if first == 0:
                    sq[i] = sq_pool.tile([P, BLK, 2, 2, 2, G], F32, name="sq_new")
                    held.append(ps_spec.tile([P, BLK, P], F32, tag="spec", name="spec0"))
                for t in range(first, first + 2):
                    nc.tensor.matmul(out=held[0][:, t, :], lhsT=x_cols[i][:, t, :], rhs=x_matrix[:], start=True, stop=True)
                if first == 2:
                    nc.scalar.activation(out=sq[i][:, :, :, 0, 0, :], in_=held[0][:].rearrange("p t (r g) -> p t r g", r=2), func=AF.Square)

            plain_pairs.extend([lambda: pair(0), lambda: pair(2)])

        def targets(i):
            held = []

            def turn():
                load_targets(i)
                t_t = ps_t.tile([P, BLK, P], BF16, tag="spec")
                for t in range(BLK):
                    nc.tensor.transpose(t_t[:, t, :], t_pads[i][:, t, :], ident_bf[:])
                t_cols = stage.tile([P, BLK, P], F32)
                nc.scalar.copy(out=t_cols[:], in_=t_t[:])
                held.append(t_cols)

            def pair(first):
                if first == 0:
                    th[i] = th_pool.tile([P, BLK, 2 * G], F32, name="th_new")
                    held.append(ps_t.tile([P, BLK, P], F32, tag="spec", name="th_acc"))
                t_cols, th_acc = held
                for t in range(first, first + 2):
                    if BLK * i + t == TILES - 1:
                        nc.tensor.transpose(th_acc[:, t, :], t_cols[:, t, :], ident[:])
                        nc.tensor.matmul(out=th_acc[:, t, 0:P - 1], lhsT=t_cols[:, t, :], rhs=t_matrix[:, 0:P - 1], start=True, stop=True)
                    else:
                        nc.tensor.matmul(out=th_acc[:, t, :], lhsT=t_cols[:, t, :], rhs=t_matrix[:], start=True, stop=True)
                if first == 2:
                    nc.scalar.copy(out=th[i][:], in_=th_acc[:])
                    if i == NBLK - 1:
                        products = stage.tile([P, N], F32)
                        nc.gpsimd.tensor_tensor(out=products[:], in0=t_pads[i][:, BLK - 1, :], in1=last_col[:], op=ALU.mult)
                        summed = stage.tile([P, N], F32)
                        nc.scalar.activation(out=summed[:], in_=products[:], func=AF.Copy, accum_out=th[i][:, BLK - 1, N - 1:N])

            turn()
            plain_pairs.extend([lambda: pair(0), lambda: pair(2)])

        def lag_zero(i, sig):
            for t in range(BLK):
                x_squares = stage.tile([P, N], F32)
                nc.scalar.activation(out=x_squares[:], in_=x_rows[i][:, sig, t, :], func=AF.Square,
                                     accum_out=r0[:, sig, BLK * i + t:BLK * i + t + 1])

        def turned(out, x, y):
            tensor_tensor(out=out[:, :, 0:2, :], in0=x, in1=y[:, :, ::-1, :], op=ALU.add)
            tensor_tensor(out=out[:, :, 2:4, :], in0=x[:, :, ::-1, :], in1=y, op=ALU.subtract)

        def join(a, b, n, fours, order, put):
            def slanted(k):
                t = math.sin(math.pi * k / n) / math.cos(math.pi * k / n)
                d = fft.tile([P, a.shape[1], 4, a.shape[3]], F32, name="d", tag="d", bufs=4)
                first, second = b[:, :, fours[k]:fours[k] + 2, :], b[:, :, fours[k] + 2:fours[k] + 4, :]
                mul_add(out=d[:, :, 0:2, :], in0=second, scalar=t, in1=first, op0=ALU.mult, op1=ALU.add)
                mul_add(out=d[:, :, 2:4, :], in0=first, scalar=-t, in1=second, op0=ALU.mult, op1=ALU.add)
                return d

            def joined(k, d):
                c = math.cos(math.pi * k / n)
                for at, factor in ((k, c), (n + k, -c)):
                    out, step = put(at)
                    mul_add(out=out, in0=d[:, :, ::step, :], scalar=factor, in1=a[:, :, fours[k]:fours[k] + 4, :][:, :, ::step, :],
                            op0=ALU.mult, op1=ALU.add)

            made = [slanted(k) for k in order[0:2]]
            out = put(0)[0]
            tensor_tensor(out=out[0], in0=a[:, :, 0:2, :], in1=b[:, :, 0:2, :], op=ALU.add)
            tensor_tensor(out=out[1], in0=a[:, :, 0:2, :], in1=b[:, :, 0:2, :], op=ALU.subtract)
            turned(put(n // 2)[0], a[:, :, 2:4, :], b[:, :, 2:4, :])
            for at, k in enumerate(order):
                if at + 2 < len(order):
                    made.append(slanted(order[at + 2]))
                joined(k, made[at])

        def transforms(b):
            z = 6 * BLK * BATCHES[b][1]
            x = v[b][:].rearrange("p r (m g e) z -> p r m g (e z)", m=8, e=2)
            halved = fft.tile([P, 2, 4, 8, z], F32, tag="sixteenths")
            add4, sub4 = halved[:, 0, :, :, :], halved[:, 1, :, :, :]
            for out, op in ((add4, ALU.add), (sub4, ALU.subtract)):
                tensor_tensor(out=out.rearrange("p g (r m) z -> p r m g z", r=2), in0=x[:, :, 0:4, :, :], in1=x[:, :, 4:8, :, :], op=op)
            add2 = fft.tile([P, 4, 4, z], F32, tag="add2")
            sub2 = fft.tile([P, 4, 4, z], F32, tag="sub2")
            diag = fft.tile([P, 4, 4, z], F32, tag="diag")
            straight = fft.tile([P, 4, 4, z], F32, tag="straight")
            eighths = fft.tile([P, 4, 16, z], F32, tag="mid", bufs=2)
            pairs = add4.rearrange("p g (r m) z -> p (g r) m z", r=2)
            tensor_tensor(out=add2[:].rearrange("p g (r m) z -> p (g r) m z", r=2), in0=pairs[:, :, 0:2, :], in1=pairs[:, :, 2:4, :], op=ALU.add)
            tensor_tensor(out=diag[:, :, 0:2, :], in0=sub4[:, :, 1:4:2, :], in1=sub4[:, :, 5:8:2, :], op=ALU.add)
            tensor_tensor(out=sub2[:].rearrange("p g (r m) z -> p (g r) m z", r=2), in0=pairs[:, :, 0:2, :], in1=pairs[:, :, 2:4, :], op=ALU.subtract)
            tensor_tensor(out=diag[:, :, 2:4, :], in0=sub4[:, :, 5:2:-2, :], in1=sub4[:, :, 1:8:6, :], op=ALU.subtract)
            tensor_tensor(out=eighths[:, :, 0:2, :], in0=add2[:, :, 0:4:2, :], in1=add2[:, :, 1:4:2, :], op=ALU.add)
            tensor_tensor(out=eighths[:, :, 2:4, :], in0=add2[:, :, 0:4:2, :], in1=add2[:, :, 1:4:2, :], op=ALU.subtract)
            turned(straight[:], sub4[:, :, 0:8:4, :], sub4[:, :, 2:8:4, :])
            slant = fft.tile([P, 4, 4, z], F32, tag="add2")
            tensor_tensor(out=slant[:, :, 0:4:2, :], in0=diag[:, :, 0:4:2, :], in1=diag[:, :, 3::-2, :], op=ALU.subtract)
            tensor_tensor(out=slant[:, :, 1:4:2, :], in0=diag[:, :, 0:4:2, :], in1=diag[:, :, 3::-2, :], op=ALU.add)
            turned(eighths[:, :, 4:8, :], sub2[:, :, 0:4:2, :], sub2[:, :, 1:4:2, :])
            for at, sign in ((8, 1.0), (12, -1.0)):
                mul_add(out=eighths[:, :, at:at + 3, :], in0=slant[:, :, 0:3, :], scalar=sign * RHO, in1=straight[:, :, 0:3, :], op0=ALU.mult, op1=ALU.add)
                mul_add(out=eighths[:, :, at + 3, :], in0=slant[:, :, 3, :], scalar=-sign * RHO, in1=straight[:, :, 3, :], op0=ALU.mult, op1=ALU.add)
            sixteenths = fft.tile([P, 2, L, z], F32, tag="sixteenths")
            fours = {4: 4, 2: 8, 10: 12, 1: 16, 9: 20, 5: 24, 13: 28}

            def into_sixteenths(k):
                if k == 0:
                    return (sixteenths[:, :, 0:2, :], sixteenths[:, :, 2:4, :]), 1
                return sixteenths[:, :, fours[k]:fours[k] + 4, :], 1

            join(eighths[:, 0:2, :, :], eighths[:, 2:4, :, :], 8, {2: 4, 1: 8, 5: 12}, (2, 1, 5), into_sixteenths)
            planes = fft.tile([P, 1, 4, L // 2, z], F32, name="planes", tag="mid", bufs=2)
            spectrum[b] = planes

            def into_planes(k):
                if k == 0:
                    return (planes[:, :, 0:4:2, 0, :], planes[:, :, 1:4:2, 0, :]), 1
                k, step = (k, 1) if k < L // 2 else (L - k, -1)
                return planes[:, :, :, k // 2 + L // 4 * (k % 2), :], step

            join(sixteenths[:, 0:1, :, :], sixteenths[:, 1:2, :, :], 16, fours, (4, 2, 10, 1, 9, 5, 13), into_planes)

        def squares(i, s, first=0, last=L // 2):
            b, tb, sub = place(i)
            sig, hf = FAST[s]
            view = spectrum[b][:, 0, :, first:last, :].rearrange("p c k (e s t) -> p s c (k e) t", e=2, s=3)
            if last - first == L // 2:
                out = sq[i][:, :, :, sig, hf, :].rearrange("p t r x -> p r x t")
                part = spectrum[b][:, 0, :, :, :].rearrange("p c k (e s t) -> p s (c k e) t", e=2, s=3)[:, s, :, sub].rearrange("p (r x) t -> p r x t", r=2)
                nc.scalar.activation(out=out, in_=part, func=AF.Square)
                return
            for r in range(2):
                out = sq[i][:, :, r, sig, hf, :].rearrange("p t (c x) -> p c x t", c=2)[:, :, 2 * first:2 * last, :]
                part = view[:, s, 2 * r:2 * r + 2, :, sub]
                if i == NBLK - 1 and s == 1 and first > 0:
                    tensor_tensor(out=out, in0=part, in1=part, op=ALU.mult)
                else:
                    nc.scalar.activation(out=out, in_=part, func=AF.Square)

        def differences(i, sig):
            diff = ps_spec.tile([P, BLK, P], F32, tag="spec", name="diff")
            for t in range(BLK):
                if t == 2 and plain_pairs:
                    next_pair()
                for r in range(2):
                    nc.tensor.matmul(out=diff[:, t, :], lhsT=sq[i][:, t, r, sig, :, :].rearrange("p f g -> p (f g)"), rhs=ident[:],
                                     is_transpose=True, start=r == 0, stop=False)
                nc.tensor.matmul(out=diff[:, t, :], lhsT=th[i][:, t, :], rhs=ident[:], is_transpose=True, start=False, stop=True)
            held["d", i, sig] = diff

        def errors(i, sig):
            squared = stage.tile([P, BLK, P], F32)
            into = d2_sums[:, sig, i:i + 1] if i < NBLK - 1 else shares[1][:, sig:sig + 1]
            nc.scalar.activation(out=squared[:], in_=held["d", i, sig][:], func=AF.Square, scale=1.0 / math.sqrt(128.0 * MEAN), accum_out=into)

        matrix_tables()

        def blocks_of(b):
            return range(BATCHES[b][0], BATCHES[b][0] + BATCHES[b][1]) if 0 <= b < len(BATCHES) else range(0)

        last = len(BATCHES) - 1

        def front_a(f):
            if f < NBLK:
                if f + 2 < NBLK:
                    load_h1(f + 2)
                turn_h1(f, 0)
                group_h1(f, 0)

        def front_b(f):
            if f < NBLK:
                turn_h1(f, 1)
                group_h1(f, 1)
                quantize_h1(f)

        def front_c(f, c):
            if f < NBLK:
                if f > 0 and c == 0:
                    load_roots(f)
                for cc in (c, c + 1):
                    hidden(f, cc)
                    relu(f, cc)
                if c == 2:
                    group_h2(f)
                    quantize_h2(f)

        def front_d(f):
            if f < NBLK:
                product(f)
                columns(f)
                clip_columns(f)

        def front_e(f):
            if f < NBLK:
                turn_x(f)
                rows(f)
                clip_rows(f)

        def do_fold(i, s):
            fold(i, s)
            folded(i, s)

        def twists(f):
            if f < NBLK:
                for s in range(3):
                    for w in range(4):
                        twist_copy(f, s, w)

        def compare(i, sig):
            for s in range(3):
                if FAST[s][0] == sig:
                    if i < NBLK - 1:
                        squares(i, s)
                    else:
                        squares(i, s, L // 4, L // 2)
            differences(i, sig)
            errors(i, sig)

        front_a(0)
        front_b(0)
        front_c(0, 0)
        front_c(0, 2)
        second_weights()
        front_d(0)
        front_e(0)
        twists(0)
        for b in range(last + 3):
            for j in blocks_of(b - 1) if b <= last else range(0):
                matrices(j)
                targets(j)
            todo = [j for j in blocks_of(b - 2)]
            here = [i for i in blocks_of(b)]
            ahead = [f for f in blocks_of(b + 1)]
            for f in ahead:
                front_a(f)
                front_b(f)
            for c in (0, 2):
                for f in ahead:
                    front_c(f, c)
            for n, i in enumerate(here):
                do_fold(i, 0)
                do_fold(i, 1)
                do_fold(i, 2)
                if n < len(ahead):
                    front_d(ahead[n])
            for f in ahead[len(here):]:
                front_d(f)
            for j in todo if here else []:
                compare(j, 0)
                compare(j, 1)
            for f in ahead:
                twists(f)
                front_e(f)
            if b > last:
                for j in blocks_of(last) if b == last + 1 else range(0):
                    matrices(j)
                    targets(j)
                for j in todo if b == last + 2 else range(0):
                    for s in range(3):
                        squares(j, s, 0, L // 4)
                for j in todo:
                    for sig in range(2):
                        compare(j, sig)
                        if plain_pairs:
                            next_pair()
            while plain_pairs:
                next_pair()
            if b == last + 1:
                lag_zero(NBLK - 1, 0)
                lag_zero(NBLK - 1, 1)
            if b <= last:
                for j in blocks_of(b - 1):
                    lag_zero(j, 0)
                    lag_zero(j, 1)
            if 0 < b < last + 2:
                transforms(b - 1)

        r0_sums = keep.tile([P, 2], F32)
        r0_squares = keep.tile([P, TILES], F32)
        for sig in range(2):
            nc.scalar.activation(out=r0_squares[:], in_=r0[:, sig, :], func=AF.Square, scale=1.0 / math.sqrt(MEAN),
                                 accum_out=r0_sums[:, sig:sig + 1])
        d2_total = keep.tile([P, 2], F32)
        nc.vector.tensor_reduce(out=d2_total[:], in_=d2_sums[:], axis=AX.X, op=ALU.add)
        tensor_tensor(out=shares[0][:, 0:2], in0=d2_total[:], in1=r0_sums[:], op=ALU.subtract)
        shares_t = ps_spec.tile([P, P], F32, tag="spec")
        for at in range(2):
            nc.tensor.matmul(out=shares_t[:], lhsT=shares[at][:], rhs=ident[:], is_transpose=True, start=at == 0, stop=at == 1)
        err = keep.tile([P, 1], F32)
        nc.vector.tensor_reduce(out=err[:], in_=shares_t[:], axis=AX.X, op=ALU.add)
        nc.sync.dma_start(out=out_1.rearrange("(a b) -> a b", a=1), in_=err[0:1, 0:1])
        nc.sync.dma_start(out=out_3.rearrange("(a b) -> a b", a=1), in_=err[1:2, 0:1])
